import numpy as np
import ml_dtypes


def mxq(x, axis, fmt="e4m3"):
    dtype, down = {"e4m3": (ml_dtypes.float8_e4m3fn, 7), "e5m2": (ml_dtypes.float8_e5m2, 14)}[fmt]
    v = np.moveaxis(np.asarray(x, np.float32).astype(ml_dtypes.bfloat16).astype(np.float64), axis, -1)
    blocks = v.reshape(v.shape[:-1] + (-1, 32))
    amax = np.abs(blocks).max(-1, keepdims=True)
    byte = np.maximum(np.where(amax > 0, np.frexp(amax)[1] - 1 + 127, 0) - down, 1)
    scale = np.exp2(byte - 127.0)
    codes = (blocks / scale).astype(np.float32).astype(dtype).astype(np.float64)
    return np.moveaxis((codes * scale).reshape(v.shape), -1, axis)


WIDE = False


def mx_kscale(k):
    if not WIDE:
        return np.ones(k)
    levels = np.array([10, -10, 5, -5, 0])
    if k % 512:
        return np.exp2(np.random.permutation(np.resize(levels, k // 32))).repeat(32)
    a = np.empty((k // 512, 16))
    for p in range(k // 512):
        a[p, :8] = np.random.permutation(np.resize(levels, 8))
        for g in range(8):
            far = levels[np.abs(levels - a[p, g]) >= 10]
            a[p, g + 8] = far[np.random.randint(len(far))]
    return np.exp2(a.ravel()).repeat(32)


BF16 = ml_dtypes.bfloat16


def bf(x):
    return np.asarray(x, np.float32).astype(BF16)


def f64(x):
    return np.asarray(x).astype(np.float64)


E2M1 = np.array([0.0, 0.5, 1.0, 1.5, 2.0, 3.0, 4.0, 6.0, -0.0, -0.5, -1.0, -1.5, -2.0, -3.0, -4.0, -6.0])


def pack_weight(w, fmt):
    k, n = w.shape
    w = f64(bf(w)).reshape(k // 32, 32, n)
    amax = np.abs(w).max(1)
    if fmt == "e4m3":
        byte = np.frexp(amax)[1] - 1 + 127 - 7
    else:
        mant, ex = np.frexp(amax / 6.0)
        byte = np.where(mant > 0.5, ex, ex - 1) + 127
    byte = np.clip(np.where(amax > 0, byte, 1), 1, 254)
    scaled = (w * np.exp2(127.0 - byte)[:, None, :]).reshape(k, n).astype(np.float32)
    by_word = np.ascontiguousarray(scaled.reshape(k // 512, 128, 4, n).transpose(0, 1, 3, 2))
    if fmt == "e4m3":
        words = by_word.astype(ml_dtypes.float8_e4m3fn).view(np.uint8)
    else:
        c = by_word.astype(ml_dtypes.float4_e2m1fn).view(np.uint8) & 0xF
        words = c[..., 0::2] | (c[..., 1::2] << 4)
    return np.ascontiguousarray(words), np.ascontiguousarray(byte.astype(np.uint8).reshape(k // 512, 16, n))


def unpack_weight(words, scales, fmt):
    g, p, n, _ = words.shape
    if fmt == "e4m3":
        vals = np.ascontiguousarray(words).view(ml_dtypes.float8_e4m3fn).astype(np.float64)
    else:
        nib = np.empty((g, p, n, 4), np.uint8)
        nib[..., 0::2] = words & 0xF
        nib[..., 1::2] = words >> 4
        vals = E2M1[nib]
    vals = vals * np.repeat(np.exp2(scales.astype(np.float64) - 127.0), 8, axis=1)[..., None]
    return vals.transpose(0, 1, 3, 2).reshape(g * 512, n)
def pack4(w):
    words, scales = pack_weight(w, "e2m1")
    return words.reshape(words.shape[0], 128, -1), scales


def unpack4(words, scales):
    return unpack_weight(words.reshape(words.shape[0], 128, -1, 2), scales, "e2m1")


NB, D, CO, CV, R = 8, 256, 1024, 512, 512


def draw0():
    s, t = mx_kscale(CV), mx_kscale(R)
    x1 = bf(np.random.standard_normal((NB, D, CO)))
    A = bf(np.random.standard_normal((D, R)) / np.sqrt(D) * t)
    t2 = bf(np.random.standard_normal((NB, R, CV)) * s)
    w = bf(np.random.standard_normal((NB, CO, CV)) / np.sqrt(CV) / s)
    words, scales = pack4((np.random.standard_normal((D, R)) / np.sqrt(R) / t).T)
    return {"x1": x1,
            "A": A,
            "t2": t2,
            "w": w,
            "C_words": words,
            "C_scales": scales}


def core(x1, A, t2, w, C_words, C_scales):
    t1 = f64(A).T @ f64(x1)
    t3 = mxq(f64(t2), 2, "e4m3") @ mxq(f64(w).transpose(0, 2, 1), 1, "e4m3")
    h = t1 * t3
    return unpack4(C_words, C_scales).T @ mxq(h, 1, "e4m3")


def e4m3fn_bytes(y):
    return np.clip(np.asarray(y, np.float64), -448.0, 448.0).astype(np.float32).astype(ml_dtypes.float8_e4m3fn).view(np.uint8)


def e4m3fn_values(b):
    return np.asarray(b, np.uint8).view(ml_dtypes.float8_e4m3fn).astype(np.float64)


def setup_inputs():
    d = draw0()
    x0 = np.asarray(d['w']).astype(np.float64)
    s = (np.max(np.abs(x0), axis=(0, 1), keepdims=True) / 448.0).astype(np.float32)
    out = {}
    for k, v in d.items():
        if k == 'w':
            out['w_bytes'] = e4m3fn_bytes(x0 / s.astype(np.float64))
            out['w_scale'] = s
        else:
            out[k] = v
    return out


def reference(x1, A, t2, w_bytes, w_scale, C_words, C_scales):
    return core(x1, A, t2, e4m3fn_values(w_bytes) * w_scale.astype(np.float64), C_words, C_scales)

@@ -1,0 +1,289 @@
+from contextlib import ExitStack
+
+import concourse.mybir as mybir
+from concourse.masks import make_identity
+
+NB, D, CO, CV, R = 8, 256, 1024, 512, 512
+FLOPS = 2 * NB * (R * D * CO + R * CV * CO + D * R * CO)
+
+F32 = mybir.dt.float32
+BF16 = mybir.dt.bfloat16
+I32 = mybir.dt.int32
+U32 = mybir.dt.uint32
+U8 = mybir.dt.uint8
+FP8 = mybir.dt.float8_e4m3fn
+FP8X4 = mybir.dt.float8_e4m3fn_x4
+FP4X4 = mybir.dt.float4_e2m1fn_x4
+MULT = mybir.AluOpType.mult
+
+P = 128
+PACK = 4
+HALF = 512
+BLOCKS = HALF // P
+UNITS = NB * CO // HALF
+LAST = UNITS - 1
+ROWS2 = 2 * CV
+W_COLS = 2 * ROWS2
+
+SHARE = 384
+OVERLAP = 2
+FIRST_SHARED = 2
+T1_LEAD = 3
+TURN_STEPS = 3
+WARM_UPS = 4
+
+
+def tile_cptensorproduct_pa_t_w4_kernel(tc, x1, A, t2, w_bytes, w_scale, C_words, C_scales, out):
+    nc = tc.nc
+    with ExitStack() as ctx:
+        const = ctx.enter_context(tc.tile_pool(name="const", bufs=1))
+        loads = ctx.enter_context(tc.tile_pool(name="loads", bufs=NB))
+        work = ctx.enter_context(tc.tile_pool(name="work", bufs=3))
+        psum = ctx.enter_context(tc.psum_pool(name="psum", bufs=2))
+        ctx.enter_context(tc.manual_schedule())
+
+        x1_raw, t2_raw, w_raw = {}, {}, {}
+        w_wide, w_scaled, w_grouped, w_codes, w_scales = {}, {}, {}, {}, {}
+        t2_grouped, t2_codes, t2_scales = {}, {}, {}
+        t1_sb, h_grouped, h_codes, h_scales = {}, {}, {}, {}
+        turning = {}
+
+        def load_w(i):
+            b, half = divmod(i, 2)
+            w_raw[i] = loads.tile([P, W_COLS], U8, name="w_raw_bytes", bufs=UNITS)
+            rows = w_bytes[b, half * HALF : (half + 1) * HALF, :].rearrange("(j p) c -> p j c", p=P)
+            nc.sync.dma_start(out=w_raw[i][:].rearrange("p (j c) -> p j c", j=BLOCKS), in_=rows)
+
+        def load_t2(b):
+            t2_raw[b] = loads.tile([P, PACK * CV], BF16, name="t2_rows")
+            nc.sync.dma_start(out=t2_raw[b][:], in_=t2[b].rearrange("(m t) c -> m (t c)", t=PACK))
+
+        def load_x1(b):
+            x1_raw[b] = loads.tile([P, 2, CO], BF16, name="x1_rows")
+            nc.sync.dma_start(out=x1_raw[b][:], in_=x1[b].rearrange("(p k) o -> p k o", k=2))
+
+        def scale_w(i, first, count):
+            if i > LAST:
+                return
+            if i not in w_scaled:
+                w_scaled[i] = work.tile([P, W_COLS], BF16, name="w_bf16", align_bytes=64)
+            cols = slice(first, first + count)
+            factors = scale_rows[:, first % CV : first % CV + count]
+            nc.vector.tensor_tensor(out=w_scaled[i][:, cols], in0=w_raw[i][:, cols].bitcast(FP8), in1=factors, op=MULT)
+
+        def widen_share(i):
+            if i > LAST:
+                return
+            w_wide[i] = work.tile([P, SHARE], BF16, name="w_share")
+            nc.scalar.copy(out=w_wide[i][:], in_=w_raw[i][:, W_COLS - SHARE :].bitcast(FP8))
+
+        def scale_share(i):
+            if i > LAST:
+                return
+            factors = scale_rows[:, CV - SHARE : CV]
+            nc.gpsimd.tensor_tensor(out=w_scaled[i][:, W_COLS - SHARE :], in0=w_wide[i][:], in1=factors, op=MULT)
+
+        def turns(kind, index, half):
+            return [(kind, index, half, n) for n in range(4)]
+
+        def turn(step):
+            kind, index, half, n = step
+            if index >= (UNITS if kind == "w" else NB):
+                return
+            raw, grouped = (w_scaled, w_grouped) if kind == "w" else (t2_raw, t2_grouped)
+            if n == 0:
+                turning["bank"] = psum.tile([P, 2, 2, P], F32, name="turn_bank")
+            bank = turning["bank"]
+            if index not in grouped:
+                grouped[index] = work.tile([P, PACK * HALF], BF16, name=kind + "_by_column", align_bytes=64)
+            words = raw[index][:].bitcast(F32)
+            j, u = divmod(n, 2)
+            first = (2 * half + j) * CV // 2
+            nc.tensor.transpose(bank[:, j, u, :], words[:, first + u : first + CV // 2 : 2], ident[:])
+            if n == 3:
+                target = grouped[index][:].bitcast(F32)[:, 4 * P * half : 4 * P * (half + 1)]
+                target = target.rearrange("p (j r u) -> p j r u", j=2, u=2)
+                nc.scalar.copy(out=target, in_=bank[:].rearrange("p j u r -> p j r u"))
+
+        def quantise_w(i):
+            if i > LAST:
+                return
+            w_codes[i] = work.tile([P, HALF], U32, name="w_code", align_bytes=64)
+            w_scales[i] = work.tile([P, HALF], U8, name="w_code_scale", align_bytes=64)
+            nc.vector.quantize_mx(out=w_codes[i][:].bitcast(FP8X4), scales=w_scales[i][:], in_=w_grouped[i][:])
+
+        def quantise_t2(b, half):
+            if b >= NB:
+                return
+            if half == 0:
+                t2_codes[b] = work.tile([P, R], U32, name="t2_code", align_bytes=64)
+                t2_scales[b] = work.tile([P, R], U8, name="t2_code_scale", align_bytes=64)
+            m = slice(R // 2 * half, R // 2 * (half + 1))
+            columns = t2_grouped[b][:, PACK * m.start : PACK * m.stop]
+            nc.vector.quantize_mx(out=t2_codes[b][:, m].bitcast(FP8X4), scales=t2_scales[b][:, m], in_=columns)
+
+        def quantise_h(i, first, count):
+            if i < 0:
+                return
+            if first == 0:
+                h_codes[i] = work.tile([P, HALF], U32, name="h_code", align_bytes=64)
+                h_scales[i] = work.tile([P, HALF], U8, name="h_code_scale", align_bytes=64)
+            n = slice(first, first + count)
+            columns = h_grouped[i][:, PACK * first : PACK * (first + count)]
+            nc.vector.quantize_mx(out=h_codes[i][:, n].bitcast(FP8X4), scales=h_scales[i][:, n], in_=columns)
+
+        def product_t1(s, steps):
+            if s < UNITS * BLOCKS:
+                b, block = divmod(s, CO // P)
+                bank = psum.tile([P, PACK, P], F32, name="t1_bank")
+                for t in range(PACK):
+                    if 0 < t <= len(steps):
+                        turn(steps[t - 1])
+                    for k in range(2):
+                        rhs = x1_raw[b][:, k, P * block : P * (block + 1)]
+                        nc.tensor.matmul(bank[:, t, :], lhsT=a_perm[:, k, t, :], rhs=rhs, start=(k == 0), stop=(k == 1))
+                t1_sb[s] = work.tile([P, P, PACK], F32, name="t1_copy", bufs=T1_LEAD + 4)
+                nc.scalar.copy(out=t1_sb[s][:], in_=bank[:].rearrange("p t o -> p o t"))
+
+        def product_t3(s):
+            i, j = divmod(s, BLOCKS)
+            b = i // 2
+            bank = psum.tile([P, PACK, P], F32, name="t3_bank")
+            n = slice(P * j, P * (j + 1))
+            for t in range(PACK):
+                m = slice(P * t, P * (t + 1))
+                nc.tensor.matmul_mx(
+                    out=bank[:, t, :],
+                    lhsT=t2_codes[b][:, m].bitcast(FP8X4),
+                    lhsT_scale=t2_scales[b][:, m],
+                    rhs=w_codes[i][:, n].bitcast(FP8X4),
+                    rhs_scale=w_scales[i][:, n],
+                    start=True,
+                    stop=True,
+                )
+            return bank
+
+        def multiply_h(s, bank):
+            i, j = divmod(s, BLOCKS)
+            if j == 0:
+                h_grouped[i] = work.tile([P, PACK * HALF], BF16, name="h_by_column", align_bytes=64)
+            h = h_grouped[i][:, PACK * P * j : PACK * P * (j + 1)].rearrange("p (o t) -> p o t", t=PACK)
+            nc.vector.tensor_tensor(out=h, in0=bank[:].rearrange("p t o -> p o t"), in1=t1_sb[s][:], op=MULT)
+
+        def product_out(i, m, first=0, count=HALF, bank_name="out_bank", copy=nc.scalar.copy):
+            if i < 0:
+                return
+            b, half = divmod(i, 2)
+            n = slice(first, first + count)
+            bank = psum.tile([P, HALF], F32, name=bank_name)
+            nc.tensor.matmul_mx(
+                out=bank[:, :count],
+                lhsT=c_words[:, 2 * P * m : 2 * P * (m + 1)].bitcast(FP4X4),
+                lhsT_scale=c_scales[:, P * m : P * (m + 1)],
+                rhs=h_codes[i][:, n].bitcast(FP8X4),
+                rhs_scale=h_scales[i][:, n],
+                start=True,
+                stop=True,
+            )
+            result = work.tile([P, HALF], F32, name="out_copy", bufs=8)
+            copy(out=result[:, :count], in_=bank[:, :count])
+            col = half * HALF + first
+            nc.sync.dma_start(out=out[b, P * m : P * (m + 1), col : col + count], in_=result[:, :count])
+
+        scale_cols = const.tile([P, PACK], F32)
+        nc.scalar.dma_start(out=scale_cols[:], in_=w_scale.rearrange("a b (p t) -> p (a b t)", t=PACK))
+        zeros = const.tile([P, HALF], BF16)
+        nc.vector.memset(zeros[:], 0.0)
+        ident = const.tile([P, P], F32)
+        make_identity(nc, ident[:])
+        c_scales = const.tile([P, D], U8, align_bytes=64)
+        nc.vector.memset(c_scales[:].bitcast(I32), 0)
+
+        load_w(0)
+        a_raw = const.tile([P, 2, R], BF16)
+        nc.sync.dma_start(out=a_raw[:], in_=A.rearrange("(p k) r -> p k r", k=2))
+        load_t2(0)
+        load_x1(0)
+        load_w(1)
+        load_w(2)
+        load_t2(1)
+        load_x1(1)
+        load_w(3)
+        c_words = const.tile([P, 2 * D], U8, align_bytes=64)
+        nc.sync.dma_start(out=c_words[:], in_=C_words[0])
+        for q in range(4):
+            rows = C_scales[0, 4 * q : 4 * q + 4, :].bitcast(I32)
+            nc.sync.dma_start(out=c_scales[32 * q : 32 * q + 4, :].bitcast(I32), in_=rows)
+        for b in range(2, NB):
+            load_w(2 * b)
+            load_t2(b)
+            load_x1(b)
+            load_w(2 * b + 1)
+
+        warm_bank = psum.tile([P, HALF], F32, name="out_bank")
+        for repeat in range(WARM_UPS):
+            nc.tensor.matmul(warm_bank[:], lhsT=zeros[:, :P], rhs=zeros[:], start=True, stop=True)
+        row_bank = psum.tile([P, PACK, P], F32, name="out_bank")
+        for t in range(PACK):
+            column = scale_cols[:, t : t + 1].to_broadcast([P, P])
+            nc.tensor.matmul(row_bank[:, t, :], lhsT=column, rhs=ident[:], start=True, stop=True)
+        scale_rows = const.tile([P, 2 * CV], F32)
+        nc.scalar.copy(out=scale_rows[:, :CV].rearrange("p (q t) -> p q t", t=PACK), in_=row_bank[:].rearrange("p t q -> p q t"))
+
+        for step in turns("t2", 0, 0) + turns("t2", 0, 1):
+            turn(step)
+        a_perm = const.tile([P, 2, PACK, P], BF16)
+        nc.vector.tensor_copy(out=a_perm[:], in_=a_raw[:].rearrange("p k (m t) -> p k t m", t=PACK))
+        product_t1(0, [])
+        product_t1(1, [])
+        nc.scalar.copy(out=scale_rows[:, CV:], in_=scale_rows[:, :CV])
+        for j in range(BLOCKS):
+            scale_w(0, CV * j, CV)
+        for step in turns("w", 0, 0) + turns("w", 0, 1):
+            turn(step)
+        product_t1(2, [])
+        widen_share(FIRST_SHARED)
+        quantise_t2(0, 0)
+        quantise_t2(0, 1)
+        scale_w(1, 0, ROWS2)
+        for step in turns("t2", 1, 0) + turns("w", 1, 0):
+            turn(step)
+        quantise_w(0)
+        scale_w(1, ROWS2, ROWS2)
+        quantise_t2(1, 0)
+        scale_w(FIRST_SHARED, ROWS2, ROWS2 - SHARE + OVERLAP)
+        scale_share(FIRST_SHARED)
+
+        for i in range(UNITS):
+            b, half = divmod(i, 2)
+            steps = turns("w", i + 1, 1) if i < LAST - 1 else []
+            steps += turns("t2", b + 1 + half, 1 - half) if i < LAST - 2 else turns("w", i + 2, 1)
+            steps += turns("w", i + 2, 0)
+            for k in range(2):
+                blocks = (BLOCKS * i + 2 * k, BLOCKS * i + 2 * k + 1)
+                t3_banks = [product_t3(s) for s in blocks]
+                product_out(i - 2, k)
+                for s in blocks:
+                    first = TURN_STEPS * (s % BLOCKS)
+                    product_t1(s + T1_LEAD, steps[first : first + TURN_STEPS])
+                for s, bank in zip(blocks, t3_banks):
+                    multiply_h(s, bank)
+                if k == 0:
+                    widen_share(i + 3)
+                    scale_w(i + 2, 0, ROWS2)
+                    quantise_h(i - 1, 0, HALF)
+                    quantise_w(i + 1)
+                else:
+                    scale_w(i + 3, ROWS2, ROWS2 - SHARE + OVERLAP)
+                    quantise_t2(b + 1 + half, 1 - half)
+                    scale_share(i + 3)
+                if i == LAST:
+                    quantise_h(LAST, HALF // 2 * k, HALF // 2)
+
+        n = HALF // 2
+        product_out(LAST - 1, 0, bank_name="t1_bank")
+        product_out(LAST, 0, 0, n, bank_name="t3_bank")
+        product_out(LAST, 1, 0, n, bank_name="t3_bank")
+        product_out(LAST - 1, 1, bank_name="t1_bank", copy=nc.vector.tensor_copy)
+        product_out(LAST, 0, n, n)
+        product_out(LAST, 1, n, n, copy=nc.vector.tensor_copy)

@@ -22,51 +22,61 @@ HALF = 512
 BLOCKS = HALF // P
 UNITS = NB * CO // HALF
 LAST = UNITS - 1
+W_COLS = BLOCKS * CV
+SHARED = 4
 ROWS2 = 2 * CV
-W_COLS = 2 * ROWS2
-
-SHARE = 384
-OVERLAP = 2
-FIRST_SHARED = 2
-T1_LEAD = 3
-TURN_STEPS = 3
-WARM_UPS = 4
+WIDE = 2 * P
+FIRST_SHARED = 3
+VN = 1
+AFTER = (0, 1, 3, 4, 4)
+SHARE = 1024
+COPIES = max(2, -(-SHARE // CV))
+RING = 4
 
 
 def tile_cptensorproduct_pa_t_w4_kernel(tc, x1, A, t2, w_bytes, w_scale, C_words, C_scales, out):
     nc = tc.nc
     with ExitStack() as ctx:
         const = ctx.enter_context(tc.tile_pool(name="const", bufs=1))
-        loads = ctx.enter_context(tc.tile_pool(name="loads", bufs=NB))
+        loads = ctx.enter_context(tc.tile_pool(name="loads", bufs=UNITS))
         work = ctx.enter_context(tc.tile_pool(name="work", bufs=3))
-        psum = ctx.enter_context(tc.psum_pool(name="psum", bufs=2))
+        psum = ctx.enter_context(tc.psum_pool(name="psum", bufs=1))
         ctx.enter_context(tc.manual_schedule())
 
         x1_raw, t2_raw, w_raw = {}, {}, {}
         w_wide, w_scaled, w_grouped, w_codes, w_scales = {}, {}, {}, {}, {}
         t2_grouped, t2_codes, t2_scales = {}, {}, {}
-        t1_sb, h_grouped, h_codes, h_scales = {}, {}, {}, {}
-        turning = {}
+        t1_banks, t1_sb, t3_banks, h_grouped, h_codes, h_scales = {}, {}, {}, {}, {}, {}
+        ring_taken = []
+        turn_banks = {}
+
+        def ring_bank(shape):
+            ring_taken.append(shape)
+            return psum.tile(shape, F32, name="ring%d" % (len(ring_taken) % RING))
 
         def load_w(i):
             b, half = divmod(i, 2)
-            w_raw[i] = loads.tile([P, W_COLS], U8, name="w_raw_bytes", bufs=UNITS)
+            w_raw[i] = loads.tile([P, 2 * ROWS2], U8, name="w_raw_bytes")
             rows = w_bytes[b, half * HALF : (half + 1) * HALF, :].rearrange("(j p) c -> p j c", p=P)
             nc.sync.dma_start(out=w_raw[i][:].rearrange("p (j c) -> p j c", j=BLOCKS), in_=rows)
 
-        def load_t2(b):
-            t2_raw[b] = loads.tile([P, PACK * CV], BF16, name="t2_rows")
-            nc.sync.dma_start(out=t2_raw[b][:], in_=t2[b].rearrange("(m t) c -> m (t c)", t=PACK))
+        def load_t2(n):
+            b, half = divmod(n, 2)
+            t2_raw[n] = loads.tile([P, ROWS2], BF16, name="t2_rows")
+            rows = t2[b].rearrange("(m t) c -> m (t c)", t=PACK)
+            nc.sync.dma_start(out=t2_raw[n][:], in_=rows[:, half * ROWS2 : (half + 1) * ROWS2])
 
-        def load_x1(b):
-            x1_raw[b] = loads.tile([P, 2, CO], BF16, name="x1_rows")
-            nc.sync.dma_start(out=x1_raw[b][:], in_=x1[b].rearrange("(p k) o -> p k o", k=2))
+        def load_x1(i):
+            b, half = divmod(i, 2)
+            x1_raw[i] = loads.tile([P, 2, HALF], BF16, name="x1_rows")
+            rows = x1[b].rearrange("(p k) o -> p k o", k=2)
+            nc.sync.dma_start(out=x1_raw[i][:], in_=rows[:, :, half * HALF : (half + 1) * HALF])
 
         def scale_w(i, first, count):
             if i > LAST:
                 return
             if i not in w_scaled:
-                w_scaled[i] = work.tile([P, W_COLS], BF16, name="w_bf16", align_bytes=64)
+                w_scaled[i] = work.tile([P, W_COLS], BF16, name="w_bf16", bufs=FIRST_SHARED, align_bytes=64)
             cols = slice(first, first + count)
             factors = scale_rows[:, first % CV : first % CV + count]
             nc.vector.tensor_tensor(out=w_scaled[i][:, cols], in0=w_raw[i][:, cols].bitcast(FP8), in1=factors, op=MULT)
@@ -80,28 +90,32 @@ def tile_cptensorproduct_pa_t_w4_kernel(tc, x1, A, t2, w_bytes, w_scale, C_words
         def scale_share(i):
             if i > LAST:
                 return
-            factors = scale_rows[:, CV - SHARE : CV]
+            w_scaled[i] = work.tile([P, W_COLS], BF16, name="shared%d" % ((i - 1) % SHARED), bufs=1, align_bytes=64)
+            factors = scale_rows[:, COPIES * CV - SHARE :]
             nc.gpsimd.tensor_tensor(out=w_scaled[i][:, W_COLS - SHARE :], in0=w_wide[i][:], in1=factors, op=MULT)
 
-        def turns(kind, index, half):
+        def turns(kind, index, half=0):
+            if index > LAST:
+                return []
             return [(kind, index, half, n) for n in range(4)]
 
         def turn(step):
             kind, index, half, n = step
-            if index >= (UNITS if kind == "w" else NB):
-                return
-            raw, grouped = (w_scaled, w_grouped) if kind == "w" else (t2_raw, t2_grouped)
-            if n == 0:
-                turning["bank"] = psum.tile([P, 2, 2, P], F32, name="turn_bank")
-            bank = turning["bank"]
-            if index not in grouped:
-                grouped[index] = work.tile([P, PACK * HALF], BF16, name=kind + "_by_column", align_bytes=64)
-            words = raw[index][:].bitcast(F32)
+            if (kind, index, half) not in turn_banks:
+                turn_banks[kind, index, half] = ring_bank([P, 2, 2, P])
+            bank = turn_banks[kind, index, half]
+            words = (w_scaled if kind == "w" else t2_raw)[index][:].bitcast(F32)
             j, u = divmod(n, 2)
             first = (2 * half + j) * CV // 2
             nc.tensor.transpose(bank[:, j, u, :], words[:, first + u : first + CV // 2 : 2], ident[:])
             if n == 3:
-                target = grouped[index][:].bitcast(F32)[:, 4 * P * half : 4 * P * (half + 1)]
+                if kind == "t2":
+                    t2_grouped[index] = work.tile([P, ROWS2], BF16, name="shared%d" % (index % SHARED), bufs=1, align_bytes=64)
+                    target = t2_grouped[index][:].bitcast(F32)
+                else:
+                    if index not in w_grouped:
+                        w_grouped[index] = work.tile([P, PACK * HALF], BF16, name="w_by_column", align_bytes=64)
+                    target = w_grouped[index][:].bitcast(F32)[:, 4 * P * half : 4 * P * (half + 1)]
                 target = target.rearrange("p (j r u) -> p j r u", j=2, u=2)
                 nc.scalar.copy(out=target, in_=bank[:].rearrange("p j u r -> p j r u"))
 
@@ -112,17 +126,17 @@ def tile_cptensorproduct_pa_t_w4_kernel(tc, x1, A, t2, w_bytes, w_scale, C_words
             w_scales[i] = work.tile([P, HALF], U8, name="w_code_scale", align_bytes=64)
             nc.vector.quantize_mx(out=w_codes[i][:].bitcast(FP8X4), scales=w_scales[i][:], in_=w_grouped[i][:])
 
-        def quantise_t2(b, half):
-            if b >= NB:
+        def quantise_t2(n):
+            if n > LAST:
                 return
+            b, half = divmod(n, 2)
             if half == 0:
                 t2_codes[b] = work.tile([P, R], U32, name="t2_code", align_bytes=64)
                 t2_scales[b] = work.tile([P, R], U8, name="t2_code_scale", align_bytes=64)
             m = slice(R // 2 * half, R // 2 * (half + 1))
-            columns = t2_grouped[b][:, PACK * m.start : PACK * m.stop]
-            nc.vector.quantize_mx(out=t2_codes[b][:, m].bitcast(FP8X4), scales=t2_scales[b][:, m], in_=columns)
+            nc.vector.quantize_mx(out=t2_codes[b][:, m].bitcast(FP8X4), scales=t2_scales[b][:, m], in_=t2_grouped[n][:])
 
-        def quantise_h(i, first, count):
+        def quantise_h(i, first=0, count=HALF):
             if i < 0:
                 return
             if first == 0:
@@ -132,23 +146,36 @@ def tile_cptensorproduct_pa_t_w4_kernel(tc, x1, A, t2, w_bytes, w_scale, C_words
             columns = h_grouped[i][:, PACK * first : PACK * (first + count)]
             nc.vector.quantize_mx(out=h_codes[i][:, n].bitcast(FP8X4), scales=h_scales[i][:, n], in_=columns)
 
-        def product_t1(s, steps):
-            if s < UNITS * BLOCKS:
-                b, block = divmod(s, CO // P)
-                bank = psum.tile([P, PACK, P], F32, name="t1_bank")
-                for t in range(PACK):
-                    if 0 < t <= len(steps):
-                        turn(steps[t - 1])
-                    for k in range(2):
-                        rhs = x1_raw[b][:, k, P * block : P * (block + 1)]
-                        nc.tensor.matmul(bank[:, t, :], lhsT=a_perm[:, k, t, :], rhs=rhs, start=(k == 0), stop=(k == 1))
-                t1_sb[s] = work.tile([P, P, PACK], F32, name="t1_copy", bufs=T1_LEAD + 4)
-                nc.scalar.copy(out=t1_sb[s][:], in_=bank[:].rearrange("p t o -> p o t"))
+        def product_t1(i, n, steps):
+            steps = steps[n]
+            if i > LAST:
+                for step in steps:
+                    turn(step)
+                return
+            half, pair = divmod(n, 2)
+            if pair == 0:
+                t1_sb[i, half] = work.tile([P, 2, WIDE, 2], F32, name="t1_copy", bufs=5)
+            if steps:
+                turn_banks[steps[0][:3]] = ring_bank([P, 2, 2, P])
+            bank = psum.tile([P, 2, WIDE], F32, name="vector_bank") if n == VN else ring_bank([P, 2, WIDE])
+            t1_banks[i, n] = bank
+            for m in range(4):
+                e, k = divmod(m, 2)
+                rhs = x1_raw[i][:, k, WIDE * half : WIDE * (half + 1)]
+                nc.tensor.matmul(bank[:, e, :], lhsT=a_perm[:, k, 2 * pair + e, :], rhs=rhs, start=(k == 0), stop=(k == 1))
+                for step in steps[AFTER[m] : AFTER[m + 1]]:
+                    turn(step)
 
-        def product_t3(s):
-            i, j = divmod(s, BLOCKS)
+        def copy_t1(i, n, copy):
+            if i > LAST:
+                return
+            half, pair = divmod(n, 2)
+            copy(out=t1_sb[i, half][:, pair, :, :], in_=t1_banks[i, n][:].rearrange("p e o -> p o e"))
+
+        def product_t3(i, j):
             b = i // 2
-            bank = psum.tile([P, PACK, P], F32, name="t3_bank")
+            bank = psum.tile([P, PACK, P], F32, name="t3_bank", bufs=3)
+            t3_banks[i, j] = bank
             n = slice(P * j, P * (j + 1))
             for t in range(PACK):
                 m = slice(P * t, P * (t + 1))
@@ -161,21 +188,19 @@ def tile_cptensorproduct_pa_t_w4_kernel(tc, x1, A, t2, w_bytes, w_scale, C_words
                     start=True,
                     stop=True,
                 )
-            return bank
 
-        def multiply_h(s, bank):
-            i, j = divmod(s, BLOCKS)
+        def multiply_h(i, j):
             if j == 0:
                 h_grouped[i] = work.tile([P, PACK * HALF], BF16, name="h_by_column", align_bytes=64)
-            h = h_grouped[i][:, PACK * P * j : PACK * P * (j + 1)].rearrange("p (o t) -> p o t", t=PACK)
-            nc.vector.tensor_tensor(out=h, in0=bank[:].rearrange("p t o -> p o t"), in1=t1_sb[s][:], op=MULT)
+            h = h_grouped[i][:, PACK * P * j : PACK * P * (j + 1)].rearrange("p (o g e) -> p o g e", g=2, e=2)
+            half, part = divmod(j, 2)
+            t1 = t1_sb[i, half][:, :, P * part : P * (part + 1), :].rearrange("p g o e -> p o g e")
+            t3 = t3_banks[i, j][:].rearrange("p (g e) o -> p o g e", g=2)
+            nc.vector.tensor_tensor(out=h, in0=t3, in1=t1, op=MULT)
 
-        def product_out(i, m, first=0, count=HALF, bank_name="out_bank", copy=nc.scalar.copy):
-            if i < 0:
-                return
-            b, half = divmod(i, 2)
+        def product_out(i, m, first=0, count=HALF):
             n = slice(first, first + count)
-            bank = psum.tile([P, HALF], F32, name=bank_name)
+            bank = ring_bank([P, HALF])
             nc.tensor.matmul_mx(
                 out=bank[:, :count],
                 lhsT=c_words[:, 2 * P * m : 2 * P * (m + 1)].bitcast(FP4X4),
@@ -185,6 +210,10 @@ def tile_cptensorproduct_pa_t_w4_kernel(tc, x1, A, t2, w_bytes, w_scale, C_words
                 start=True,
                 stop=True,
             )
+            return bank
+
+        def store_out(bank, copy, i, m, first=0, count=HALF):
+            b, half = divmod(i, 2)
             result = work.tile([P, HALF], F32, name="out_copy", bufs=8)
             copy(out=result[:, :count], in_=bank[:, :count])
             col = half * HALF + first
@@ -192,98 +221,99 @@ def tile_cptensorproduct_pa_t_w4_kernel(tc, x1, A, t2, w_bytes, w_scale, C_words
 
         scale_cols = const.tile([P, PACK], F32)
         nc.scalar.dma_start(out=scale_cols[:], in_=w_scale.rearrange("a b (p t) -> p (a b t)", t=PACK))
-        zeros = const.tile([P, HALF], BF16)
-        nc.vector.memset(zeros[:], 0.0)
         ident = const.tile([P, P], F32)
         make_identity(nc, ident[:])
         c_scales = const.tile([P, D], U8, align_bytes=64)
         nc.vector.memset(c_scales[:].bitcast(I32), 0)
 
-        load_w(0)
         a_raw = const.tile([P, 2, R], BF16)
         nc.sync.dma_start(out=a_raw[:], in_=A.rearrange("(p k) r -> p k r", k=2))
-        load_t2(0)
         load_x1(0)
+        load_w(0)
+        load_t2(0)
+        load_t2(1)
         load_w(1)
         load_w(2)
-        load_t2(1)
+        load_t2(2)
         load_x1(1)
-        load_w(3)
         c_words = const.tile([P, 2 * D], U8, align_bytes=64)
         nc.sync.dma_start(out=c_words[:], in_=C_words[0])
         for q in range(4):
             rows = C_scales[0, 4 * q : 4 * q + 4, :].bitcast(I32)
             nc.sync.dma_start(out=c_scales[32 * q : 32 * q + 4, :].bitcast(I32), in_=rows)
-        for b in range(2, NB):
-            load_w(2 * b)
-            load_t2(b)
-            load_x1(b)
-            load_w(2 * b + 1)
+        for i in range(3, UNITS):
+            load_w(i)
+            load_t2(i)
+            load_x1(i - 1)
+        load_x1(LAST)
 
-        warm_bank = psum.tile([P, HALF], F32, name="out_bank")
-        for repeat in range(WARM_UPS):
-            nc.tensor.matmul(warm_bank[:], lhsT=zeros[:, :P], rhs=zeros[:], start=True, stop=True)
-        row_bank = psum.tile([P, PACK, P], F32, name="out_bank")
+        row_bank = ring_bank([P, PACK, P])
         for t in range(PACK):
-            column = scale_cols[:, t : t + 1].to_broadcast([P, P])
-            nc.tensor.matmul(row_bank[:, t, :], lhsT=column, rhs=ident[:], start=True, stop=True)
-        scale_rows = const.tile([P, 2 * CV], F32)
-        nc.scalar.copy(out=scale_rows[:, :CV].rearrange("p (q t) -> p q t", t=PACK), in_=row_bank[:].rearrange("p t q -> p q t"))
-
-        for step in turns("t2", 0, 0) + turns("t2", 0, 1):
-            turn(step)
+            nc.tensor.transpose(row_bank[:, t, :], scale_cols[:, t : t + 1].to_broadcast([P, P]), ident[:])
+        scale_rows = const.tile([P, COPIES * CV], F32)
+        for copy in range(COPIES):
+            target = scale_rows[:, copy * CV : (copy + 1) * CV].rearrange("p (q t) -> p q t", t=PACK)
+            nc.scalar.copy(out=target, in_=row_bank[:].rearrange("p t q -> p q t"))
         a_perm = const.tile([P, 2, PACK, P], BF16)
         nc.vector.tensor_copy(out=a_perm[:], in_=a_raw[:].rearrange("p k (m t) -> p k t m", t=PACK))
-        product_t1(0, [])
-        product_t1(1, [])
-        nc.scalar.copy(out=scale_rows[:, CV:], in_=scale_rows[:, :CV])
-        for j in range(BLOCKS):
-            scale_w(0, CV * j, CV)
-        for step in turns("w", 0, 0) + turns("w", 0, 1):
-            turn(step)
-        product_t1(2, [])
-        widen_share(FIRST_SHARED)
-        quantise_t2(0, 0)
-        quantise_t2(0, 1)
+
+        scale_w(0, 0, CV)
+        scale_w(0, CV, CV)
+        scale_w(0, ROWS2, ROWS2)
         scale_w(1, 0, ROWS2)
-        for step in turns("t2", 1, 0) + turns("w", 1, 0):
-            turn(step)
-        quantise_w(0)
         scale_w(1, ROWS2, ROWS2)
-        quantise_t2(1, 0)
-        scale_w(FIRST_SHARED, ROWS2, ROWS2 - SHARE + OVERLAP)
-        scale_share(FIRST_SHARED)
+        steps = [turns("t2", 0), turns("w", 0, 0), turns("w", 0, 1), turns("t2", 1)]
+        for n in range(4):
+            product_t1(0, n, steps)
+            copy_t1(0, n, nc.scalar.copy)
+        for step in turns("w", 1, 0) + turns("w", 1, 1) + turns("t2", 2):
+            turn(step)
+        quantise_t2(0)
+        scale_w(2, ROWS2, ROWS2)
+        quantise_w(0)
+        quantise_t2(1)
 
-        for i in range(UNITS):
-            b, half = divmod(i, 2)
-            steps = turns("w", i + 1, 1) if i < LAST - 1 else []
-            steps += turns("t2", b + 1 + half, 1 - half) if i < LAST - 2 else turns("w", i + 2, 1)
-            steps += turns("w", i + 2, 0)
-            for k in range(2):
-                blocks = (BLOCKS * i + 2 * k, BLOCKS * i + 2 * k + 1)
-                t3_banks = [product_t3(s) for s in blocks]
-                product_out(i - 2, k)
-                for s in blocks:
-                    first = TURN_STEPS * (s % BLOCKS)
-                    product_t1(s + T1_LEAD, steps[first : first + TURN_STEPS])
-                for s, bank in zip(blocks, t3_banks):
-                    multiply_h(s, bank)
-                if k == 0:
-                    widen_share(i + 3)
-                    scale_w(i + 2, 0, ROWS2)
-                    quantise_h(i - 1, 0, HALF)
-                    quantise_w(i + 1)
-                else:
-                    scale_w(i + 3, ROWS2, ROWS2 - SHARE + OVERLAP)
-                    quantise_t2(b + 1 + half, 1 - half)
-                    scale_share(i + 3)
-                if i == LAST:
-                    quantise_h(LAST, HALF // 2 * k, HALF // 2)
+        for i in range(LAST):
+            steps = [turns("t2", i + 3), turns("w", i + 2, 1), turns("w", i + 2, 0), []]
+            on_vector = VN if i + 3 <= LAST else None
+            widen_share(i + 3)
+            scale_w(i + 2, 0, W_COLS - SHARE if i + 2 >= FIRST_SHARED else ROWS2)
+            if i < LAST - 1:
+                quantise_h(i - 1)
+            quantise_t2(i + 2)
+            quantise_w(i + 1)
+            if i == LAST - 1:
+                quantise_h(i - 1)
+            scale_share(i + 3)
+            for n in range(BLOCKS):
+                if n == BLOCKS - 1:
+                    multiply_h(i, 0)
+                product_t3(i, n)
+                if i > 0 and n >= 2:
+                    store_out(product_out(i - 1, n - 2), nc.scalar.copy, i - 1, n - 2)
+                product_t1(i + 1, n, steps)
+                if n != on_vector:
+                    copy_t1(i + 1, n, nc.scalar.copy)
+            for n in range(1, BLOCKS):
+                multiply_h(i, n)
+            if on_vector is not None:
+                copy_t1(i + 1, on_vector, nc.vector.tensor_copy)
 
-        n = HALF // 2
-        product_out(LAST - 1, 0, bank_name="t1_bank")
-        product_out(LAST, 0, 0, n, bank_name="t3_bank")
-        product_out(LAST, 1, 0, n, bank_name="t3_bank")
-        product_out(LAST - 1, 1, bank_name="t1_bank", copy=nc.vector.tensor_copy)
-        product_out(LAST, 0, n, n)
-        product_out(LAST, 1, n, n, copy=nc.vector.tensor_copy)
+        for n in range(BLOCKS - 1):
+            product_t3(LAST, n)
+        multiply_h(LAST, 0)
+        quantise_h(LAST - 1)
+        product_t3(LAST, BLOCKS - 1)
+        for m in range(2):
+            store_out(product_out(LAST - 1, m), nc.scalar.copy, LAST - 1, m)
+        multiply_h(LAST, 1)
+        multiply_h(LAST, 2)
+        quantise_h(LAST, 0, WIDE)
+        for m in range(2):
+            store_out(product_out(LAST, m, 0, WIDE), nc.scalar.copy, LAST, m, 0, WIDE)
+        multiply_h(LAST, 3)
+        for first in (WIDE, WIDE + P):
+            quantise_h(LAST, first, P)
+        for first in (WIDE, WIDE + P):
+            store_out(product_out(LAST, 0, first, P), nc.scalar.copy, LAST, 0, first, P)
+            store_out(product_out(LAST, 1, first, P), nc.vector.tensor_copy, LAST, 1, first, P)

@@ -31,7 +31,7 @@ VN = 1
 AFTER = (0, 1, 3, 4, 4)
 SHARE = 1024
 COPIES = max(2, -(-SHARE // CV))
-RING = 4
+RING = 5
 
 
 def tile_cptensorproduct_pa_t_w4_kernel(tc, x1, A, t2, w_bytes, w_scale, C_words, C_scales, out):
@@ -85,7 +85,7 @@ def tile_cptensorproduct_pa_t_w4_kernel(tc, x1, A, t2, w_bytes, w_scale, C_words
             if i > LAST:
                 return
             w_wide[i] = work.tile([P, SHARE], BF16, name="w_share")
-            nc.scalar.copy(out=w_wide[i][:], in_=w_raw[i][:, W_COLS - SHARE :].bitcast(FP8))
+            nc.vector.tensor_copy(out=w_wide[i][:], in_=w_raw[i][:, W_COLS - SHARE :].bitcast(FP8))
 
         def scale_share(i):
             if i > LAST:
@@ -157,7 +157,7 @@ def tile_cptensorproduct_pa_t_w4_kernel(tc, x1, A, t2, w_bytes, w_scale, C_words
                 t1_sb[i, half] = work.tile([P, 2, WIDE, 2], F32, name="t1_copy", bufs=5)
             if steps:
                 turn_banks[steps[0][:3]] = ring_bank([P, 2, 2, P])
-            bank = psum.tile([P, 2, WIDE], F32, name="vector_bank") if n == VN else ring_bank([P, 2, WIDE])
+            bank = ring_bank([P, 2, WIDE])
             t1_banks[i, n] = bank
             for m in range(4):
                 e, k = divmod(m, 2)
@@ -275,7 +275,7 @@ def tile_cptensorproduct_pa_t_w4_kernel(tc, x1, A, t2, w_bytes, w_scale, C_words
 
         for i in range(LAST):
             steps = [turns("t2", i + 3), turns("w", i + 2, 1), turns("w", i + 2, 0), []]
-            on_vector = VN if i + 3 <= LAST else None
+            on_vector = None
             widen_share(i + 3)
             scale_w(i + 2, 0, W_COLS - SHARE if i + 2 >= FIRST_SHARED else ROWS2)
             if i < LAST - 1:

@@ -27,10 +27,6 @@ SHARED = 4
 ROWS2 = 2 * CV
 WIDE = 2 * P
 FIRST_SHARED = 3
-VN = 1
-AFTER = (0, 1, 3, 4, 4)
-SHARE = 1024
-COPIES = max(2, -(-SHARE // CV))
 RING = 5
 
 
@@ -50,9 +46,9 @@ def tile_cptensorproduct_pa_t_w4_kernel(tc, x1, A, t2, w_bytes, w_scale, C_words
         ring_taken = []
         turn_banks = {}
 
-        def ring_bank(shape):
+        def ring_bank(shape, dtype=F32):
             ring_taken.append(shape)
-            return psum.tile(shape, F32, name="ring%d" % (len(ring_taken) % RING))
+            return psum.tile(shape, dtype, name="ring%d" % (len(ring_taken) % RING))
 
         def load_w(i):
             b, half = divmod(i, 2)
@@ -72,27 +68,29 @@ def tile_cptensorproduct_pa_t_w4_kernel(tc, x1, A, t2, w_bytes, w_scale, C_words
             rows = x1[b].rearrange("(p k) o -> p k o", k=2)
             nc.sync.dma_start(out=x1_raw[i][:], in_=rows[:, :, half * HALF : (half + 1) * HALF])
 
-        def scale_w(i, first, count):
+        def scale_w(i, half, first=0, count=ROWS2):
             if i > LAST:
                 return
-            if i not in w_scaled:
-                w_scaled[i] = work.tile([P, W_COLS], BF16, name="w_bf16", bufs=FIRST_SHARED, align_bytes=64)
+            if first == 0:
+                w_scaled[i, half] = work.tile([P, ROWS2], BF16, name="w_bf16", bufs=4, align_bytes=64)
+            codes = w_raw[i][:, half * ROWS2 + first : half * ROWS2 + first + count].bitcast(FP8)
             cols = slice(first, first + count)
-            factors = scale_rows[:, first % CV : first % CV + count]
-            nc.vector.tensor_tensor(out=w_scaled[i][:, cols], in0=w_raw[i][:, cols].bitcast(FP8), in1=factors, op=MULT)
+            nc.vector.tensor_tensor(out=w_scaled[i, half][:, cols], in0=codes, in1=scale_rows[:, :count], op=MULT)
 
         def widen_share(i):
             if i > LAST:
                 return
-            w_wide[i] = work.tile([P, SHARE], BF16, name="w_share")
-            nc.vector.tensor_copy(out=w_wide[i][:], in_=w_raw[i][:, W_COLS - SHARE :].bitcast(FP8))
+            w_wide[i] = work.tile([P, ROWS2], BF16, name="w_share", bufs=2)
+            nc.vector.tensor_copy(out=w_wide[i][:], in_=w_raw[i][:, ROWS2:].bitcast(FP8))
 
         def scale_share(i):
             if i > LAST:
                 return
-            w_scaled[i] = work.tile([P, W_COLS], BF16, name="shared%d" % ((i - 1) % SHARED), bufs=1, align_bytes=64)
-            factors = scale_rows[:, COPIES * CV - SHARE :]
-            nc.gpsimd.tensor_tensor(out=w_scaled[i][:, W_COLS - SHARE :], in0=w_wide[i][:], in1=factors, op=MULT)
+            w_scaled[i, 1] = work.tile([P, ROWS2], BF16, name="shared%d" % ((i - 1) % SHARED), bufs=1, align_bytes=64)
+            target = w_scaled[i, 1][:].rearrange("p (u q e) -> p u q e", u=2, e=2)
+            values = w_wide[i][:].rearrange("p (q u e) -> p u q e", u=2, e=2)
+            factors = scale_sorted[:].rearrange("p (u q e) -> p u q e", u=2, e=2)
+            nc.gpsimd.tensor_tensor(out=target, in0=values, in1=factors, op=MULT)
 
         def turns(kind, index, half=0):
             if index > LAST:
@@ -104,10 +102,13 @@ def tile_cptensorproduct_pa_t_w4_kernel(tc, x1, A, t2, w_bytes, w_scale, C_words
             if (kind, index, half) not in turn_banks:
                 turn_banks[kind, index, half] = ring_bank([P, 2, 2, P])
             bank = turn_banks[kind, index, half]
-            words = (w_scaled if kind == "w" else t2_raw)[index][:].bitcast(F32)
+            words = (w_scaled[index, half] if kind == "w" else t2_raw[index])[:].bitcast(F32)
             j, u = divmod(n, 2)
-            first = (2 * half + j) * CV // 2
-            nc.tensor.transpose(bank[:, j, u, :], words[:, first + u : first + CV // 2 : 2], ident[:])
+            if kind == "w" and half == 1 and index >= FIRST_SHARED:
+                words = words[:, (2 * u + j) * P : (2 * u + j + 1) * P]
+            else:
+                words = words[:, j * WIDE + u : (j + 1) * WIDE : 2]
+            nc.tensor.transpose(bank[:, j, u, :], words, ident[:])
             if n == 3:
                 if kind == "t2":
                     t2_grouped[index] = work.tile([P, ROWS2], BF16, name="shared%d" % (index % SHARED), bufs=1, align_bytes=64)
@@ -146,31 +147,28 @@ def tile_cptensorproduct_pa_t_w4_kernel(tc, x1, A, t2, w_bytes, w_scale, C_words
             columns = h_grouped[i][:, PACK * first : PACK * (first + count)]
             nc.vector.quantize_mx(out=h_codes[i][:, n].bitcast(FP8X4), scales=h_scales[i][:, n], in_=columns)
 
-        def product_t1(i, n, steps):
-            steps = steps[n]
+        def product_t1(i, half, steps):
+            steps = list(steps)
             if i > LAST:
                 for step in steps:
                     turn(step)
                 return
-            half, pair = divmod(n, 2)
-            if pair == 0:
-                t1_sb[i, half] = work.tile([P, 2, WIDE, 2], F32, name="t1_copy", bufs=5)
-            if steps:
+            t1_sb[i, half] = work.tile([P, 2, WIDE, 2], F32, name="t1_copy", bufs=5)
+            done = 0
+            if len(steps) > 4:
                 turn_banks[steps[0][:3]] = ring_bank([P, 2, 2, P])
-            bank = ring_bank([P, 2, WIDE])
-            t1_banks[i, n] = bank
-            for m in range(4):
-                e, k = divmod(m, 2)
-                rhs = x1_raw[i][:, k, WIDE * half : WIDE * (half + 1)]
-                nc.tensor.matmul(bank[:, e, :], lhsT=a_perm[:, k, 2 * pair + e, :], rhs=rhs, start=(k == 0), stop=(k == 1))
-                for step in steps[AFTER[m] : AFTER[m + 1]]:
-                    turn(step)
-
-        def copy_t1(i, n, copy):
-            if i > LAST:
-                return
-            half, pair = divmod(n, 2)
-            copy(out=t1_sb[i, half][:, pair, :, :], in_=t1_banks[i, n][:].rearrange("p e o -> p o e"))
+            for pair in range(2):
+                bank = ring_bank([P, 2, WIDE])
+                for m in range(4):
+                    e, k = divmod(m, 2)
+                    rhs = x1_raw[i][:, k, WIDE * half : WIDE * (half + 1)]
+                    nc.tensor.matmul(bank[:, e, :], lhsT=a_perm[:, k, 2 * pair + e, :], rhs=rhs, start=(k == 0), stop=(k == 1))
+                    if m == 3:
+                        nc.scalar.copy(out=t1_sb[i, half][:, pair, :, :], in_=bank[:].rearrange("p e o -> p o e"))
+                    until = min(len(steps), -(-len(steps) * (4 * pair + m + 1) // 7))
+                    for step in steps[done:until]:
+                        turn(step)
+                    done = until
 
         def product_t3(i, j):
             b = i // 2
@@ -214,7 +212,7 @@ def tile_cptensorproduct_pa_t_w4_kernel(tc, x1, A, t2, w_bytes, w_scale, C_words
 
         def store_out(bank, copy, i, m, first=0, count=HALF):
             b, half = divmod(i, 2)
-            result = work.tile([P, HALF], F32, name="out_copy", bufs=8)
+            result = work.tile([P, HALF], F32, name="out_copy", bufs=10)
             copy(out=result[:, :count], in_=bank[:, :count])
             col = half * HALF + first
             nc.sync.dma_start(out=out[b, P * m : P * (m + 1), col : col + count], in_=result[:, :count])
@@ -228,13 +226,14 @@ def tile_cptensorproduct_pa_t_w4_kernel(tc, x1, A, t2, w_bytes, w_scale, C_words
 
         a_raw = const.tile([P, 2, R], BF16)
         nc.sync.dma_start(out=a_raw[:], in_=A.rearrange("(p k) r -> p k r", k=2))
-        load_x1(0)
-        load_w(0)
         load_t2(0)
+        load_w(0)
+        load_x1(0)
         load_t2(1)
         load_w(1)
         load_w(2)
         load_t2(2)
+        load_t2(3)
         load_x1(1)
         c_words = const.tile([P, 2 * D], U8, align_bytes=64)
         nc.sync.dma_start(out=c_words[:], in_=C_words[0])
@@ -243,64 +242,72 @@ def tile_cptensorproduct_pa_t_w4_kernel(tc, x1, A, t2, w_bytes, w_scale, C_words
             nc.sync.dma_start(out=c_scales[32 * q : 32 * q + 4, :].bitcast(I32), in_=rows)
         for i in range(3, UNITS):
             load_w(i)
-            load_t2(i)
+            if i < LAST:
+                load_t2(i + 1)
             load_x1(i - 1)
         load_x1(LAST)
 
         row_bank = ring_bank([P, PACK, P])
         for t in range(PACK):
             nc.tensor.transpose(row_bank[:, t, :], scale_cols[:, t : t + 1].to_broadcast([P, P]), ident[:])
-        scale_rows = const.tile([P, COPIES * CV], F32)
-        for copy in range(COPIES):
+        scale_rows = const.tile([P, 2 * CV], F32)
+        for copy in range(2):
             target = scale_rows[:, copy * CV : (copy + 1) * CV].rearrange("p (q t) -> p q t", t=PACK)
             nc.scalar.copy(out=target, in_=row_bank[:].rearrange("p t q -> p q t"))
         a_perm = const.tile([P, 2, PACK, P], BF16)
         nc.vector.tensor_copy(out=a_perm[:], in_=a_raw[:].rearrange("p k (m t) -> p k t m", t=PACK))
 
-        scale_w(0, 0, CV)
-        scale_w(0, CV, CV)
-        scale_w(0, ROWS2, ROWS2)
-        scale_w(1, 0, ROWS2)
-        scale_w(1, ROWS2, ROWS2)
-        steps = [turns("t2", 0), turns("w", 0, 0), turns("w", 0, 1), turns("t2", 1)]
-        for n in range(4):
-            product_t1(0, n, steps)
-            copy_t1(0, n, nc.scalar.copy)
-        for step in turns("w", 1, 0) + turns("w", 1, 1) + turns("t2", 2):
+        scale_sorted = const.tile([P, ROWS2], F32)
+        for j in range(2):
+            target = scale_sorted[:].rearrange("p (u j q e) -> p u j q e", u=2, j=2, e=2)[:, :, j, :, :]
+            nc.scalar.copy(out=target, in_=scale_rows[:, :CV].rearrange("p (q u e) -> p u q e", u=2, e=2))
+        scale_w(0, 0, 0, CV)
+        scale_w(0, 0, CV, CV)
+        scale_w(0, 1)
+        scale_w(1, 0)
+        scale_w(1, 1)
+        for step in turns("t2", 0):
+            turn(step)
+        product_t1(0, 0, turns("w", 0, 0) + turns("t2", 1))
+        product_t1(0, 1, turns("w", 0, 1) + turns("w", 1, 0))
+        for step in turns("w", 1, 1) + turns("t2", 2) + turns("t2", 3):
             turn(step)
         quantise_t2(0)
-        scale_w(2, ROWS2, ROWS2)
+        scale_w(2, 0)
         quantise_w(0)
+        scale_w(2, 1)
         quantise_t2(1)
 
+        product_t3(0, 0)
+
         for i in range(LAST):
-            steps = [turns("t2", i + 3), turns("w", i + 2, 1), turns("w", i + 2, 0), []]
-            on_vector = None
             widen_share(i + 3)
-            scale_w(i + 2, 0, W_COLS - SHARE if i + 2 >= FIRST_SHARED else ROWS2)
-            if i < LAST - 1:
+            if i + 3 <= LAST:
+                quantise_h(i - 1)
+            quantise_w(i + 1)
+            if i + 3 > LAST:
                 quantise_h(i - 1)
             quantise_t2(i + 2)
-            quantise_w(i + 1)
-            if i == LAST - 1:
-                quantise_h(i - 1)
+            scale_w(i + 3, 0)
             scale_share(i + 3)
-            for n in range(BLOCKS):
-                if n == BLOCKS - 1:
-                    multiply_h(i, 0)
-                product_t3(i, n)
-                if i > 0 and n >= 2:
-                    store_out(product_out(i - 1, n - 2), nc.scalar.copy, i - 1, n - 2)
-                product_t1(i + 1, n, steps)
-                if n != on_vector:
-                    copy_t1(i + 1, n, nc.scalar.copy)
-            for n in range(1, BLOCKS):
-                multiply_h(i, n)
-            if on_vector is not None:
-                copy_t1(i + 1, on_vector, nc.vector.tensor_copy)
+            product_t3(i, 1)
+            product_t3(i, 2)
+            if i > 1:
+                store_out(product_out(i - 2, 1), nc.scalar.copy, i - 2, 1)
+            product_t1(i + 1, 0, turns("w", i + 2, 0) + turns("w", i + 2, 1))
+            multiply_h(i, 0)
+            product_t3(i, 3)
+            multiply_h(i, 1)
+            product_t3(i + 1, 0)
+            if i > 0:
+                store_out(product_out(i - 1, 0), nc.scalar.copy, i - 1, 0)
+            product_t1(i + 1, 1, turns("t2", i + 4))
+            multiply_h(i, 2)
+            multiply_h(i, 3)
 
-        for n in range(BLOCKS - 1):
-            product_t3(LAST, n)
+        product_t3(LAST, 1)
+        product_t3(LAST, 2)
+        store_out(product_out(LAST - 2, 1), nc.scalar.copy, LAST - 2, 1)
         multiply_h(LAST, 0)
         quantise_h(LAST - 1)
         product_t3(LAST, BLOCKS - 1)

@@ -27,7 +27,9 @@ SHARED = 4
 ROWS2 = 2 * CV
 WIDE = 2 * P
 FIRST_SHARED = 3
-RING = 5
+SPLIT = 896
+T1_LEAD = 3
+RING = 4
 
 
 def tile_cptensorproduct_pa_t_w4_kernel(tc, x1, A, t2, w_bytes, w_scale, C_words, C_scales, out):
@@ -40,7 +42,8 @@ def tile_cptensorproduct_pa_t_w4_kernel(tc, x1, A, t2, w_bytes, w_scale, C_words
         ctx.enter_context(tc.manual_schedule())
 
         x1_raw, t2_raw, w_raw = {}, {}, {}
-        w_wide, w_scaled, w_grouped, w_codes, w_scales = {}, {}, {}, {}, {}
+        w_scaled = {}
+        w_wide, w_sorted, w_grouped, w_codes, w_scales = {}, {}, {}, {}, {}
         t2_grouped, t2_codes, t2_scales = {}, {}, {}
         t1_banks, t1_sb, t3_banks, h_grouped, h_codes, h_scales = {}, {}, {}, {}, {}, {}
         ring_taken = []
@@ -68,28 +71,34 @@ def tile_cptensorproduct_pa_t_w4_kernel(tc, x1, A, t2, w_bytes, w_scale, C_words
             rows = x1[b].rearrange("(p k) o -> p k o", k=2)
             nc.sync.dma_start(out=x1_raw[i][:], in_=rows[:, :, half * HALF : (half + 1) * HALF])
 
-        def scale_w(i, half, first=0, count=ROWS2):
+        def widen_sorted(i, half):
             if i > LAST:
                 return
-            if first == 0:
-                w_scaled[i, half] = work.tile([P, ROWS2], BF16, name="w_bf16", bufs=4, align_bytes=64)
-            codes = w_raw[i][:, half * ROWS2 + first : half * ROWS2 + first + count].bitcast(FP8)
-            cols = slice(first, first + count)
-            nc.vector.tensor_tensor(out=w_scaled[i, half][:, cols], in0=codes, in1=scale_rows[:, :count], op=MULT)
+            w_sorted[i, half] = work.tile([P, ROWS2], BF16, name="w_wide_sorted", align_bytes=64)
+            target = w_sorted[i, half][:].rearrange("p (u q e) -> p q u e", u=2, e=2)
+            codes = w_raw[i][:, half * ROWS2 : (half + 1) * ROWS2].bitcast(FP8).rearrange("p (q u e) -> p q u e", u=2, e=2)
+            nc.vector.tensor_scalar(out=target, in0=codes, scalar1=ones[:], scalar2=None, op0=MULT)
 
-        def widen_share(i):
-            if i > LAST:
-                return
-            w_wide[i] = work.tile([P, ROWS2], BF16, name="w_share", bufs=2)
-            nc.vector.tensor_copy(out=w_wide[i][:], in_=w_raw[i][:, ROWS2:].bitcast(FP8))
+        def scale_w(i, half):
+            w_scaled[i, half] = work.tile([P, ROWS2], BF16, name="w_bf16", align_bytes=64)
+            for j in range(2):
+                codes = w_raw[i][:, half * ROWS2 + j * CV : half * ROWS2 + (j + 1) * CV].bitcast(FP8)
+                nc.vector.tensor_tensor(out=w_scaled[i, half][:, j * CV : (j + 1) * CV], in0=codes, in1=scale_rows[:], op=MULT)
 
-        def scale_share(i):
+        def widen_share(i, first=0, last=ROWS2, copy=nc.scalar.copy):
+            if i > LAST or first == last:
+                return
+            if i not in w_wide:
+                w_wide[i] = work.tile([P, ROWS2], BF16, name="w_share")
+            copy(out=w_wide[i][:, first:last], in_=w_raw[i][:, ROWS2 + first : ROWS2 + last].bitcast(FP8))
+
+        def scale_share(i, buffer):
             if i > LAST:
                 return
-            w_scaled[i, 1] = work.tile([P, ROWS2], BF16, name="shared%d" % ((i - 1) % SHARED), bufs=1, align_bytes=64)
-            target = w_scaled[i, 1][:].rearrange("p (u q e) -> p u q e", u=2, e=2)
-            values = w_wide[i][:].rearrange("p (q u e) -> p u q e", u=2, e=2)
-            factors = scale_sorted[:].rearrange("p (u q e) -> p u q e", u=2, e=2)
+            w_sorted[i, 1] = work.tile([P, ROWS2], BF16, name="shared%d" % (buffer % SHARED), bufs=1, align_bytes=64)
+            target = w_sorted[i, 1][:].rearrange("p (u j q e) -> p u j q e", u=2, j=2, e=2)
+            values = w_wide[i][:].rearrange("p (j q u e) -> p u j q e", j=2, u=2, e=2)
+            factors = scale_sorted[:].rearrange("p (u q e) -> p u q e", u=2, e=2).unsqueeze(2).to_broadcast([P, 2, 2, P, 2])
             nc.gpsimd.tensor_tensor(out=target, in0=values, in1=factors, op=MULT)
 
         def turns(kind, index, half=0):
@@ -97,28 +106,48 @@ def tile_cptensorproduct_pa_t_w4_kernel(tc, x1, A, t2, w_bytes, w_scale, C_words
                 return []
             return [(kind, index, half, n) for n in range(4)]
 
+        def w_target(i, half):
+            if i not in w_grouped:
+                w_grouped[i] = work.tile([P, PACK * HALF], BF16, name="w_by_column", align_bytes=64)
+            return w_grouped[i][:, ROWS2 * half : ROWS2 * (half + 1)]
+
+        def turn_bank(kind, index, half):
+            if kind == "w" and half == 0 and (index, half) not in w_scaled:
+                return psum.tile([P, 2, WIDE], F32, name="unscaled_bank")
+            if kind == "t2" and index < 3:
+                return psum.tile([P, 2, WIDE], F32, name="t3_bank", bufs=3)
+            return ring_bank([P, 2, WIDE])
+
         def turn(step):
             kind, index, half, n = step
             if (kind, index, half) not in turn_banks:
-                turn_banks[kind, index, half] = ring_bank([P, 2, 2, P])
+                turn_banks[kind, index, half] = turn_bank(kind, index, half)
             bank = turn_banks[kind, index, half]
-            words = (w_scaled[index, half] if kind == "w" else t2_raw[index])[:].bitcast(F32)
-            j, u = divmod(n, 2)
-            if kind == "w" and half == 1 and index >= FIRST_SHARED:
-                words = words[:, (2 * u + j) * P : (2 * u + j + 1) * P]
+            u, j = divmod(n, 2)
+            if kind == "w" and (index, half) in w_sorted:
+                words = w_sorted[index, half][:].bitcast(F32)[:, n * P : (n + 1) * P]
             else:
-                words = words[:, j * WIDE + u : (j + 1) * WIDE : 2]
-            nc.tensor.transpose(bank[:, j, u, :], words, ident[:])
-            if n == 3:
-                if kind == "t2":
-                    t2_grouped[index] = work.tile([P, ROWS2], BF16, name="shared%d" % (index % SHARED), bufs=1, align_bytes=64)
-                    target = t2_grouped[index][:].bitcast(F32)
-                else:
-                    if index not in w_grouped:
-                        w_grouped[index] = work.tile([P, PACK * HALF], BF16, name="w_by_column", align_bytes=64)
-                    target = w_grouped[index][:].bitcast(F32)[:, 4 * P * half : 4 * P * (half + 1)]
-                target = target.rearrange("p (j r u) -> p j r u", j=2, u=2)
-                nc.scalar.copy(out=target, in_=bank[:].rearrange("p j u r -> p j r u"))
+                rows = w_scaled[index, half] if kind == "w" else t2_raw[index]
+                words = rows[:].bitcast(F32)[:, j * WIDE + u : (j + 1) * WIDE : 2]
+            nc.tensor.transpose(bank[:, u, j * P : (j + 1) * P], words, ident[:])
+            if n == 3 and kind == "t2":
+                t2_grouped[index] = work.tile([P, ROWS2], BF16, name="shared%d" % (index % SHARED), bufs=1, align_bytes=64)
+                target = t2_grouped[index][:]
+            elif n == 3 and (half == 1 or (index, half) in w_scaled):
+                target = w_target(index, half)
+            else:
+                return
+            target = target.bitcast(F32).rearrange("p (r u) -> p r u", u=2)
+            nc.scalar.copy(out=target, in_=bank[:].rearrange("p u r -> p r u"))
+
+        def scale_turned(i, half):
+            if i > LAST:
+                return
+            bank = turn_banks["w", i, half]
+            values = bank[:].rearrange("p u r -> p (u r)").bitcast(BF16).rearrange("p (u r e) -> p r u e", u=2, e=2)
+            factors = scale_cols[:].rearrange("p (u e) -> p u e", u=2).unsqueeze(1).to_broadcast([P, WIDE, 2, 2])
+            target = w_target(i, half).rearrange("p (r u e) -> p r u e", u=2, e=2)
+            nc.vector.tensor_tensor(out=target, in0=values, in1=factors, op=MULT)
 
         def quantise_w(i):
             if i > LAST:
@@ -147,16 +176,16 @@ def tile_cptensorproduct_pa_t_w4_kernel(tc, x1, A, t2, w_bytes, w_scale, C_words
             columns = h_grouped[i][:, PACK * first : PACK * (first + count)]
             nc.vector.quantize_mx(out=h_codes[i][:, n].bitcast(FP8X4), scales=h_scales[i][:, n], in_=columns)
 
-        def product_t1(i, half, steps):
-            steps = list(steps)
+        def product_t1(index, steps):
+            i, half = divmod(index, 2)
             if i > LAST:
                 for step in steps:
                     turn(step)
                 return
-            t1_sb[i, half] = work.tile([P, 2, WIDE, 2], F32, name="t1_copy", bufs=5)
+            t1_sb[i, half] = work.tile([P, 2, WIDE, 2], F32, name="t1_copy", bufs=T1_LEAD + 3)
             done = 0
             if len(steps) > 4:
-                turn_banks[steps[0][:3]] = ring_bank([P, 2, 2, P])
+                turn_banks[steps[0][:3]] = turn_bank(*steps[0][:3])
             for pair in range(2):
                 bank = ring_bank([P, 2, WIDE])
                 for m in range(4):
@@ -224,17 +253,20 @@ def tile_cptensorproduct_pa_t_w4_kernel(tc, x1, A, t2, w_bytes, w_scale, C_words
         c_scales = const.tile([P, D], U8, align_bytes=64)
         nc.vector.memset(c_scales[:].bitcast(I32), 0)
 
+        ones = const.tile([P, 1], F32)
+        nc.vector.memset(ones[:], 1.0)
+        load_w(0)
         a_raw = const.tile([P, 2, R], BF16)
         nc.sync.dma_start(out=a_raw[:], in_=A.rearrange("(p k) r -> p k r", k=2))
         load_t2(0)
-        load_w(0)
         load_x1(0)
-        load_t2(1)
         load_w(1)
+        load_t2(1)
         load_w(2)
         load_t2(2)
         load_t2(3)
         load_x1(1)
+        load_x1(2)
         c_words = const.tile([P, 2 * D], U8, align_bytes=64)
         nc.sync.dma_start(out=c_words[:], in_=C_words[0])
         for q in range(4):
@@ -244,65 +276,61 @@ def tile_cptensorproduct_pa_t_w4_kernel(tc, x1, A, t2, w_bytes, w_scale, C_words
             load_w(i)
             if i < LAST:
                 load_t2(i + 1)
-            load_x1(i - 1)
-        load_x1(LAST)
+            load_x1(i)
 
         row_bank = ring_bank([P, PACK, P])
         for t in range(PACK):
             nc.tensor.transpose(row_bank[:, t, :], scale_cols[:, t : t + 1].to_broadcast([P, P]), ident[:])
-        scale_rows = const.tile([P, 2 * CV], F32)
-        for copy in range(2):
-            target = scale_rows[:, copy * CV : (copy + 1) * CV].rearrange("p (q t) -> p q t", t=PACK)
-            nc.scalar.copy(out=target, in_=row_bank[:].rearrange("p t q -> p q t"))
+        scale_rows = const.tile([P, CV], F32)
+        nc.scalar.copy(out=scale_rows[:].rearrange("p (q t) -> p q t", t=PACK), in_=row_bank[:].rearrange("p t q -> p q t"))
+        scale_sorted = const.tile([P, CV], F32)
+        target = scale_sorted[:].rearrange("p (u q e) -> p u q e", u=2, e=2)
+        nc.scalar.copy(out=target, in_=row_bank[:].rearrange("p (u e) q -> p u q e", u=2))
+        widen_sorted(0, 0)
         a_perm = const.tile([P, 2, PACK, P], BF16)
         nc.vector.tensor_copy(out=a_perm[:], in_=a_raw[:].rearrange("p k (m t) -> p k t m", t=PACK))
-
-        scale_sorted = const.tile([P, ROWS2], F32)
-        for j in range(2):
-            target = scale_sorted[:].rearrange("p (u j q e) -> p u j q e", u=2, j=2, e=2)[:, :, j, :, :]
-            nc.scalar.copy(out=target, in_=scale_rows[:, :CV].rearrange("p (q u e) -> p u q e", u=2, e=2))
-        scale_w(0, 0, 0, CV)
-        scale_w(0, 0, CV, CV)
         scale_w(0, 1)
+        for step in turns("w", 0, 0) + turns("t2", 0):
+            turn(step)
+        scale_turned(0, 0)
         scale_w(1, 0)
+        product_t1(0, turns("w", 0, 1) + turns("t2", 1))
         scale_w(1, 1)
-        for step in turns("t2", 0):
-            turn(step)
-        product_t1(0, 0, turns("w", 0, 0) + turns("t2", 1))
-        product_t1(0, 1, turns("w", 0, 1) + turns("w", 1, 0))
-        for step in turns("w", 1, 1) + turns("t2", 2) + turns("t2", 3):
-            turn(step)
         quantise_t2(0)
-        scale_w(2, 0)
-        quantise_w(0)
         scale_w(2, 1)
+        product_t1(1, turns("w", 1, 0) + turns("w", 1, 1))
+        quantise_w(0)
         quantise_t2(1)
-
+        widen_sorted(2, 0)
+        product_t1(2, turns("t2", 2) + turns("w", 2, 1))
+        widen_share(3, copy=nc.vector.tensor_copy)
         product_t3(0, 0)
+        widen_share(4, 0, SPLIT // 2)
 
         for i in range(LAST):
-            widen_share(i + 3)
-            if i + 3 <= LAST:
-                quantise_h(i - 1)
             quantise_w(i + 1)
-            if i + 3 > LAST:
-                quantise_h(i - 1)
+            quantise_h(i - 1)
+            if i > 0:
+                widen_share(i + 3, SPLIT, ROWS2, nc.vector.tensor_copy)
             quantise_t2(i + 2)
-            scale_w(i + 3, 0)
-            scale_share(i + 3)
+            widen_sorted(i + 3, 0)
+            scale_share(i + 3, i + 2)
             product_t3(i, 1)
             product_t3(i, 2)
             if i > 1:
                 store_out(product_out(i - 2, 1), nc.scalar.copy, i - 2, 1)
-            product_t1(i + 1, 0, turns("w", i + 2, 0) + turns("w", i + 2, 1))
+            product_t1(2 * i + T1_LEAD, turns("w", i + 2, 0) + (turns("w", i + 2, 1) if i > 0 else turns("t2", 3)))
+            widen_share(i + 4, SPLIT // 2, SPLIT)
             multiply_h(i, 0)
             product_t3(i, 3)
             multiply_h(i, 1)
             product_t3(i + 1, 0)
             if i > 0:
                 store_out(product_out(i - 1, 0), nc.scalar.copy, i - 1, 0)
-            product_t1(i + 1, 1, turns("t2", i + 4))
+            product_t1(2 * i + T1_LEAD + 1, turns("t2", i + 4))
+            widen_share(i + 5, 0, SPLIT // 2)
             multiply_h(i, 2)
+            scale_turned(i + 2, 0)
             multiply_h(i, 3)
 
         product_t3(LAST, 1)

@@ -184,7 +184,9 @@ def tile_cptensorproduct_pa_t_w4_kernel(tc, x1, A, t2, w_bytes, w_scale, C_words
                 return
             t1_sb[i, half] = work.tile([P, 2, WIDE, 2], F32, name="t1_copy", bufs=T1_LEAD + 3)
             done = 0
-            if len(steps) > 4:
+            contiguous = all(step[0] == "w" and step[1:3] in w_sorted for step in steps)
+            ends = (0, 0, 0, 8, 8, 8, 8, 8) if contiguous else [-(-len(steps) * n // 7) for n in range(1, 9)]
+            if len(steps) > 4 and not all(step[0] == "w" and step[1:3] in w_sorted for step in steps):
                 turn_banks[steps[0][:3]] = turn_bank(*steps[0][:3])
             for pair in range(2):
                 bank = ring_bank([P, 2, WIDE])
@@ -194,7 +196,7 @@ def tile_cptensorproduct_pa_t_w4_kernel(tc, x1, A, t2, w_bytes, w_scale, C_words
                     nc.tensor.matmul(bank[:, e, :], lhsT=a_perm[:, k, 2 * pair + e, :], rhs=rhs, start=(k == 0), stop=(k == 1))
                     if m == 3:
                         nc.scalar.copy(out=t1_sb[i, half][:, pair, :, :], in_=bank[:].rearrange("p e o -> p o e"))
-                    until = min(len(steps), -(-len(steps) * (4 * pair + m + 1) // 7))
+                    until = min(len(steps), ends[4 * pair + m])
                     for step in steps[done:until]:
                         turn(step)
                     done = until

@@ -27,7 +27,7 @@ SHARED = 4
 ROWS2 = 2 * CV
 WIDE = 2 * P
 FIRST_SHARED = 3
-SPLIT = 896
+SPLIT = 1024
 T1_LEAD = 3
 RING = 4
 
@@ -201,10 +201,19 @@ def tile_cptensorproduct_pa_t_w4_kernel(tc, x1, A, t2, w_bytes, w_scale, C_words
                         turn(step)
                     done = until
 
-        def product_t3(i, j):
+        def t3_bank(i, j, spare=False):
             b = i // 2
-            bank = psum.tile([P, PACK, P], F32, name="t3_bank", bufs=3)
+            if spare:
+                bank = psum.tile([P, PACK, P], F32, name="unscaled_bank")
+            else:
+                bank = psum.tile([P, PACK, P], F32, name="t3_bank", bufs=3)
             t3_banks[i, j] = bank
+
+        def product_t3(i, j, spare=False):
+            b = i // 2
+            if (i, j) not in t3_banks:
+                t3_bank(i, j, spare)
+            bank = t3_banks[i, j]
             n = slice(P * j, P * (j + 1))
             for t in range(PACK):
                 m = slice(P * t, P * (t + 1))
@@ -227,9 +236,9 @@ def tile_cptensorproduct_pa_t_w4_kernel(tc, x1, A, t2, w_bytes, w_scale, C_words
             t3 = t3_banks[i, j][:].rearrange("p (g e) o -> p o g e", g=2)
             nc.vector.tensor_tensor(out=h, in0=t3, in1=t1, op=MULT)
 
-        def product_out(i, m, first=0, count=HALF):
+        def product_out(i, m, first=0, count=HALF, spare=False):
             n = slice(first, first + count)
-            bank = ring_bank([P, HALF])
+            bank = psum.tile([P, HALF], F32, name="t3_bank", bufs=3) if spare else ring_bank([P, HALF])
             nc.tensor.matmul_mx(
                 out=bank[:, :count],
                 lhsT=c_words[:, 2 * P * m : 2 * P * (m + 1)].bitcast(FP4X4),
@@ -317,16 +326,22 @@ def tile_cptensorproduct_pa_t_w4_kernel(tc, x1, A, t2, w_bytes, w_scale, C_words
             quantise_t2(i + 2)
             widen_sorted(i + 3, 0)
             scale_share(i + 3, i + 2)
-            product_t3(i, 1)
+            t3_bank(i, 1)
             product_t3(i, 2)
+            product_t3(i, 1)
+            if i >= LAST - 1:
+                product_t3(i, 3, spare=True)
             if i > 1:
                 store_out(product_out(i - 2, 1), nc.scalar.copy, i - 2, 1)
             product_t1(2 * i + T1_LEAD, turns("w", i + 2, 0) + (turns("w", i + 2, 1) if i > 0 else turns("t2", 3)))
             widen_share(i + 4, SPLIT // 2, SPLIT)
             multiply_h(i, 0)
-            product_t3(i, 3)
             multiply_h(i, 1)
+            if i < LAST - 1:
+                t3_bank(i, 3)
             product_t3(i + 1, 0)
+            if i < LAST - 1:
+                product_t3(i, 3)
             if i > 0:
                 store_out(product_out(i - 1, 0), nc.scalar.copy, i - 1, 0)
             product_t1(2 * i + T1_LEAD + 1, turns("t2", i + 4))
@@ -337,10 +352,10 @@ def tile_cptensorproduct_pa_t_w4_kernel(tc, x1, A, t2, w_bytes, w_scale, C_words
 
         product_t3(LAST, 1)
         product_t3(LAST, 2)
+        product_t3(LAST, 3, spare=True)
         store_out(product_out(LAST - 2, 1), nc.scalar.copy, LAST - 2, 1)
         multiply_h(LAST, 0)
         quantise_h(LAST - 1)
-        product_t3(LAST, BLOCKS - 1)
         for m in range(2):
             store_out(product_out(LAST - 1, m), nc.scalar.copy, LAST - 1, m)
         multiply_h(LAST, 1)
@@ -353,4 +368,4 @@ def tile_cptensorproduct_pa_t_w4_kernel(tc, x1, A, t2, w_bytes, w_scale, C_words
             quantise_h(LAST, first, P)
         for first in (WIDE, WIDE + P):
             store_out(product_out(LAST, 0, first, P), nc.scalar.copy, LAST, 0, first, P)
-            store_out(product_out(LAST, 1, first, P), nc.vector.tensor_copy, LAST, 1, first, P)
+            store_out(product_out(LAST, 1, first, P, spare=True), nc.vector.tensor_copy, LAST, 1, first, P)

@@ -182,38 +182,32 @@ def tile_cptensorproduct_pa_t_w4_kernel(tc, x1, A, t2, w_bytes, w_scale, C_words
                 for step in steps:
                     turn(step)
                 return
-            t1_sb[i, half] = work.tile([P, 2, WIDE, 2], F32, name="t1_copy", bufs=T1_LEAD + 3)
+            t1_sb[i, half] = work.tile([P, 2, P, PACK], F32, name="t1_copy", bufs=T1_LEAD + 3)
             done = 0
             contiguous = all(step[0] == "w" and step[1:3] in w_sorted for step in steps)
             ends = (0, 0, 0, 8, 8, 8, 8, 8) if contiguous else [-(-len(steps) * n // 7) for n in range(1, 9)]
             if len(steps) > 4 and not all(step[0] == "w" and step[1:3] in w_sorted for step in steps):
                 turn_banks[steps[0][:3]] = turn_bank(*steps[0][:3])
             for pair in range(2):
-                bank = ring_bank([P, 2, WIDE])
+                bank = ring_bank([P, PACK, P])
                 for m in range(4):
-                    e, k = divmod(m, 2)
-                    rhs = x1_raw[i][:, k, WIDE * half : WIDE * (half + 1)]
-                    nc.tensor.matmul(bank[:, e, :], lhsT=a_perm[:, k, 2 * pair + e, :], rhs=rhs, start=(k == 0), stop=(k == 1))
+                    for k in range(2):
+                        rhs = x1_raw[i][:, k, WIDE * half + P * pair : WIDE * half + P * (pair + 1)]
+                        nc.tensor.matmul(bank[:, m, :], lhsT=a_perm[:, k, m, :], rhs=rhs, start=(k == 0), stop=(k == 1))
                     if m == 3:
-                        nc.scalar.copy(out=t1_sb[i, half][:, pair, :, :], in_=bank[:].rearrange("p e o -> p o e"))
+                        nc.scalar.copy(out=t1_sb[i, half][:, pair, :, :], in_=bank[:].rearrange("p t o -> p o t"))
                     until = min(len(steps), ends[4 * pair + m])
                     for step in steps[done:until]:
                         turn(step)
                     done = until
 
-        def t3_bank(i, j, spare=False):
+        def product_t3(i, j, spare=False):
             b = i // 2
             if spare:
                 bank = psum.tile([P, PACK, P], F32, name="unscaled_bank")
             else:
                 bank = psum.tile([P, PACK, P], F32, name="t3_bank", bufs=3)
             t3_banks[i, j] = bank
-
-        def product_t3(i, j, spare=False):
-            b = i // 2
-            if (i, j) not in t3_banks:
-                t3_bank(i, j, spare)
-            bank = t3_banks[i, j]
             n = slice(P * j, P * (j + 1))
             for t in range(PACK):
                 m = slice(P * t, P * (t + 1))
@@ -230,10 +224,10 @@ def tile_cptensorproduct_pa_t_w4_kernel(tc, x1, A, t2, w_bytes, w_scale, C_words
         def multiply_h(i, j):
             if j == 0:
                 h_grouped[i] = work.tile([P, PACK * HALF], BF16, name="h_by_column", align_bytes=64)
-            h = h_grouped[i][:, PACK * P * j : PACK * P * (j + 1)].rearrange("p (o g e) -> p o g e", g=2, e=2)
+            h = h_grouped[i][:, PACK * P * j : PACK * P * (j + 1)].rearrange("p (o t) -> p o t", t=PACK)
             half, part = divmod(j, 2)
-            t1 = t1_sb[i, half][:, :, P * part : P * (part + 1), :].rearrange("p g o e -> p o g e")
-            t3 = t3_banks[i, j][:].rearrange("p (g e) o -> p o g e", g=2)
+            t1 = t1_sb[i, half][:, part, :, :]
+            t3 = t3_banks[i, j][:].rearrange("p t o -> p o t")
             nc.vector.tensor_tensor(out=h, in0=t3, in1=t1, op=MULT)
 
         def product_out(i, m, first=0, count=HALF, spare=False):
@@ -326,9 +320,8 @@ def tile_cptensorproduct_pa_t_w4_kernel(tc, x1, A, t2, w_bytes, w_scale, C_words
             quantise_t2(i + 2)
             widen_sorted(i + 3, 0)
             scale_share(i + 3, i + 2)
-            t3_bank(i, 1)
-            product_t3(i, 2)
             product_t3(i, 1)
+            product_t3(i, 2)
             if i >= LAST - 1:
                 product_t3(i, 3, spare=True)
             if i > 1:
@@ -336,12 +329,10 @@ def tile_cptensorproduct_pa_t_w4_kernel(tc, x1, A, t2, w_bytes, w_scale, C_words
             product_t1(2 * i + T1_LEAD, turns("w", i + 2, 0) + (turns("w", i + 2, 1) if i > 0 else turns("t2", 3)))
             widen_share(i + 4, SPLIT // 2, SPLIT)
             multiply_h(i, 0)
-            multiply_h(i, 1)
-            if i < LAST - 1:
-                t3_bank(i, 3)
-            product_t3(i + 1, 0)
             if i < LAST - 1:
                 product_t3(i, 3)
+            multiply_h(i, 1)
+            product_t3(i + 1, 0)
             if i > 0:
                 store_out(product_out(i - 1, 0), nc.scalar.copy, i - 1, 0)
             product_t1(2 * i + T1_LEAD + 1, turns("t2", i + 4))

@@ -18,18 +18,20 @@ MULT = mybir.AluOpType.mult
 
 P = 128
 PACK = 4
-HALF = 512
-BLOCKS = HALF // P
-UNITS = NB * CO // HALF
+UNIT = 512
+BLOCKS = UNIT // P
+UNITS = NB * CO // UNIT
 LAST = UNITS - 1
-W_COLS = BLOCKS * CV
-SHARED = 4
 ROWS2 = 2 * CV
 WIDE = 2 * P
-FIRST_SHARED = 3
-SPLIT = 1024
-T1_LEAD = 3
+
+SCALAR_WIDENS = 768
+T1_LEAD = 4
+GAPS = 7
+HANDED_ON = 4
+T3_BANKS = 3
 RING = 4
+RESULTS = 10
 
 
 def tile_cptensorproduct_pa_t_w4_kernel(tc, x1, A, t2, w_bytes, w_scale, C_words, C_scales, out):
@@ -42,21 +44,30 @@ def tile_cptensorproduct_pa_t_w4_kernel(tc, x1, A, t2, w_bytes, w_scale, C_words
         ctx.enter_context(tc.manual_schedule())
 
         x1_raw, t2_raw, w_raw = {}, {}, {}
-        w_scaled = {}
-        w_wide, w_sorted, w_grouped, w_codes, w_scales = {}, {}, {}, {}, {}
+        w_late, w_plain, w_wide, w_shared, w_start = {}, {}, {}, {}, {}
+        w_grouped, w_codes, w_scales = {}, {}, {}
         t2_grouped, t2_codes, t2_scales = {}, {}, {}
-        t1_banks, t1_sb, t3_banks, h_grouped, h_codes, h_scales = {}, {}, {}, {}, {}, {}
+        t1_sb, t3_banks, late_banks = {}, {}, {}
+        h_grouped, h_codes, h_scales = {}, {}, {}
         ring_taken = []
-        turn_banks = {}
 
-        def ring_bank(shape, dtype=F32):
+        def ring_bank(shape):
             ring_taken.append(shape)
-            return psum.tile(shape, dtype, name="ring%d" % (len(ring_taken) % RING))
+            return psum.tile(shape, F32, name="ring%d" % (len(ring_taken) % RING))
+
+        def t3_bank(shape):
+            return psum.tile(shape, F32, name="t3_bank", bufs=T3_BANKS)
+
+        def block_bank(shape):
+            return psum.tile(shape, F32, name="block_bank")
+
+        def handed_on(n):
+            return work.tile([P, ROWS2], BF16, name="handed_on%d" % (n % HANDED_ON), bufs=1, align_bytes=64)
 
         def load_w(i):
             b, half = divmod(i, 2)
-            w_raw[i] = loads.tile([P, 2 * ROWS2], U8, name="w_raw_bytes")
-            rows = w_bytes[b, half * HALF : (half + 1) * HALF, :].rearrange("(j p) c -> p j c", p=P)
+            w_raw[i] = loads.tile([P, BLOCKS * CV], U8, name="w_raw_bytes")
+            rows = w_bytes[b, half * UNIT : (half + 1) * UNIT, :].rearrange("(j p) c -> p j c", p=P)
             nc.sync.dma_start(out=w_raw[i][:].rearrange("p (j c) -> p j c", j=BLOCKS), in_=rows)
 
         def load_t2(n):
@@ -67,152 +78,168 @@ def tile_cptensorproduct_pa_t_w4_kernel(tc, x1, A, t2, w_bytes, w_scale, C_words
 
         def load_x1(i):
             b, half = divmod(i, 2)
-            x1_raw[i] = loads.tile([P, 2, HALF], BF16, name="x1_rows")
+            x1_raw[i] = loads.tile([P, 2, UNIT], BF16, name="x1_rows")
             rows = x1[b].rearrange("(p k) o -> p k o", k=2)
-            nc.sync.dma_start(out=x1_raw[i][:], in_=rows[:, :, half * HALF : (half + 1) * HALF])
+            nc.sync.dma_start(out=x1_raw[i][:], in_=rows[:, :, half * UNIT : (half + 1) * UNIT])
 
-        def widen_sorted(i, half):
-            if i > LAST:
-                return
-            w_sorted[i, half] = work.tile([P, ROWS2], BF16, name="w_wide_sorted", align_bytes=64)
-            target = w_sorted[i, half][:].rearrange("p (u q e) -> p q u e", u=2, e=2)
-            codes = w_raw[i][:, half * ROWS2 : (half + 1) * ROWS2].bitcast(FP8).rearrange("p (q u e) -> p q u e", u=2, e=2)
-            nc.vector.tensor_scalar(out=target, in0=codes, scalar1=ones[:], scalar2=None, op0=MULT)
+        def scale_block(i, j, target):
+            values = w_raw[i][:, j * CV : (j + 1) * CV].bitcast(FP8)
+            nc.vector.tensor_tensor(out=target, in0=values, in1=scale_rows[:], op=MULT)
 
-        def scale_w(i, half):
-            w_scaled[i, half] = work.tile([P, ROWS2], BF16, name="w_bf16", align_bytes=64)
+        def scale_start(i, half):
+            w_start[i, half] = work.tile([P, ROWS2], BF16, name="w_start", bufs=4, align_bytes=64)
             for j in range(2):
-                codes = w_raw[i][:, half * ROWS2 + j * CV : half * ROWS2 + (j + 1) * CV].bitcast(FP8)
-                nc.vector.tensor_tensor(out=w_scaled[i, half][:, j * CV : (j + 1) * CV], in0=codes, in1=scale_rows[:], op=MULT)
+                scale_block(i, 2 * half + j, w_start[i, half][:, j * CV : (j + 1) * CV])
 
-        def widen_share(i, first=0, last=ROWS2, copy=nc.scalar.copy):
-            if i > LAST or first == last:
-                return
-            if i not in w_wide:
-                w_wide[i] = work.tile([P, ROWS2], BF16, name="w_share")
-            copy(out=w_wide[i][:, first:last], in_=w_raw[i][:, ROWS2 + first : ROWS2 + last].bitcast(FP8))
+        def scale_plain(i):
+            if i <= LAST:
+                w_plain[i] = work.tile([P, CV], BF16, name="w_plain", align_bytes=64)
+                scale_block(i, 1, w_plain[i][:])
 
-        def scale_share(i, buffer):
-            if i > LAST:
-                return
-            w_sorted[i, 1] = work.tile([P, ROWS2], BF16, name="shared%d" % (buffer % SHARED), bufs=1, align_bytes=64)
-            target = w_sorted[i, 1][:].rearrange("p (u j q e) -> p u j q e", u=2, j=2, e=2)
-            values = w_wide[i][:].rearrange("p (j q u e) -> p u j q e", j=2, u=2, e=2)
-            factors = scale_sorted[:].rearrange("p (u q e) -> p u q e", u=2, e=2).unsqueeze(2).to_broadcast([P, 2, 2, P, 2])
-            nc.gpsimd.tensor_tensor(out=target, in0=values, in1=factors, op=MULT)
+        def widen_late(i):
+            if i <= LAST:
+                w_late[i] = work.tile([P, CV], BF16, name="w_late", align_bytes=64)
+                target = w_late[i][:].rearrange("p (u q e) -> p q u e", u=2, e=2)
+                values = w_raw[i][:, :CV].bitcast(FP8).rearrange("p (q u e) -> p q u e", u=2, e=2)
+                nc.vector.tensor_scalar(out=target, in0=values, scalar1=ones[:], scalar2=None, op0=MULT)
 
-        def turns(kind, index, half=0):
-            if index > LAST:
-                return []
-            return [(kind, index, half, n) for n in range(4)]
+        def scale_late(i):
+            if i <= LAST:
+                values = late_banks[i][:].rearrange("p u r -> p (u r)").bitcast(BF16)
+                values = values.rearrange("p (u r e) -> p r u e", u=2, e=2)
+                factors = scale_cols[:].rearrange("p (u e) -> p u e", u=2).unsqueeze(1).to_broadcast([P, P, 2, 2])
+                target = w_columns(i, 0, 1).rearrange("p (r u e) -> p r u e", u=2, e=2)
+                nc.vector.tensor_tensor(out=target, in0=values, in1=factors, op=MULT)
 
-        def w_target(i, half):
+        def widen_shared(i, first, last, copy):
+            if i <= LAST:
+                if i not in w_wide:
+                    w_wide[i] = work.tile([P, ROWS2], BF16, name="w_wide")
+                copy(out=w_wide[i][:, first:last], in_=w_raw[i][:, ROWS2 + first : ROWS2 + last].bitcast(FP8))
+
+        def scale_shared(i):
+            if i <= LAST:
+                w_shared[i] = handed_on(i - 1)
+                target = w_shared[i][:].rearrange("p (u j q e) -> p u j q e", u=2, j=2, e=2)
+                values = w_wide[i][:].rearrange("p (j q u e) -> p u j q e", j=2, u=2, e=2)
+                factors = scale_sorted[:].rearrange("p (u q e) -> p u q e", u=2, e=2)
+                factors = factors.unsqueeze(2).to_broadcast([P, 2, 2, P, 2])
+                nc.gpsimd.tensor_tensor(out=target, in0=values, in1=factors, op=MULT)
+
+        def w_columns(i, first, last):
             if i not in w_grouped:
-                w_grouped[i] = work.tile([P, PACK * HALF], BF16, name="w_by_column", align_bytes=64)
-            return w_grouped[i][:, ROWS2 * half : ROWS2 * (half + 1)]
+                w_grouped[i] = work.tile([P, PACK * UNIT], BF16, name="w_by_column", align_bytes=64)
+            return w_grouped[i][:, PACK * P * first : PACK * P * last]
 
-        def turn_bank(kind, index, half):
-            if kind == "w" and half == 0 and (index, half) not in w_scaled:
-                return psum.tile([P, 2, WIDE], F32, name="unscaled_bank")
-            if kind == "t2" and index < 3:
-                return psum.tile([P, 2, WIDE], F32, name="t3_bank", bufs=3)
-            return ring_bank([P, 2, WIDE])
+        def turns(sources, take_bank, finish, early=False):
+            blocks = len(sources[0])
+            taken = [take_bank([P, 2, blocks * P])] if early else []
 
-        def turn(step):
-            kind, index, half, n = step
-            if (kind, index, half) not in turn_banks:
-                turn_banks[kind, index, half] = turn_bank(kind, index, half)
-            bank = turn_banks[kind, index, half]
-            u, j = divmod(n, 2)
-            if kind == "w" and (index, half) in w_sorted:
-                words = w_sorted[index, half][:].bitcast(F32)[:, n * P : (n + 1) * P]
-            else:
-                rows = w_scaled[index, half] if kind == "w" else t2_raw[index]
-                words = rows[:].bitcast(F32)[:, j * WIDE + u : (j + 1) * WIDE : 2]
-            nc.tensor.transpose(bank[:, u, j * P : (j + 1) * P], words, ident[:])
-            if n == 3 and kind == "t2":
-                t2_grouped[index] = work.tile([P, ROWS2], BF16, name="shared%d" % (index % SHARED), bufs=1, align_bytes=64)
-                target = t2_grouped[index][:]
-            elif n == 3 and (half == 1 or (index, half) in w_scaled):
-                target = w_target(index, half)
-            else:
-                return
-            target = target.bitcast(F32).rearrange("p (r u) -> p r u", u=2)
-            nc.scalar.copy(out=target, in_=bank[:].rearrange("p u r -> p r u"))
+            def turn(u, j):
+                if not taken:
+                    taken.append(take_bank([P, 2, blocks * P]))
+                nc.tensor.transpose(taken[0][:, u, j * P : (j + 1) * P], sources[u][j], ident[:])
+                if (u, j) == (1, blocks - 1):
+                    finish(taken[0])
 
-        def scale_turned(i, half):
-            if i > LAST:
-                return
-            bank = turn_banks["w", i, half]
-            values = bank[:].rearrange("p u r -> p (u r)").bitcast(BF16).rearrange("p (u r e) -> p r u e", u=2, e=2)
-            factors = scale_cols[:].rearrange("p (u e) -> p u e", u=2).unsqueeze(1).to_broadcast([P, WIDE, 2, 2])
-            target = w_target(i, half).rearrange("p (r u e) -> p r u e", u=2, e=2)
-            nc.vector.tensor_tensor(out=target, in0=values, in1=factors, op=MULT)
+            return [lambda u=u, j=j: turn(u, j) for u in range(2) for j in range(blocks)]
+
+        def pairs_unsorted(tile, blocks):
+            words = tile[:].bitcast(F32)
+            return [[words[:, j * WIDE + u : (j + 1) * WIDE : 2] for j in range(blocks)] for u in range(2)]
+
+        def pairs_sorted(tile, blocks):
+            words = tile[:].bitcast(F32)
+            return [[words[:, (u * blocks + j) * P : (u * blocks + j + 1) * P] for j in range(blocks)] for u in range(2)]
+
+        def copy_turned(target, bank):
+            words = target.bitcast(F32).rearrange("p (r u) -> p r u", u=2)
+            nc.scalar.copy(out=words, in_=bank[:].rearrange("p u r -> p r u"))
+
+        def turns_t2(n, take_bank=ring_bank, early=False):
+            def finish(bank):
+                t2_grouped[n] = handed_on(n)
+                copy_turned(t2_grouped[n][:], bank)
+
+            return turns(pairs_unsorted(t2_raw[n], 2), take_bank, finish, early) if n <= LAST else []
+
+        def turns_start(i, half, take_bank=ring_bank, early=False):
+            def finish(bank):
+                copy_turned(w_columns(i, 2 * half, 2 * half + 2), bank)
+
+            return turns(pairs_unsorted(w_start[i, half], 2), take_bank, finish, early)
+
+        def turns_plain(i):
+            def finish(bank):
+                copy_turned(w_columns(i, 1, 2), bank)
+
+            return turns(pairs_unsorted(w_plain[i], 1), block_bank, finish) if i <= LAST else []
+
+        def turns_late(i):
+            def finish(bank):
+                late_banks[i] = bank
+
+            return turns(pairs_sorted(w_late[i], 1), block_bank, finish) if i <= LAST else []
+
+        def turns_shared(i):
+            def finish(bank):
+                copy_turned(w_columns(i, 2, BLOCKS), bank)
+
+            return turns(pairs_sorted(w_shared[i], 2), ring_bank, finish) if i <= LAST else []
 
         def quantise_w(i):
-            if i > LAST:
-                return
-            w_codes[i] = work.tile([P, HALF], U32, name="w_code", align_bytes=64)
-            w_scales[i] = work.tile([P, HALF], U8, name="w_code_scale", align_bytes=64)
+            w_codes[i] = work.tile([P, UNIT], U32, name="w_code", align_bytes=64)
+            w_scales[i] = work.tile([P, UNIT], U8, name="w_code_scale", align_bytes=64)
             nc.vector.quantize_mx(out=w_codes[i][:].bitcast(FP8X4), scales=w_scales[i][:], in_=w_grouped[i][:])
 
         def quantise_t2(n):
-            if n > LAST:
-                return
-            b, half = divmod(n, 2)
-            if half == 0:
-                t2_codes[b] = work.tile([P, R], U32, name="t2_code", align_bytes=64)
-                t2_scales[b] = work.tile([P, R], U8, name="t2_code_scale", align_bytes=64)
-            m = slice(R // 2 * half, R // 2 * (half + 1))
-            nc.vector.quantize_mx(out=t2_codes[b][:, m].bitcast(FP8X4), scales=t2_scales[b][:, m], in_=t2_grouped[n][:])
+            if n <= LAST:
+                b, half = divmod(n, 2)
+                if half == 0:
+                    t2_codes[b] = work.tile([P, R], U32, name="t2_code", align_bytes=64)
+                    t2_scales[b] = work.tile([P, R], U8, name="t2_code_scale", align_bytes=64)
+                m = slice(R // 2 * half, R // 2 * (half + 1))
+                nc.vector.quantize_mx(out=t2_codes[b][:, m].bitcast(FP8X4), scales=t2_scales[b][:, m], in_=t2_grouped[n][:])
 
-        def quantise_h(i, first=0, count=HALF):
-            if i < 0:
-                return
+        def quantise_h(i, first=0, count=UNIT):
             if first == 0:
-                h_codes[i] = work.tile([P, HALF], U32, name="h_code", align_bytes=64)
-                h_scales[i] = work.tile([P, HALF], U8, name="h_code_scale", align_bytes=64)
+                h_codes[i] = work.tile([P, UNIT], U32, name="h_code", align_bytes=64)
+                h_scales[i] = work.tile([P, UNIT], U8, name="h_code_scale", align_bytes=64)
             n = slice(first, first + count)
             columns = h_grouped[i][:, PACK * first : PACK * (first + count)]
             nc.vector.quantize_mx(out=h_codes[i][:, n].bitcast(FP8X4), scales=h_scales[i][:, n], in_=columns)
 
-        def product_t1(index, steps):
+        def product_t1(index, steps, in_a_run=False):
             i, half = divmod(index, 2)
             if i > LAST:
-                for step in steps:
-                    turn(step)
                 return
-            t1_sb[i, half] = work.tile([P, 2, P, PACK], F32, name="t1_copy", bufs=T1_LEAD + 3)
+            t1_sb[index] = work.tile([P, 2, WIDE, 2], F32, name="t1_copy", bufs=T1_LEAD + 3)
             done = 0
-            contiguous = all(step[0] == "w" and step[1:3] in w_sorted for step in steps)
-            ends = (0, 0, 0, 8, 8, 8, 8, 8) if contiguous else [-(-len(steps) * n // 7) for n in range(1, 9)]
-            if len(steps) > 4 and not all(step[0] == "w" and step[1:3] in w_sorted for step in steps):
-                turn_banks[steps[0][:3]] = turn_bank(*steps[0][:3])
-            for pair in range(2):
-                bank = ring_bank([P, PACK, P])
+            for g in range(2):
+                bank = ring_bank([P, 2, WIDE])
                 for m in range(4):
-                    for k in range(2):
-                        rhs = x1_raw[i][:, k, WIDE * half + P * pair : WIDE * half + P * (pair + 1)]
-                        nc.tensor.matmul(bank[:, m, :], lhsT=a_perm[:, k, m, :], rhs=rhs, start=(k == 0), stop=(k == 1))
+                    e, k = divmod(m, 2)
+                    rhs = x1_raw[i][:, k, WIDE * half : WIDE * (half + 1)]
+                    nc.tensor.matmul(bank[:, e, :], lhsT=a_perm[:, k, 2 * g + e, :], rhs=rhs, start=(k == 0), stop=(k == 1))
                     if m == 3:
-                        nc.scalar.copy(out=t1_sb[i, half][:, pair, :, :], in_=bank[:].rearrange("p t o -> p o t"))
-                    until = min(len(steps), ends[4 * pair + m])
+                        nc.scalar.copy(out=t1_sb[index][:, g, :, :], in_=bank[:].rearrange("p e o -> p o e"))
+                    gap = 4 * g + m + 1
+                    if in_a_run:
+                        until = len(steps) if gap >= 4 else 0
+                    else:
+                        until = min(len(steps), -(-len(steps) * gap // GAPS))
                     for step in steps[done:until]:
-                        turn(step)
+                        step()
                     done = until
 
-        def product_t3(i, j, spare=False):
+        def product_t3(i, j, take_bank=t3_bank):
             b = i // 2
-            if spare:
-                bank = psum.tile([P, PACK, P], F32, name="unscaled_bank")
-            else:
-                bank = psum.tile([P, PACK, P], F32, name="t3_bank", bufs=3)
-            t3_banks[i, j] = bank
+            t3_banks[i, j] = take_bank([P, PACK, P])
             n = slice(P * j, P * (j + 1))
             for t in range(PACK):
                 m = slice(P * t, P * (t + 1))
                 nc.tensor.matmul_mx(
-                    out=bank[:, t, :],
+                    out=t3_banks[i, j][:, t, :],
                     lhsT=t2_codes[b][:, m].bitcast(FP8X4),
                     lhsT_scale=t2_scales[b][:, m],
                     rhs=w_codes[i][:, n].bitcast(FP8X4),
@@ -223,16 +250,17 @@ def tile_cptensorproduct_pa_t_w4_kernel(tc, x1, A, t2, w_bytes, w_scale, C_words
 
         def multiply_h(i, j):
             if j == 0:
-                h_grouped[i] = work.tile([P, PACK * HALF], BF16, name="h_by_column", align_bytes=64)
-            h = h_grouped[i][:, PACK * P * j : PACK * P * (j + 1)].rearrange("p (o t) -> p o t", t=PACK)
+                h_grouped[i] = work.tile([P, PACK * UNIT], BF16, name="h_by_column", align_bytes=64)
+            h = h_grouped[i][:, PACK * P * j : PACK * P * (j + 1)].rearrange("p (o g e) -> p o g e", g=2, e=2)
             half, part = divmod(j, 2)
-            t1 = t1_sb[i, half][:, part, :, :]
-            t3 = t3_banks[i, j][:].rearrange("p t o -> p o t")
+            t1 = t1_sb[2 * i + half][:, :, P * part : P * (part + 1), :].rearrange("p g o e -> p o g e")
+            t3 = t3_banks[i, j][:].rearrange("p (g e) o -> p o g e", g=2)
             nc.vector.tensor_tensor(out=h, in0=t3, in1=t1, op=MULT)
 
-        def product_out(i, m, first=0, count=HALF, spare=False):
+        def product_out(i, m, first=0, count=UNIT, take_bank=ring_bank, copy=nc.scalar.copy):
+            b, half = divmod(i, 2)
             n = slice(first, first + count)
-            bank = psum.tile([P, HALF], F32, name="t3_bank", bufs=3) if spare else ring_bank([P, HALF])
+            bank = take_bank([P, UNIT])
             nc.tensor.matmul_mx(
                 out=bank[:, :count],
                 lhsT=c_words[:, 2 * P * m : 2 * P * (m + 1)].bitcast(FP4X4),
@@ -242,13 +270,9 @@ def tile_cptensorproduct_pa_t_w4_kernel(tc, x1, A, t2, w_bytes, w_scale, C_words
                 start=True,
                 stop=True,
             )
-            return bank
-
-        def store_out(bank, copy, i, m, first=0, count=HALF):
-            b, half = divmod(i, 2)
-            result = work.tile([P, HALF], F32, name="out_copy", bufs=10)
+            result = work.tile([P, UNIT], F32, name="out_copy", bufs=RESULTS)
             copy(out=result[:, :count], in_=bank[:, :count])
-            col = half * HALF + first
+            col = half * UNIT + first
             nc.sync.dma_start(out=out[b, P * m : P * (m + 1), col : col + count], in_=result[:, :count])
 
         scale_cols = const.tile([P, PACK], F32)
@@ -257,20 +281,20 @@ def tile_cptensorproduct_pa_t_w4_kernel(tc, x1, A, t2, w_bytes, w_scale, C_words
         make_identity(nc, ident[:])
         c_scales = const.tile([P, D], U8, align_bytes=64)
         nc.vector.memset(c_scales[:].bitcast(I32), 0)
-
         ones = const.tile([P, 1], F32)
         nc.vector.memset(ones[:], 1.0)
-        load_w(0)
+
         a_raw = const.tile([P, 2, R], BF16)
         nc.sync.dma_start(out=a_raw[:], in_=A.rearrange("(p k) r -> p k r", k=2))
-        load_t2(0)
         load_x1(0)
+        load_w(0)
+        load_t2(0)
         load_w(1)
+        load_x1(1)
         load_t2(1)
         load_w(2)
         load_t2(2)
         load_t2(3)
-        load_x1(1)
         load_x1(2)
         c_words = const.tile([P, 2 * D], U8, align_bytes=64)
         nc.sync.dma_start(out=c_words[:], in_=C_words[0])
@@ -291,72 +315,82 @@ def tile_cptensorproduct_pa_t_w4_kernel(tc, x1, A, t2, w_bytes, w_scale, C_words
         scale_sorted = const.tile([P, CV], F32)
         target = scale_sorted[:].rearrange("p (u q e) -> p u q e", u=2, e=2)
         nc.scalar.copy(out=target, in_=row_bank[:].rearrange("p (u e) q -> p u q e", u=2))
-        widen_sorted(0, 0)
         a_perm = const.tile([P, 2, PACK, P], BF16)
         nc.vector.tensor_copy(out=a_perm[:], in_=a_raw[:].rearrange("p k (m t) -> p k t m", t=PACK))
-        scale_w(0, 1)
-        for step in turns("w", 0, 0) + turns("t2", 0):
-            turn(step)
-        scale_turned(0, 0)
-        scale_w(1, 0)
-        product_t1(0, turns("w", 0, 1) + turns("t2", 1))
-        scale_w(1, 1)
-        quantise_t2(0)
-        scale_w(2, 1)
-        product_t1(1, turns("w", 1, 0) + turns("w", 1, 1))
-        quantise_w(0)
-        quantise_t2(1)
-        widen_sorted(2, 0)
-        product_t1(2, turns("t2", 2) + turns("w", 2, 1))
-        widen_share(3, copy=nc.vector.tensor_copy)
-        product_t3(0, 0)
-        widen_share(4, 0, SPLIT // 2)
 
+        scale_start(0, 0)
+        scale_start(0, 1)
+        scale_start(1, 0)
+        product_t1(0, [])
+        product_t1(1, turns_t2(0, t3_bank, early=True) + turns_start(0, 0, block_bank))
+        scale_start(1, 1)
+        quantise_t2(0)
+        scale_start(2, 1)
+        product_t1(2, turns_start(0, 1, early=True) + turns_t2(1, t3_bank) + turns_start(1, 0, block_bank))
+        quantise_w(0)
+        scale_plain(2)
+        widen_late(2)
+        quantise_t2(1)
+        product_t1(3, turns_start(1, 1, early=True) + turns_t2(2, t3_bank) + turns_plain(2))
+        widen_shared(3, 0, SCALAR_WIDENS, nc.vector.tensor_copy)
+        product_t3(0, 0)
+        widen_shared(4, 0, SCALAR_WIDENS // 2, nc.scalar.copy)
+
+        t1_halves = list(range(T1_LEAD, 2 * UNITS + 1))
         for i in range(LAST):
+            widen_shared(i + 3, SCALAR_WIDENS, ROWS2, nc.vector.tensor_copy)
+            widen_late(i + 3)
             quantise_w(i + 1)
-            quantise_h(i - 1)
             if i > 0:
-                widen_share(i + 3, SPLIT, ROWS2, nc.vector.tensor_copy)
+                quantise_h(i - 1)
             quantise_t2(i + 2)
-            widen_sorted(i + 3, 0)
-            scale_share(i + 3, i + 2)
+            scale_plain(i + 3)
+            scale_shared(i + 3)
+
+            spare = i + 2 > LAST
             product_t3(i, 1)
             product_t3(i, 2)
-            if i >= LAST - 1:
-                product_t3(i, 3, spare=True)
+            if spare:
+                product_t3(i, 3, block_bank)
             if i > 1:
-                store_out(product_out(i - 2, 1), nc.scalar.copy, i - 2, 1)
-            product_t1(2 * i + T1_LEAD, turns("w", i + 2, 0) + (turns("w", i + 2, 1) if i > 0 else turns("t2", 3)))
-            widen_share(i + 4, SPLIT // 2, SPLIT)
+                product_out(i - 2, 1)
+            if i == 0:
+                product_t1(t1_halves.pop(0), turns_late(2) + turns_start(2, 1) + turns_t2(3))
+            elif i + 2 != LAST:
+                product_t1(t1_halves.pop(0), turns_late(i + 2) + turns_shared(i + 2), in_a_run=True)
+            else:
+                for step in turns_late(LAST) + turns_shared(LAST):
+                    step()
+            widen_shared(i + 4, SCALAR_WIDENS // 2, SCALAR_WIDENS, nc.scalar.copy)
             multiply_h(i, 0)
-            if i < LAST - 1:
+            if not spare:
                 product_t3(i, 3)
             multiply_h(i, 1)
             product_t3(i + 1, 0)
             if i > 0:
-                store_out(product_out(i - 1, 0), nc.scalar.copy, i - 1, 0)
-            product_t1(2 * i + T1_LEAD + 1, turns("t2", i + 4))
-            widen_share(i + 5, 0, SPLIT // 2)
+                product_out(i - 1, 0)
             multiply_h(i, 2)
-            scale_turned(i + 2, 0)
+            scale_late(i + 2)
+            product_t1(t1_halves.pop(0), turns_t2(i + 4) + turns_plain(i + 3))
+            widen_shared(i + 5, 0, SCALAR_WIDENS // 2, nc.scalar.copy)
             multiply_h(i, 3)
 
         product_t3(LAST, 1)
         product_t3(LAST, 2)
-        product_t3(LAST, 3, spare=True)
-        store_out(product_out(LAST - 2, 1), nc.scalar.copy, LAST - 2, 1)
+        product_t3(LAST, 3, block_bank)
+        product_out(LAST - 2, 1)
         multiply_h(LAST, 0)
         quantise_h(LAST - 1)
         for m in range(2):
-            store_out(product_out(LAST - 1, m), nc.scalar.copy, LAST - 1, m)
+            product_out(LAST - 1, m)
         multiply_h(LAST, 1)
         multiply_h(LAST, 2)
         quantise_h(LAST, 0, WIDE)
         for m in range(2):
-            store_out(product_out(LAST, m, 0, WIDE), nc.scalar.copy, LAST, m, 0, WIDE)
+            product_out(LAST, m, 0, WIDE)
         multiply_h(LAST, 3)
         for first in (WIDE, WIDE + P):
             quantise_h(LAST, first, P)
         for first in (WIDE, WIDE + P):
-            store_out(product_out(LAST, 0, first, P), nc.scalar.copy, LAST, 0, first, P)
-            store_out(product_out(LAST, 1, first, P, spare=True), nc.vector.tensor_copy, LAST, 1, first, P)
+            product_out(LAST, 0, first, P)
+            product_out(LAST, 1, first, P, t3_bank, nc.vector.tensor_copy)

@@ -332,13 +332,12 @@ def tile_cptensorproduct_pa_t_w4_kernel(tc, x1, A, t2, w_bytes, w_scale, C_words
         widen_late(2)
         quantise_t2(1)
         product_t1(3, turns_start(1, 1, early=True) + turns_t2(2, t3_bank) + turns_plain(2))
-        widen_shared(3, 0, SCALAR_WIDENS, nc.vector.tensor_copy)
+        widen_shared(3, 0, ROWS2, nc.vector.tensor_copy)
         product_t3(0, 0)
         widen_shared(4, 0, SCALAR_WIDENS // 2, nc.scalar.copy)
 
         t1_halves = list(range(T1_LEAD, 2 * UNITS + 1))
         for i in range(LAST):
-            widen_shared(i + 3, SCALAR_WIDENS, ROWS2, nc.vector.tensor_copy)
             widen_late(i + 3)
             quantise_w(i + 1)
             if i > 0:
@@ -346,6 +345,7 @@ def tile_cptensorproduct_pa_t_w4_kernel(tc, x1, A, t2, w_bytes, w_scale, C_words
             quantise_t2(i + 2)
             scale_plain(i + 3)
             scale_shared(i + 3)
+            widen_shared(i + 4, SCALAR_WIDENS, ROWS2, nc.gpsimd.tensor_copy)
 
             spare = i + 2 > LAST
             product_t3(i, 1)

@@ -99,9 +99,7 @@ def tile_cptensorproduct_pa_t_w4_kernel(tc, x1, A, t2, w_bytes, w_scale, C_words
         def widen_late(i):
             if i <= LAST:
                 w_late[i] = work.tile([P, CV], BF16, name="w_late", align_bytes=64)
-                target = w_late[i][:].rearrange("p (u q e) -> p q u e", u=2, e=2)
-                values = w_raw[i][:, :CV].bitcast(FP8).rearrange("p (q u e) -> p q u e", u=2, e=2)
-                nc.vector.tensor_scalar(out=target, in0=values, scalar1=ones[:], scalar2=None, op0=MULT)
+                nc.vector.tensor_copy(out=w_late[i][:], in_=w_raw[i][:, :CV].bitcast(FP8))
 
         def scale_late(i):
             if i <= LAST:
@@ -120,10 +118,9 @@ def tile_cptensorproduct_pa_t_w4_kernel(tc, x1, A, t2, w_bytes, w_scale, C_words
         def scale_shared(i):
             if i <= LAST:
                 w_shared[i] = handed_on(i - 1)
-                target = w_shared[i][:].rearrange("p (u j q e) -> p u j q e", u=2, j=2, e=2)
-                values = w_wide[i][:].rearrange("p (j q u e) -> p u j q e", j=2, u=2, e=2)
-                factors = scale_sorted[:].rearrange("p (u q e) -> p u q e", u=2, e=2)
-                factors = factors.unsqueeze(2).to_broadcast([P, 2, 2, P, 2])
+                target = w_shared[i][:].rearrange("p (j c) -> p j c", j=2)
+                values = w_wide[i][:].rearrange("p (j c) -> p j c", j=2)
+                factors = scale_rows[:].unsqueeze(1).to_broadcast([P, 2, CV])
                 nc.gpsimd.tensor_tensor(out=target, in0=values, in1=factors, op=MULT)
 
         def w_columns(i, first, last):
@@ -147,10 +144,6 @@ def tile_cptensorproduct_pa_t_w4_kernel(tc, x1, A, t2, w_bytes, w_scale, C_words
         def pairs_unsorted(tile, blocks):
             words = tile[:].bitcast(F32)
             return [[words[:, j * WIDE + u : (j + 1) * WIDE : 2] for j in range(blocks)] for u in range(2)]
-
-        def pairs_sorted(tile, blocks):
-            words = tile[:].bitcast(F32)
-            return [[words[:, (u * blocks + j) * P : (u * blocks + j + 1) * P] for j in range(blocks)] for u in range(2)]
 
         def copy_turned(target, bank):
             words = target.bitcast(F32).rearrange("p (r u) -> p r u", u=2)
@@ -179,13 +172,13 @@ def tile_cptensorproduct_pa_t_w4_kernel(tc, x1, A, t2, w_bytes, w_scale, C_words
             def finish(bank):
                 late_banks[i] = bank
 
-            return turns(pairs_sorted(w_late[i], 1), block_bank, finish) if i <= LAST else []
+            return turns(pairs_unsorted(w_late[i], 1), block_bank, finish) if i <= LAST else []
 
         def turns_shared(i):
             def finish(bank):
                 copy_turned(w_columns(i, 2, BLOCKS), bank)
 
-            return turns(pairs_sorted(w_shared[i], 2), ring_bank, finish) if i <= LAST else []
+            return turns(pairs_unsorted(w_shared[i], 2), ring_bank, finish) if i <= LAST else []
 
         def quantise_w(i):
             w_codes[i] = work.tile([P, UNIT], U32, name="w_code", align_bytes=64)
@@ -281,8 +274,6 @@ def tile_cptensorproduct_pa_t_w4_kernel(tc, x1, A, t2, w_bytes, w_scale, C_words
         make_identity(nc, ident[:])
         c_scales = const.tile([P, D], U8, align_bytes=64)
         nc.vector.memset(c_scales[:].bitcast(I32), 0)
-        ones = const.tile([P, 1], F32)
-        nc.vector.memset(ones[:], 1.0)
 
         a_raw = const.tile([P, 2, R], BF16)
         nc.sync.dma_start(out=a_raw[:], in_=A.rearrange("(p k) r -> p k r", k=2))
@@ -312,9 +303,6 @@ def tile_cptensorproduct_pa_t_w4_kernel(tc, x1, A, t2, w_bytes, w_scale, C_words
             nc.tensor.transpose(row_bank[:, t, :], scale_cols[:, t : t + 1].to_broadcast([P, P]), ident[:])
         scale_rows = const.tile([P, CV], F32)
         nc.scalar.copy(out=scale_rows[:].rearrange("p (q t) -> p q t", t=PACK), in_=row_bank[:].rearrange("p t q -> p q t"))
-        scale_sorted = const.tile([P, CV], F32)
-        target = scale_sorted[:].rearrange("p (u q e) -> p u q e", u=2, e=2)
-        nc.scalar.copy(out=target, in_=row_bank[:].rearrange("p (u e) q -> p u q e", u=2))
         a_perm = const.tile([P, 2, PACK, P], BF16)
         nc.vector.tensor_copy(out=a_perm[:], in_=a_raw[:].rearrange("p k (m t) -> p k t m", t=PACK))
 
@@ -357,7 +345,7 @@ def tile_cptensorproduct_pa_t_w4_kernel(tc, x1, A, t2, w_bytes, w_scale, C_words
             if i == 0:
                 product_t1(t1_halves.pop(0), turns_late(2) + turns_start(2, 1) + turns_t2(3))
             elif i + 2 != LAST:
-                product_t1(t1_halves.pop(0), turns_late(i + 2) + turns_shared(i + 2), in_a_run=True)
+                product_t1(t1_halves.pop(0), turns_late(i + 2) + turns_shared(i + 2))
             else:
                 for step in turns_late(LAST) + turns_shared(LAST):
                     step()

@@ -27,7 +27,7 @@ WIDE = 2 * P
 
 SCALAR_WIDENS = 768
 T1_LEAD = 4
-GAPS = 7
+GAPS = 3
 HANDED_ON = 4
 T3_BANKS = 3
 RING = 4
@@ -202,25 +202,21 @@ def tile_cptensorproduct_pa_t_w4_kernel(tc, x1, A, t2, w_bytes, w_scale, C_words
             columns = h_grouped[i][:, PACK * first : PACK * (first + count)]
             nc.vector.quantize_mx(out=h_codes[i][:, n].bitcast(FP8X4), scales=h_scales[i][:, n], in_=columns)
 
-        def product_t1(index, steps, in_a_run=False):
+        def product_t1(index, steps):
             i, half = divmod(index, 2)
             if i > LAST:
                 return
-            t1_sb[index] = work.tile([P, 2, WIDE, 2], F32, name="t1_copy", bufs=T1_LEAD + 3)
+            if half == 0:
+                t1_sb[i] = work.tile([P, PACK, UNIT], F32, name="t1_copy", bufs=T1_LEAD // 2 + 2)
             done = 0
-            for g in range(2):
-                bank = ring_bank([P, 2, WIDE])
-                for m in range(4):
-                    e, k = divmod(m, 2)
-                    rhs = x1_raw[i][:, k, WIDE * half : WIDE * (half + 1)]
-                    nc.tensor.matmul(bank[:, e, :], lhsT=a_perm[:, k, 2 * g + e, :], rhs=rhs, start=(k == 0), stop=(k == 1))
-                    if m == 3:
-                        nc.scalar.copy(out=t1_sb[index][:, g, :, :], in_=bank[:].rearrange("p e o -> p o e"))
-                    gap = 4 * g + m + 1
-                    if in_a_run:
-                        until = len(steps) if gap >= 4 else 0
-                    else:
-                        until = min(len(steps), -(-len(steps) * gap // GAPS))
+            for e in range(2):
+                t = 2 * half + e
+                bank = ring_bank([P, UNIT])
+                for k in range(2):
+                    nc.tensor.matmul(bank[:], lhsT=a_perm[:, k, t, :], rhs=x1_raw[i][:, k, :], start=(k == 0), stop=(k == 1))
+                    if k == 1:
+                        nc.scalar.copy(out=t1_sb[i][:, t, :], in_=bank[:])
+                    until = min(len(steps), -(-len(steps) * (2 * e + k + 1) // GAPS))
                     for step in steps[done:until]:
                         step()
                     done = until
@@ -244,10 +240,9 @@ def tile_cptensorproduct_pa_t_w4_kernel(tc, x1, A, t2, w_bytes, w_scale, C_words
         def multiply_h(i, j):
             if j == 0:
                 h_grouped[i] = work.tile([P, PACK * UNIT], BF16, name="h_by_column", align_bytes=64)
-            h = h_grouped[i][:, PACK * P * j : PACK * P * (j + 1)].rearrange("p (o g e) -> p o g e", g=2, e=2)
-            half, part = divmod(j, 2)
-            t1 = t1_sb[2 * i + half][:, :, P * part : P * (part + 1), :].rearrange("p g o e -> p o g e")
-            t3 = t3_banks[i, j][:].rearrange("p (g e) o -> p o g e", g=2)
+            h = h_grouped[i][:, PACK * P * j : PACK * P * (j + 1)].rearrange("p (c n t) -> p c t n", n=2, t=PACK)
+            t1 = t1_sb[i][:, :, P * j : P * (j + 1)].rearrange("p t (c n) -> p c t n", n=2)
+            t3 = t3_banks[i, j][:].rearrange("p t (c n) -> p c t n", n=2)
             nc.vector.tensor_tensor(out=h, in0=t3, in1=t1, op=MULT)
 
         def product_out(i, m, first=0, count=UNIT, take_bank=ring_bank, copy=nc.scalar.copy):

@@ -23,15 +23,21 @@ BLOCKS = UNIT // P
 UNITS = NB * CO // UNIT
 LAST = UNITS - 1
 ROWS2 = 2 * CV
-WIDE = 2 * P
+WORDS = CV // 2
+SAMPLE_COLS = 2 * BLOCKS * CV
+SHARED_FIRST, SHARED_COUNT = 2, 3
 
-SCALAR_WIDENS = 768
-T1_LEAD = 4
+GPSIMD_WIDENS = 2816
+FIRST_WIDENS = 1792
+T1_LEAD = 3
+SKIPS = (2, 10)
+EXTRA = (12,)
 GAPS = 3
-HANDED_ON = 4
+HANDED_ON = 3
 T3_BANKS = 3
 RING = 4
 RESULTS = 10
+KEPT = 12
 
 
 def tile_cptensorproduct_pa_t_w4_kernel(tc, x1, A, t2, w_bytes, w_scale, C_words, C_scales, out):
@@ -44,10 +50,10 @@ def tile_cptensorproduct_pa_t_w4_kernel(tc, x1, A, t2, w_bytes, w_scale, C_words
         ctx.enter_context(tc.manual_schedule())
 
         x1_raw, t2_raw, w_raw = {}, {}, {}
-        w_late, w_plain, w_wide, w_shared, w_start = {}, {}, {}, {}, {}
+        w_wide, w_shared, w_plain, late_banks = {}, {}, {}, {}
         w_grouped, w_codes, w_scales = {}, {}, {}
         t2_grouped, t2_codes, t2_scales = {}, {}, {}
-        t1_sb, t3_banks, late_banks = {}, {}, {}
+        t1_sb, t3_banks = {}, {}
         h_grouped, h_codes, h_scales = {}, {}, {}
         ring_taken = []
 
@@ -58,79 +64,67 @@ def tile_cptensorproduct_pa_t_w4_kernel(tc, x1, A, t2, w_bytes, w_scale, C_words
         def t3_bank(shape):
             return psum.tile(shape, F32, name="t3_bank", bufs=T3_BANKS)
 
-        def block_bank(shape):
-            return psum.tile(shape, F32, name="block_bank")
+        def late_bank(shape):
+            return psum.tile(shape, F32, name="late_bank")
 
-        def handed_on(n):
-            return work.tile([P, ROWS2], BF16, name="handed_on%d" % (n % HANDED_ON), bufs=1, align_bytes=64)
+        def handed_on(n, columns):
+            return work.tile([P, columns], BF16, name="handed_on%d" % (n % (2 * HANDED_ON)), bufs=1, align_bytes=64)
 
-        def load_w(i):
+        def load_w(i, first=0, last=BLOCKS):
             b, half = divmod(i, 2)
-            w_raw[i] = loads.tile([P, BLOCKS * CV], U8, name="w_raw_bytes")
-            rows = w_bytes[b, half * UNIT : (half + 1) * UNIT, :].rearrange("(j p) c -> p j c", p=P)
-            nc.sync.dma_start(out=w_raw[i][:].rearrange("p (j c) -> p j c", j=BLOCKS), in_=rows)
+            if b not in w_raw:
+                w_raw[b] = loads.tile([P, SAMPLE_COLS], U8, name="w_raw_bytes", bufs=NB)
+            j0, j1 = BLOCKS * half + first, BLOCKS * half + last
+            rows = w_bytes[b, j0 * P : j1 * P, :].rearrange("(j p) c -> p j c", p=P)
+            nc.sync.dma_start(out=w_raw[b][:, j0 * CV : j1 * CV].rearrange("p (j c) -> p j c", c=CV), in_=rows)
 
         def load_t2(n):
             b, half = divmod(n, 2)
-            t2_raw[n] = loads.tile([P, ROWS2], BF16, name="t2_rows")
+            t2_raw[n] = loads.tile([P, ROWS2], BF16, name="t2_rows", bufs=KEPT)
             rows = t2[b].rearrange("(m t) c -> m (t c)", t=PACK)
             nc.sync.dma_start(out=t2_raw[n][:], in_=rows[:, half * ROWS2 : (half + 1) * ROWS2])
 
         def load_x1(i):
             b, half = divmod(i, 2)
-            x1_raw[i] = loads.tile([P, 2, UNIT], BF16, name="x1_rows")
+            x1_raw[i] = loads.tile([P, 2, UNIT], BF16, name="x1_rows", bufs=KEPT)
             rows = x1[b].rearrange("(p k) o -> p k o", k=2)
             nc.sync.dma_start(out=x1_raw[i][:], in_=rows[:, :, half * UNIT : (half + 1) * UNIT])
 
-        def scale_block(i, j, target):
-            values = w_raw[i][:, j * CV : (j + 1) * CV].bitcast(FP8)
-            nc.vector.tensor_tensor(out=target, in0=values, in1=scale_rows[:], op=MULT)
+        def scale_plain(b, j, count):
+            w_plain[b, j] = work.tile([P, count * CV], BF16, name="w_plain", align_bytes=64)
+            values = w_raw[b][:, j * CV : (j + count) * CV].bitcast(FP8)
+            nc.vector.tensor_tensor(out=w_plain[b, j][:], in0=values, in1=scale_rows[:, : count * CV], op=MULT)
 
-        def scale_start(i, half):
-            w_start[i, half] = work.tile([P, ROWS2], BF16, name="w_start", bufs=4, align_bytes=64)
-            for j in range(2):
-                scale_block(i, 2 * half + j, w_start[i, half][:, j * CV : (j + 1) * CV])
+        def widen(b, first, last, copy):
+            if b < NB:
+                copy(out=w_wide[b][:, first:last], in_=w_raw[b][:, first:last].bitcast(FP8))
 
-        def scale_plain(i):
-            if i <= LAST:
-                w_plain[i] = work.tile([P, CV], BF16, name="w_plain", align_bytes=64)
-                scale_block(i, 1, w_plain[i][:])
+        def scale_late(b, j, count):
+            values = late_banks[b, j][:].rearrange("p u r -> p (u r)").bitcast(BF16)
+            values = values.rearrange("p (u r e) -> p r u e", u=2, e=2)
+            factors = scale_cols[:].rearrange("p (u e) -> p u e", u=2).unsqueeze(1).to_broadcast([P, count * P, 2, 2])
+            target = w_columns(b, j, count).rearrange("p (r u e) -> p r u e", u=2, e=2)
+            nc.vector.tensor_tensor(out=target, in0=values, in1=factors, op=MULT)
 
-        def widen_late(i):
-            if i <= LAST:
-                w_late[i] = work.tile([P, CV], BF16, name="w_late", align_bytes=64)
-                nc.vector.tensor_copy(out=w_late[i][:], in_=w_raw[i][:, :CV].bitcast(FP8))
+        def scale_shared(b, first, n):
+            w_shared[b, first] = handed_on(n, SHARED_COUNT * CV)
+            target = w_shared[b, first][:].rearrange("p (u j q e) -> p u j q e", u=2, j=SHARED_COUNT, e=2)
+            values = w_wide[b][:, first * CV : (first + SHARED_COUNT) * CV]
+            values = values.rearrange("p (j q u e) -> p u j q e", j=SHARED_COUNT, u=2, e=2)
+            factors = scale_sorted[:].rearrange("p (u q e) -> p u q e", u=2, e=2)
+            factors = factors.unsqueeze(2).to_broadcast([P, 2, SHARED_COUNT, P, 2])
+            nc.gpsimd.tensor_tensor(out=target, in0=values, in1=factors, op=MULT)
 
-        def scale_late(i):
-            if i <= LAST:
-                values = late_banks[i][:].rearrange("p u r -> p (u r)").bitcast(BF16)
-                values = values.rearrange("p (u r e) -> p r u e", u=2, e=2)
-                factors = scale_cols[:].rearrange("p (u e) -> p u e", u=2).unsqueeze(1).to_broadcast([P, P, 2, 2])
-                target = w_columns(i, 0, 1).rearrange("p (r u e) -> p r u e", u=2, e=2)
-                nc.vector.tensor_tensor(out=target, in0=values, in1=factors, op=MULT)
-
-        def widen_shared(i, first, last, copy):
-            if i <= LAST:
-                if i not in w_wide:
-                    w_wide[i] = work.tile([P, ROWS2], BF16, name="w_wide")
-                copy(out=w_wide[i][:, first:last], in_=w_raw[i][:, ROWS2 + first : ROWS2 + last].bitcast(FP8))
-
-        def scale_shared(i):
-            if i <= LAST:
-                w_shared[i] = handed_on(i - 1)
-                target = w_shared[i][:].rearrange("p (j c) -> p j c", j=2)
-                values = w_wide[i][:].rearrange("p (j c) -> p j c", j=2)
-                factors = scale_rows[:].unsqueeze(1).to_broadcast([P, 2, CV])
-                nc.gpsimd.tensor_tensor(out=target, in0=values, in1=factors, op=MULT)
-
-        def w_columns(i, first, last):
+        def w_columns(b, j, count):
+            half, first = divmod(j, BLOCKS)
+            i = 2 * b + half
             if i not in w_grouped:
                 w_grouped[i] = work.tile([P, PACK * UNIT], BF16, name="w_by_column", align_bytes=64)
-            return w_grouped[i][:, PACK * P * first : PACK * P * last]
+            return w_grouped[i][:, PACK * P * first : PACK * P * (first + count)]
 
-        def turns(sources, take_bank, finish, early=False):
+        def turns(sources, take_bank, finish):
             blocks = len(sources[0])
-            taken = [take_bank([P, 2, blocks * P])] if early else []
+            taken = []
 
             def turn(u, j):
                 if not taken:
@@ -141,85 +135,85 @@ def tile_cptensorproduct_pa_t_w4_kernel(tc, x1, A, t2, w_bytes, w_scale, C_words
 
             return [lambda u=u, j=j: turn(u, j) for u in range(2) for j in range(blocks)]
 
-        def pairs_unsorted(tile, blocks):
+        def pairs_unsorted(tile, first, count):
             words = tile[:].bitcast(F32)
-            return [[words[:, j * WIDE + u : (j + 1) * WIDE : 2] for j in range(blocks)] for u in range(2)]
+            return [[words[:, j * WORDS + u : (j + 1) * WORDS : 2] for j in range(first, first + count)] for u in range(2)]
+
+        def pairs_sorted(tile, blocks, first, count):
+            words = tile[:].bitcast(F32)
+            return [[words[:, (u * blocks + j) * P : (u * blocks + j + 1) * P] for j in range(first, first + count)] for u in range(2)]
 
         def copy_turned(target, bank):
             words = target.bitcast(F32).rearrange("p (r u) -> p r u", u=2)
             nc.scalar.copy(out=words, in_=bank[:].rearrange("p u r -> p r u"))
 
-        def turns_t2(n, take_bank=ring_bank, early=False):
+        def turns_t2(n, take_bank=ring_bank):
             def finish(bank):
-                t2_grouped[n] = handed_on(n)
+                t2_grouped[n] = handed_on(n, ROWS2)
                 copy_turned(t2_grouped[n][:], bank)
 
-            return turns(pairs_unsorted(t2_raw[n], 2), take_bank, finish, early) if n <= LAST else []
+            return turns(pairs_unsorted(t2_raw[n], 0, 2), take_bank, finish) if n <= LAST else []
 
-        def turns_start(i, half, take_bank=ring_bank, early=False):
+        def turns_plain(b, j, count, take_bank=ring_bank):
+            return turns(pairs_unsorted(w_plain[b, j], 0, count), take_bank, lambda bank: copy_turned(w_columns(b, j, count), bank))
+
+        def turns_shared(b, j, count, first=SHARED_FIRST, take_bank=ring_bank):
+            sources = pairs_sorted(w_shared[b, first], SHARED_COUNT, j - first, count)
+            return turns(sources, take_bank, lambda bank: copy_turned(w_columns(b, j, count), bank))
+
+        def turns_late(b, j, count, sources=None, take_bank=late_bank, at_once=False):
             def finish(bank):
-                copy_turned(w_columns(i, 2 * half, 2 * half + 2), bank)
+                late_banks[b, j] = bank
+                if at_once:
+                    scale_late(b, j, count)
 
-            return turns(pairs_unsorted(w_start[i, half], 2), take_bank, finish, early)
-
-        def turns_plain(i):
-            def finish(bank):
-                copy_turned(w_columns(i, 1, 2), bank)
-
-            return turns(pairs_unsorted(w_plain[i], 1), block_bank, finish) if i <= LAST else []
-
-        def turns_late(i):
-            def finish(bank):
-                late_banks[i] = bank
-
-            return turns(pairs_unsorted(w_late[i], 1), block_bank, finish) if i <= LAST else []
-
-        def turns_shared(i):
-            def finish(bank):
-                copy_turned(w_columns(i, 2, BLOCKS), bank)
-
-            return turns(pairs_unsorted(w_shared[i], 2), ring_bank, finish) if i <= LAST else []
+            return turns(sources or pairs_unsorted(w_wide[b], j, count), take_bank, finish)
 
         def quantise_w(i):
-            w_codes[i] = work.tile([P, UNIT], U32, name="w_code", align_bytes=64)
-            w_scales[i] = work.tile([P, UNIT], U8, name="w_code_scale", align_bytes=64)
+            w_codes[i] = work.tile([P, UNIT], U32, name="w_code", bufs=3, align_bytes=64)
+            w_scales[i] = work.tile([P, UNIT], U8, name="w_code_scale", bufs=3, align_bytes=64)
             nc.vector.quantize_mx(out=w_codes[i][:].bitcast(FP8X4), scales=w_scales[i][:], in_=w_grouped[i][:])
 
         def quantise_t2(n):
             if n <= LAST:
                 b, half = divmod(n, 2)
                 if half == 0:
-                    t2_codes[b] = work.tile([P, R], U32, name="t2_code", align_bytes=64)
-                    t2_scales[b] = work.tile([P, R], U8, name="t2_code_scale", align_bytes=64)
+                    t2_codes[b] = work.tile([P, R], U32, name="t2_code", bufs=2, align_bytes=64)
+                    t2_scales[b] = work.tile([P, R], U8, name="t2_code_scale", bufs=2, align_bytes=64)
                 m = slice(R // 2 * half, R // 2 * (half + 1))
                 nc.vector.quantize_mx(out=t2_codes[b][:, m].bitcast(FP8X4), scales=t2_scales[b][:, m], in_=t2_grouped[n][:])
 
         def quantise_h(i, first=0, count=UNIT):
             if first == 0:
-                h_codes[i] = work.tile([P, UNIT], U32, name="h_code", align_bytes=64)
-                h_scales[i] = work.tile([P, UNIT], U8, name="h_code_scale", align_bytes=64)
+                h_codes[i] = work.tile([P, UNIT], U32, name="h_code", bufs=3, align_bytes=64)
+                h_scales[i] = work.tile([P, UNIT], U8, name="h_code_scale", bufs=3, align_bytes=64)
             n = slice(first, first + count)
             columns = h_grouped[i][:, PACK * first : PACK * (first + count)]
             nc.vector.quantize_mx(out=h_codes[i][:, n].bitcast(FP8X4), scales=h_scales[i][:, n], in_=columns)
 
-        def product_t1(index, steps):
-            i, half = divmod(index, 2)
-            if i > LAST:
-                return
-            if half == 0:
-                t1_sb[i] = work.tile([P, PACK, UNIT], F32, name="t1_copy", bufs=T1_LEAD // 2 + 2)
+        def a_columns(n, k):
+            t = n % PACK
+            return a_raw[:, k, t:R:PACK] if n < 2 else a_perm[:, k, t, :]
+
+        def product_t1(slots, steps):
+            slots = [n for n in slots if n < PACK * UNITS]
+            gaps = max(2 * len(slots) - 1, 1)
             done = 0
-            for e in range(2):
-                t = 2 * half + e
+            for place, n in enumerate(slots):
+                i, t = divmod(n, PACK)
+                if t == 0:
+                    t1_sb[i] = work.tile([P, PACK, UNIT], F32, name="t1_copy", bufs=4)
                 bank = ring_bank([P, UNIT])
                 for k in range(2):
-                    nc.tensor.matmul(bank[:], lhsT=a_perm[:, k, t, :], rhs=x1_raw[i][:, k, :], start=(k == 0), stop=(k == 1))
+                    nc.tensor.matmul(bank[:], lhsT=a_columns(n, k), rhs=x1_raw[i][:, k, :], start=(k == 0), stop=(k == 1))
                     if k == 1:
                         nc.scalar.copy(out=t1_sb[i][:, t, :], in_=bank[:])
-                    until = min(len(steps), -(-len(steps) * (2 * e + k + 1) // GAPS))
+                    until = min(len(steps), -(-len(steps) * (2 * place + k + 1) // gaps))
                     for step in steps[done:until]:
                         step()
                     done = until
+            for step in steps[done:]:
+                step()
 
         def product_t3(i, j, take_bank=t3_bank):
             b = i // 2
@@ -239,7 +233,7 @@ def tile_cptensorproduct_pa_t_w4_kernel(tc, x1, A, t2, w_bytes, w_scale, C_words
 
         def multiply_h(i, j):
             if j == 0:
-                h_grouped[i] = work.tile([P, PACK * UNIT], BF16, name="h_by_column", align_bytes=64)
+                h_grouped[i] = work.tile([P, PACK * UNIT], BF16, name="h_by_column", bufs=2, align_bytes=64)
             h = h_grouped[i][:, PACK * P * j : PACK * P * (j + 1)].rearrange("p (c n t) -> p c t n", n=2, t=PACK)
             t1 = t1_sb[i][:, :, P * j : P * (j + 1)].rearrange("p t (c n) -> p c t n", n=2)
             t3 = t3_banks[i, j][:].rearrange("p t (c n) -> p c t n", n=2)
@@ -269,82 +263,122 @@ def tile_cptensorproduct_pa_t_w4_kernel(tc, x1, A, t2, w_bytes, w_scale, C_words
         make_identity(nc, ident[:])
         c_scales = const.tile([P, D], U8, align_bytes=64)
         nc.vector.memset(c_scales[:].bitcast(I32), 0)
+        ones = const.tile([P, 1], F32)
+        nc.vector.memset(ones[:], 1.0)
 
+        load_w(0)
         a_raw = const.tile([P, 2, R], BF16)
         nc.sync.dma_start(out=a_raw[:], in_=A.rearrange("(p k) r -> p k r", k=2))
         load_x1(0)
-        load_w(0)
-        load_t2(0)
         load_w(1)
-        load_x1(1)
+        load_t2(0)
         load_t2(1)
+        load_x1(1)
         load_w(2)
         load_t2(2)
+        load_w(3)
+        load_w(4)
         load_t2(3)
-        load_x1(2)
         c_words = const.tile([P, 2 * D], U8, align_bytes=64)
         nc.sync.dma_start(out=c_words[:], in_=C_words[0])
         for q in range(4):
             rows = C_scales[0, 4 * q : 4 * q + 4, :].bitcast(I32)
             nc.sync.dma_start(out=c_scales[32 * q : 32 * q + 4, :].bitcast(I32), in_=rows)
-        for i in range(3, UNITS):
-            load_w(i)
-            if i < LAST:
-                load_t2(i + 1)
-            load_x1(i)
+        for i in range(2, UNITS):
+            if i < KEPT:
+                load_x1(i)
+            if i + 3 <= LAST:
+                load_w(i + 3)
+            if i + 2 < KEPT:
+                load_t2(i + 2)
 
         row_bank = ring_bank([P, PACK, P])
         for t in range(PACK):
             nc.tensor.transpose(row_bank[:, t, :], scale_cols[:, t : t + 1].to_broadcast([P, P]), ident[:])
-        scale_rows = const.tile([P, CV], F32)
-        nc.scalar.copy(out=scale_rows[:].rearrange("p (q t) -> p q t", t=PACK), in_=row_bank[:].rearrange("p t q -> p q t"))
+        scale_rows = const.tile([P, ROWS2], F32)
+        for half in range(2):
+            target = scale_rows[:, half * CV : (half + 1) * CV].rearrange("p (q t) -> p q t", t=PACK)
+            nc.scalar.copy(out=target, in_=row_bank[:].rearrange("p t q -> p q t"))
         a_perm = const.tile([P, 2, PACK, P], BF16)
-        nc.vector.tensor_copy(out=a_perm[:], in_=a_raw[:].rearrange("p k (m t) -> p k t m", t=PACK))
+        nc.scalar.copy(out=a_perm[:], in_=a_raw[:].rearrange("p k (m t) -> p k t m", t=PACK))
 
-        scale_start(0, 0)
-        scale_start(0, 1)
-        scale_start(1, 0)
-        product_t1(0, [])
-        product_t1(1, turns_t2(0, t3_bank, early=True) + turns_start(0, 0, block_bank))
-        scale_start(1, 1)
+        w_first = const.tile([P, ROWS2], BF16, align_bytes=64)
+        for j in range(2):
+            target = w_first[:].rearrange("p (u j q e) -> p j q u e", u=2, j=2, e=2)[:, j]
+            values = w_raw[0][:, j * CV : (j + 1) * CV].bitcast(FP8).rearrange("p (q u e) -> p q u e", u=2, e=2)
+            nc.vector.tensor_scalar(out=target, in0=values, scalar1=ones[:], scalar2=None, op0=MULT)
+        for step in turns_late(0, 0, 2, pairs_sorted(w_first, 2, 0, 2)):
+            step()
+        scale_plain(0, 2, 1)
+        scale_plain(0, 3, 1)
+        scale_late(0, 0, 2)
+        scale_plain(0, 4, 2)
+        product_t1([0], [])
+        scale_sorted = const.tile([P, CV], F32)
+        target = scale_sorted[:].rearrange("p (u q e) -> p u q e", u=2, e=2)
+        nc.scalar.copy(out=target, in_=scale_rows[:, :CV].rearrange("p (q u e) -> p u q e", u=2, e=2))
+        product_t1([1], [])
+        product_t1([2], turns_plain(0, 2, 1, t3_bank) + turns_plain(0, 3, 1, t3_bank) + turns_t2(0, t3_bank))
+        scale_plain(0, 6, 2)
+        product_t1([3], turns_t2(1, late_bank))
         quantise_t2(0)
-        scale_start(2, 1)
-        product_t1(2, turns_start(0, 1, early=True) + turns_t2(1, t3_bank) + turns_start(1, 0, block_bank))
         quantise_w(0)
-        scale_plain(2)
-        widen_late(2)
+        scale_plain(1, 0, 2)
         quantise_t2(1)
-        product_t1(3, turns_start(1, 1, early=True) + turns_t2(2, t3_bank) + turns_plain(2))
-        widen_shared(3, 0, ROWS2, nc.vector.tensor_copy)
+        product_t1([4, 5], turns_plain(0, 4, 2, t3_bank) + turns_plain(0, 6, 2, t3_bank) + turns_t2(2, late_bank))
+        product_t1([6], turns_plain(1, 0, 2))
+        scale_plain(1, 2, 2)
+        w_wide[1] = handed_on(0, SAMPLE_COLS)
+        widen(1, 5 * CV, SAMPLE_COLS, nc.vector.tensor_copy)
         product_t3(0, 0)
-        widen_shared(4, 0, SCALAR_WIDENS // 2, nc.scalar.copy)
 
-        t1_halves = list(range(T1_LEAD, 2 * UNITS + 1))
+        t1_slots = list(range(7, PACK * (UNITS + 2)))
         for i in range(LAST):
-            widen_late(i + 3)
-            quantise_w(i + 1)
-            if i > 0:
+            b, second = divmod(i + 2, 2)
+            busy = i + 2 < LAST
+            if i == 1:
+                scale_plain(1, 4, 1)
+            if second or i + 1 == LAST:
+                quantise_w(i + 1)
+                quantise_t2(i + 2)
                 quantise_h(i - 1)
-            quantise_t2(i + 2)
-            scale_plain(i + 3)
-            scale_shared(i + 3)
-            widen_shared(i + 4, SCALAR_WIDENS, ROWS2, nc.gpsimd.tensor_copy)
+            else:
+                if i > 0:
+                    quantise_h(i - 1)
+                quantise_t2(i + 2)
+                quantise_w(i + 1)
+            if second == 0 and b + 1 < NB:
+                w_wide[b + 1] = handed_on(i + 2, SAMPLE_COLS)
+                if i == 0:
+                    widen(b + 1, 5 * CV - FIRST_WIDENS, 5 * CV, nc.gpsimd.tensor_copy)
+                else:
+                    widen(b + 1, 0, GPSIMD_WIDENS, nc.gpsimd.tensor_copy)
+            elif second == 1 and b + 1 < NB:
+                scale_shared(b + 1, SHARED_FIRST, i + 2)
+            elif i + 3 == LAST:
+                scale_shared(b, 5, i + 2)
 
-            spare = i + 2 > LAST
             product_t3(i, 1)
             product_t3(i, 2)
+            spare = i + 2 > LAST
             if spare:
-                product_t3(i, 3, block_bank)
+                product_t3(i, 3, late_bank)
             if i > 1:
                 product_out(i - 2, 1)
+            early, pair = ((4, 1), 5) if second else ((2, 2), 0)
             if i == 0:
-                product_t1(t1_halves.pop(0), turns_late(2) + turns_start(2, 1) + turns_t2(3))
-            elif i + 2 != LAST:
-                product_t1(t1_halves.pop(0), turns_late(i + 2) + turns_shared(i + 2))
+                steps = turns_plain(1, 2, 2) + turns_t2(3)
+            elif i == 1:
+                steps = turns_plain(b, *early) + turns_late(b, pair, 2)
+            elif busy and second:
+                steps = turns_shared(b, *early) + turns_late(b, pair, 2)
+            elif busy:
+                steps = turns_late(b, pair, 2) + turns_shared(b, *early)
+            elif i + 2 == LAST:
+                steps = turns_shared(b, 4, 1) + turns_shared(b, 5, 2, 5, late_bank) + turns_shared(b, 7, 1, 5)
             else:
-                for step in turns_late(LAST) + turns_shared(LAST):
-                    step()
-            widen_shared(i + 4, SCALAR_WIDENS // 2, SCALAR_WIDENS, nc.scalar.copy)
+                steps = []
+            product_t1([t1_slots.pop(0) for n in range(2)], steps)
             multiply_h(i, 0)
             if not spare:
                 product_t3(i, 3)
@@ -352,15 +386,33 @@ def tile_cptensorproduct_pa_t_w4_kernel(tc, x1, A, t2, w_bytes, w_scale, C_words
             product_t3(i + 1, 0)
             if i > 0:
                 product_out(i - 1, 0)
+            if i > 0 and busy:
+                scale_late(b, pair, 2)
+            steps = turns_t2(i + 4)
+            if second and busy:
+                steps = steps[:2] + turns_late(b, 7, 1) + steps[2:]
+            product_t1([t1_slots.pop(0) for n in range(1 if i in SKIPS else 3 if i in EXTRA else 2)], steps)
+            if i == 0:
+                widen(2, 0, 5 * CV - FIRST_WIDENS, nc.scalar.copy)
+            elif i == 1:
+                widen(2, 5 * CV, 7 * CV, nc.scalar.copy)
+            elif second == 0:
+                if i == 2:
+                    widen(2, 7 * CV, SAMPLE_COLS, nc.scalar.copy)
+                widen(b + 1, GPSIMD_WIDENS, SAMPLE_COLS if b + 2 == NB else 7 * CV, nc.scalar.copy)
+            elif b + 2 < NB:
+                widen(b + 1, 7 * CV, SAMPLE_COLS, nc.scalar.copy)
             multiply_h(i, 2)
-            scale_late(i + 2)
-            product_t1(t1_halves.pop(0), turns_t2(i + 4) + turns_plain(i + 3))
-            widen_shared(i + 5, 0, SCALAR_WIDENS // 2, nc.scalar.copy)
             multiply_h(i, 3)
+            if i + KEPT <= LAST:
+                load_t2(i + KEPT)
+                load_x1(i + KEPT)
+            if second and busy:
+                scale_late(b, 7, 1)
 
         product_t3(LAST, 1)
         product_t3(LAST, 2)
-        product_t3(LAST, 3, block_bank)
+        product_t3(LAST, 3, late_bank)
         product_out(LAST - 2, 1)
         multiply_h(LAST, 0)
         quantise_h(LAST - 1)
@@ -368,12 +420,12 @@ def tile_cptensorproduct_pa_t_w4_kernel(tc, x1, A, t2, w_bytes, w_scale, C_words
             product_out(LAST - 1, m)
         multiply_h(LAST, 1)
         multiply_h(LAST, 2)
-        quantise_h(LAST, 0, WIDE)
+        quantise_h(LAST, 0, 2 * P)
         for m in range(2):
-            product_out(LAST, m, 0, WIDE)
+            product_out(LAST, m, 0, 2 * P)
         multiply_h(LAST, 3)
-        for first in (WIDE, WIDE + P):
+        for first in (2 * P, 3 * P):
             quantise_h(LAST, first, P)
-        for first in (WIDE, WIDE + P):
+        for first in (2 * P, 3 * P):
             product_out(LAST, 0, first, P)
             product_out(LAST, 1, first, P, t3_bank, nc.vector.tensor_copy)

@@ -27,10 +27,10 @@ WORDS = CV // 2
 SAMPLE_COLS = 2 * BLOCKS * CV
 SHARED_FIRST, SHARED_COUNT = 2, 3
 
-GPSIMD_WIDENS = 2816
-FIRST_WIDENS = 1792
+GPSIMD_WIDENS = 2176
+FIRST_WIDENS = 1536
 T1_LEAD = 3
-SKIPS = (2, 10)
+SKIPS = (2,)
 EXTRA = (12,)
 GAPS = 3
 HANDED_ON = 3
@@ -122,9 +122,9 @@ def tile_cptensorproduct_pa_t_w4_kernel(tc, x1, A, t2, w_bytes, w_scale, C_words
                 w_grouped[i] = work.tile([P, PACK * UNIT], BF16, name="w_by_column", align_bytes=64)
             return w_grouped[i][:, PACK * P * first : PACK * P * (first + count)]
 
-        def turns(sources, take_bank, finish):
+        def turns(sources, take_bank, finish, early=False):
             blocks = len(sources[0])
-            taken = []
+            taken = [take_bank([P, 2, blocks * P])] if early else []
 
             def turn(u, j):
                 if not taken:
@@ -159,7 +159,7 @@ def tile_cptensorproduct_pa_t_w4_kernel(tc, x1, A, t2, w_bytes, w_scale, C_words
 
         def turns_shared(b, j, count, first=SHARED_FIRST, take_bank=ring_bank):
             sources = pairs_sorted(w_shared[b, first], SHARED_COUNT, j - first, count)
-            return turns(sources, take_bank, lambda bank: copy_turned(w_columns(b, j, count), bank))
+            return turns(sources, take_bank, lambda bank: copy_turned(w_columns(b, j, count), bank), count == 1 and j == 4)
 
         def turns_late(b, j, count, sources=None, take_bank=late_bank, at_once=False):
             def finish(bank):
@@ -349,10 +349,8 @@ def tile_cptensorproduct_pa_t_w4_kernel(tc, x1, A, t2, w_bytes, w_scale, C_words
                 quantise_w(i + 1)
             if second == 0 and b + 1 < NB:
                 w_wide[b + 1] = handed_on(i + 2, SAMPLE_COLS)
-                if i == 0:
-                    widen(b + 1, 5 * CV - FIRST_WIDENS, 5 * CV, nc.gpsimd.tensor_copy)
-                else:
-                    widen(b + 1, 0, GPSIMD_WIDENS, nc.gpsimd.tensor_copy)
+                share = FIRST_WIDENS if i == 0 else GPSIMD_WIDENS
+                widen(b + 1, ROWS2, ROWS2 + share, nc.gpsimd.tensor_copy)
             elif second == 1 and b + 1 < NB:
                 scale_shared(b + 1, SHARED_FIRST, i + 2)
             elif i + 3 == LAST:
@@ -365,6 +363,10 @@ def tile_cptensorproduct_pa_t_w4_kernel(tc, x1, A, t2, w_bytes, w_scale, C_words
                 product_t3(i, 3, late_bank)
             if i > 1:
                 product_out(i - 2, 1)
+            if second == 0:
+                rest = (ROWS2 + share + SAMPLE_COLS) // 2
+                pieces = [(0, CV), (CV, ROWS2), (ROWS2 + share, rest), (rest, SAMPLE_COLS)]
+            widen(b + 1, *pieces.pop(0), nc.scalar.copy)
             early, pair = ((4, 1), 5) if second else ((2, 2), 0)
             if i == 0:
                 steps = turns_plain(1, 2, 2) + turns_t2(3)
@@ -386,22 +388,13 @@ def tile_cptensorproduct_pa_t_w4_kernel(tc, x1, A, t2, w_bytes, w_scale, C_words
             product_t3(i + 1, 0)
             if i > 0:
                 product_out(i - 1, 0)
+            widen(b + 1, *pieces.pop(0), nc.scalar.copy)
             if i > 0 and busy:
                 scale_late(b, pair, 2)
             steps = turns_t2(i + 4)
             if second and busy:
                 steps = steps[:2] + turns_late(b, 7, 1) + steps[2:]
             product_t1([t1_slots.pop(0) for n in range(1 if i in SKIPS else 3 if i in EXTRA else 2)], steps)
-            if i == 0:
-                widen(2, 0, 5 * CV - FIRST_WIDENS, nc.scalar.copy)
-            elif i == 1:
-                widen(2, 5 * CV, 7 * CV, nc.scalar.copy)
-            elif second == 0:
-                if i == 2:
-                    widen(2, 7 * CV, SAMPLE_COLS, nc.scalar.copy)
-                widen(b + 1, GPSIMD_WIDENS, SAMPLE_COLS if b + 2 == NB else 7 * CV, nc.scalar.copy)
-            elif b + 2 < NB:
-                widen(b + 1, 7 * CV, SAMPLE_COLS, nc.scalar.copy)
             multiply_h(i, 2)
             multiply_h(i, 3)
             if i + KEPT <= LAST:

@@ -30,8 +30,8 @@ SHARED_FIRST, SHARED_COUNT = 2, 3
 GPSIMD_WIDENS = 2176
 FIRST_WIDENS = 1536
 T1_LEAD = 3
-SKIPS = (2,)
-EXTRA = (12,)
+SKIPS = ()
+EXTRA = ()
 GAPS = 3
 HANDED_ON = 3
 T3_BANKS = 3
@@ -159,7 +159,7 @@ def tile_cptensorproduct_pa_t_w4_kernel(tc, x1, A, t2, w_bytes, w_scale, C_words
 
         def turns_shared(b, j, count, first=SHARED_FIRST, take_bank=ring_bank):
             sources = pairs_sorted(w_shared[b, first], SHARED_COUNT, j - first, count)
-            return turns(sources, take_bank, lambda bank: copy_turned(w_columns(b, j, count), bank), count == 1 and j == 4)
+            return turns(sources, take_bank, lambda bank: copy_turned(w_columns(b, j, count), bank))
 
         def turns_late(b, j, count, sources=None, take_bank=late_bank, at_once=False):
             def finish(bank):

@@ -27,7 +27,7 @@ WORDS = CV // 2
 SAMPLE_COLS = 2 * BLOCKS * CV
 SHARED_FIRST, SHARED_COUNT = 2, 3
 
-GPSIMD_WIDENS = 2176
+GPSIMD_WIDENS = 2560
 FIRST_WIDENS = 1536
 T1_LEAD = 3
 SKIPS = ()

@@ -28,14 +28,17 @@ SAMPLE_COLS = 2 * BLOCKS * CV
 SHARED_FIRST, SHARED_COUNT = 2, 3
 
 GPSIMD_WIDENS = 2560
-FIRST_WIDENS = 1536
+SHORT_WIDENS = 1536
+PIECE = 512
+AFTER_PRODUCT = 256
+FOUR_SHARED = (4, 6)
 T1_LEAD = 3
-SKIPS = ()
-EXTRA = ()
+SKIPS = (8, 13)
+EXTRA = (12,)
 GAPS = 3
 HANDED_ON = 3
 T3_BANKS = 3
-RING = 4
+RING = 5
 RESULTS = 10
 KEPT = 12
 
@@ -50,7 +53,7 @@ def tile_cptensorproduct_pa_t_w4_kernel(tc, x1, A, t2, w_bytes, w_scale, C_words
         ctx.enter_context(tc.manual_schedule())
 
         x1_raw, t2_raw, w_raw = {}, {}, {}
-        w_wide, w_shared, w_plain, late_banks = {}, {}, {}, {}
+        w_wide, w_shared, w_plain, late_banks, w_sorted, w_front = {}, {}, {}, {}, {}, {}
         w_grouped, w_codes, w_scales = {}, {}, {}
         t2_grouped, t2_codes, t2_scales = {}, {}, {}
         t1_sb, t3_banks = {}, {}
@@ -63,9 +66,6 @@ def tile_cptensorproduct_pa_t_w4_kernel(tc, x1, A, t2, w_bytes, w_scale, C_words
 
         def t3_bank(shape):
             return psum.tile(shape, F32, name="t3_bank", bufs=T3_BANKS)
-
-        def late_bank(shape):
-            return psum.tile(shape, F32, name="late_bank")
 
         def handed_on(n, columns):
             return work.tile([P, columns], BF16, name="handed_on%d" % (n % (2 * HANDED_ON)), bufs=1, align_bytes=64)
@@ -91,13 +91,24 @@ def tile_cptensorproduct_pa_t_w4_kernel(tc, x1, A, t2, w_bytes, w_scale, C_words
             nc.sync.dma_start(out=x1_raw[i][:], in_=rows[:, :, half * UNIT : (half + 1) * UNIT])
 
         def scale_plain(b, j, count):
-            w_plain[b, j] = work.tile([P, count * CV], BF16, name="w_plain", align_bytes=64)
-            values = w_raw[b][:, j * CV : (j + count) * CV].bitcast(FP8)
-            nc.vector.tensor_tensor(out=w_plain[b, j][:], in0=values, in1=scale_rows[:, : count * CV], op=MULT)
+            w_plain[b, j] = work.tile([P, count * CV], BF16, name="w_plain", bufs=4, align_bytes=64)
+            for n in range(count):
+                values = w_raw[b][:, (j + n) * CV : (j + n + 1) * CV].bitcast(FP8)
+                nc.vector.tensor_tensor(out=w_plain[b, j][:, n * CV : (n + 1) * CV], in0=values, in1=scale_rows[:], op=MULT)
+
+        def widen_sorted(b, j):
+            w_sorted[b, j] = work.tile([P, ROWS2], BF16, name="w_sorted", align_bytes=64)
+            target = w_sorted[b, j][:].rearrange("p (u q e) -> p q u e", u=2, e=2)
+            values = w_raw[b][:, j * CV : (j + 2) * CV].bitcast(FP8).rearrange("p (q u e) -> p q u e", u=2, e=2)
+            nc.vector.tensor_scalar(out=target, in0=values, scalar1=ones[:], scalar2=None, op0=MULT)
 
         def widen(b, first, last, copy):
             if b < NB:
-                copy(out=w_wide[b][:, first:last], in_=w_raw[b][:, first:last].bitcast(FP8))
+                j = first // ROWS2 * 2
+                if (j == 0 or b == 1) and (b, j) not in w_front:
+                    w_front[b, j] = work.tile([P, ROWS2], BF16, name="w_front", align_bytes=64)
+                tile, offset = (w_front[b, j], j * CV) if (b, j) in w_front else (w_wide[b], ROWS2)
+                copy(out=tile[:, first - offset : last - offset], in_=w_raw[b][:, first:last].bitcast(FP8))
 
         def scale_late(b, j, count):
             values = late_banks[b, j][:].rearrange("p u r -> p (u r)").bitcast(BF16)
@@ -106,14 +117,25 @@ def tile_cptensorproduct_pa_t_w4_kernel(tc, x1, A, t2, w_bytes, w_scale, C_words
             target = w_columns(b, j, count).rearrange("p (r u e) -> p r u e", u=2, e=2)
             nc.vector.tensor_tensor(out=target, in0=values, in1=factors, op=MULT)
 
-        def scale_shared(b, first, n):
-            w_shared[b, first] = handed_on(n, SHARED_COUNT * CV)
-            target = w_shared[b, first][:].rearrange("p (u j q e) -> p u j q e", u=2, j=SHARED_COUNT, e=2)
-            values = w_wide[b][:, first * CV : (first + SHARED_COUNT) * CV]
-            values = values.rearrange("p (j q u e) -> p u j q e", j=SHARED_COUNT, u=2, e=2)
+        def scale_shared(b, first, count, tile, offset=0):
+            columns = tile[:, offset : offset + count * CV]
+            words = columns.bitcast(F32)
+            for j in range(count):
+                w_shared[b, first + j] = [words[:, (u * count + j) * P : (u * count + j + 1) * P] for u in range(2)]
+            target = columns.rearrange("p (u j q e) -> p u j q e", u=2, j=count, e=2)
+            values = w_wide[b][:, (first - 2) * CV : (first - 2 + count) * CV]
+            values = values.rearrange("p (j q u e) -> p u j q e", j=count, u=2, e=2)
             factors = scale_sorted[:].rearrange("p (u q e) -> p u q e", u=2, e=2)
-            factors = factors.unsqueeze(2).to_broadcast([P, 2, SHARED_COUNT, P, 2])
+            factors = factors.unsqueeze(2).to_broadcast([P, 2, count, P, 2])
             nc.gpsimd.tensor_tensor(out=target, in0=values, in1=factors, op=MULT)
+
+        def widen_piece():
+            if waiting:
+                b, first, last = waiting.pop(0)
+                end = min(last, first + PIECE)
+                widen(b, first, end, nc.scalar.copy)
+                if end < last:
+                    waiting.insert(0, (b, end, last))
 
         def w_columns(b, j, count):
             half, first = divmod(j, BLOCKS)
@@ -157,17 +179,18 @@ def tile_cptensorproduct_pa_t_w4_kernel(tc, x1, A, t2, w_bytes, w_scale, C_words
         def turns_plain(b, j, count, take_bank=ring_bank):
             return turns(pairs_unsorted(w_plain[b, j], 0, count), take_bank, lambda bank: copy_turned(w_columns(b, j, count), bank))
 
-        def turns_shared(b, j, count, first=SHARED_FIRST, take_bank=ring_bank):
-            sources = pairs_sorted(w_shared[b, first], SHARED_COUNT, j - first, count)
+        def turns_shared(b, j, count, take_bank=ring_bank):
+            sources = [[w_shared[b, n][u] for n in range(j, j + count)] for u in range(2)]
             return turns(sources, take_bank, lambda bank: copy_turned(w_columns(b, j, count), bank))
 
-        def turns_late(b, j, count, sources=None, take_bank=late_bank, at_once=False):
+        def turns_late(b, j, count, take_bank=t3_bank, at_once=False):
             def finish(bank):
                 late_banks[b, j] = bank
                 if at_once:
                     scale_late(b, j, count)
 
-            return turns(sources or pairs_unsorted(w_wide[b], j, count), take_bank, finish)
+            sources = pairs_sorted(w_sorted[b, j], 2, 0, 2) if (b, j) in w_sorted else pairs_unsorted(w_front[b, j], 0, count) if (b, j) in w_front else pairs_unsorted(w_wide[b], j - 2, count)
+            return turns(sources, take_bank, finish)
 
         def quantise_w(i):
             w_codes[i] = work.tile([P, UNIT], U32, name="w_code", bufs=3, align_bytes=64)
@@ -278,6 +301,7 @@ def tile_cptensorproduct_pa_t_w4_kernel(tc, x1, A, t2, w_bytes, w_scale, C_words
         load_t2(2)
         load_w(3)
         load_w(4)
+        load_w(5)
         load_t2(3)
         c_words = const.tile([P, 2 * D], U8, align_bytes=64)
         nc.sync.dma_start(out=c_words[:], in_=C_words[0])
@@ -287,126 +311,131 @@ def tile_cptensorproduct_pa_t_w4_kernel(tc, x1, A, t2, w_bytes, w_scale, C_words
         for i in range(2, UNITS):
             if i < KEPT:
                 load_x1(i)
-            if i + 3 <= LAST:
-                load_w(i + 3)
+            if i + 4 <= LAST:
+                load_w(i + 4)
             if i + 2 < KEPT:
                 load_t2(i + 2)
 
         row_bank = ring_bank([P, PACK, P])
         for t in range(PACK):
             nc.tensor.transpose(row_bank[:, t, :], scale_cols[:, t : t + 1].to_broadcast([P, P]), ident[:])
-        scale_rows = const.tile([P, ROWS2], F32)
-        for half in range(2):
-            target = scale_rows[:, half * CV : (half + 1) * CV].rearrange("p (q t) -> p q t", t=PACK)
-            nc.scalar.copy(out=target, in_=row_bank[:].rearrange("p t q -> p q t"))
+        scale_rows = const.tile([P, CV], F32)
+        nc.scalar.copy(out=scale_rows[:].rearrange("p (q t) -> p q t", t=PACK), in_=row_bank[:].rearrange("p t q -> p q t"))
         a_perm = const.tile([P, 2, PACK, P], BF16)
         nc.scalar.copy(out=a_perm[:], in_=a_raw[:].rearrange("p k (m t) -> p k t m", t=PACK))
 
-        w_first = const.tile([P, ROWS2], BF16, align_bytes=64)
-        for j in range(2):
-            target = w_first[:].rearrange("p (u j q e) -> p j q u e", u=2, j=2, e=2)[:, j]
-            values = w_raw[0][:, j * CV : (j + 1) * CV].bitcast(FP8).rearrange("p (q u e) -> p q u e", u=2, e=2)
-            nc.vector.tensor_scalar(out=target, in0=values, scalar1=ones[:], scalar2=None, op0=MULT)
-        for step in turns_late(0, 0, 2, pairs_sorted(w_first, 2, 0, 2)):
-            step()
-        scale_plain(0, 2, 1)
-        scale_plain(0, 3, 1)
-        scale_late(0, 0, 2)
-        scale_plain(0, 4, 2)
-        product_t1([0], [])
+        widen_sorted(0, 0)
         scale_sorted = const.tile([P, CV], F32)
         target = scale_sorted[:].rearrange("p (u q e) -> p u q e", u=2, e=2)
-        nc.scalar.copy(out=target, in_=scale_rows[:, :CV].rearrange("p (q u e) -> p u q e", u=2, e=2))
-        product_t1([1], [])
-        product_t1([2], turns_plain(0, 2, 1, t3_bank) + turns_plain(0, 3, 1, t3_bank) + turns_t2(0, t3_bank))
+        nc.scalar.copy(out=target, in_=row_bank[:].rearrange("p (u e) q -> p u q e", u=2))
+        scale_plain(0, 2, 2)
+        product_t1([0], turns_late(0, 0, 2))
+        scale_late(0, 0, 2)
+        scale_plain(0, 4, 2)
+        product_t1([1], turns_plain(0, 2, 2, t3_bank))
         scale_plain(0, 6, 2)
-        product_t1([3], turns_t2(1, late_bank))
+        product_t1([2, 3], turns_t2(0, t3_bank) + turns_t2(1) + turns_plain(0, 4, 2, t3_bank))
+        scale_plain(1, 0, 2)
         quantise_t2(0)
         quantise_w(0)
-        scale_plain(1, 0, 2)
         quantise_t2(1)
-        product_t1([4, 5], turns_plain(0, 4, 2, t3_bank) + turns_plain(0, 6, 2, t3_bank) + turns_t2(2, late_bank))
+        product_t1([4, 5], turns_plain(0, 6, 2, t3_bank) + turns_t2(2))
         product_t1([6], turns_plain(1, 0, 2))
-        scale_plain(1, 2, 2)
-        w_wide[1] = handed_on(0, SAMPLE_COLS)
-        widen(1, 5 * CV, SAMPLE_COLS, nc.vector.tensor_copy)
+        widen_sorted(1, 2)
+        scale_plain(1, 4, 2)
         product_t3(0, 0)
+        product_t3(0, 1)
 
         t1_slots = list(range(7, PACK * (UNITS + 2)))
+        waiting = [(1, 6 * CV, SAMPLE_COLS), (2, 0, ROWS2)]
+        w_last = True
         for i in range(LAST):
             b, second = divmod(i + 2, 2)
-            busy = i + 2 < LAST
-            if i == 1:
-                scale_plain(1, 4, 1)
-            if second or i + 1 == LAST:
-                quantise_w(i + 1)
-                quantise_t2(i + 2)
-                quantise_h(i - 1)
-            else:
+            busy = i < LAST - 2
+            four = b in FOUR_SHARED
+            if i + 1 == LAST:
+                multiply_h(i, 0)
+            if w_last:
                 if i > 0:
                     quantise_h(i - 1)
                 quantise_t2(i + 2)
                 quantise_w(i + 1)
+            else:
+                quantise_w(i + 1)
+                quantise_t2(i + 2)
+                quantise_h(i - 1)
             if second == 0 and b + 1 < NB:
-                w_wide[b + 1] = handed_on(i + 2, SAMPLE_COLS)
-                share = FIRST_WIDENS if i == 0 else GPSIMD_WIDENS
+                w_wide[b + 1] = handed_on(i + 2, 7 * CV)
+                extra = 5 if four else None
+                if extra:
+                    scale_shared(b, extra, 1, w_wide[b + 1], 6 * CV)
+                share = SHORT_WIDENS if extra else GPSIMD_WIDENS
                 widen(b + 1, ROWS2, ROWS2 + share, nc.gpsimd.tensor_copy)
+                after = 0 if i == 0 or four else AFTER_PRODUCT
+                waiting.append((b + 1, ROWS2 + share + after, SAMPLE_COLS))
+                if b + 2 < NB:
+                    waiting.append((b + 2, 0, ROWS2))
             elif second == 1 and b + 1 < NB:
-                scale_shared(b + 1, SHARED_FIRST, i + 2)
+                count = 3
+                scale_shared(b + 1, 2, count, handed_on(i + 2, 3 * CV))
+                if after:
+                    widen(b + 1, ROWS2 + share, ROWS2 + share + after, nc.gpsimd.tensor_copy)
             elif i + 3 == LAST:
-                scale_shared(b, 5, i + 2)
+                scale_shared(b, 5, 3, handed_on(i + 2, 3 * CV))
 
-            product_t3(i, 1)
-            product_t3(i, 2)
-            spare = i + 2 > LAST
-            if spare:
-                product_t3(i, 3, late_bank)
-            if i > 1:
-                product_out(i - 2, 1)
-            if second == 0:
-                rest = (ROWS2 + share + SAMPLE_COLS) // 2
-                pieces = [(0, CV), (CV, ROWS2), (ROWS2 + share, rest), (rest, SAMPLE_COLS)]
-            widen(b + 1, *pieces.pop(0), nc.scalar.copy)
-            early, pair = ((4, 1), 5) if second else ((2, 2), 0)
+            pair = (6 if four or i == 1 else 5) if second else 2 if i == 0 else 0
+            single = busy and second and pair == 5
             if i == 0:
-                steps = turns_plain(1, 2, 2) + turns_t2(3)
+                steps = turns_late(b, pair, 2) + turns_t2(3)
             elif i == 1:
-                steps = turns_plain(b, *early) + turns_late(b, pair, 2)
+                steps = turns_late(b, pair, 2)
             elif busy and second:
-                steps = turns_shared(b, *early) + turns_late(b, pair, 2)
+                steps = turns_shared(b, 4, 2 if four else 1) + turns_late(b, pair, 2)
             elif busy:
-                steps = turns_late(b, pair, 2) + turns_shared(b, *early)
+                steps = turns_late(b, pair, 2) + turns_shared(b, 2, 2)
             elif i + 2 == LAST:
-                steps = turns_shared(b, 4, 1) + turns_shared(b, 5, 2, 5, late_bank) + turns_shared(b, 7, 1, 5)
+                steps = turns_shared(b, 4, 2) + turns_shared(b, 6, 2)
             else:
                 steps = []
             product_t1([t1_slots.pop(0) for n in range(2)], steps)
-            multiply_h(i, 0)
-            if not spare:
-                product_t3(i, 3)
+            made = [(i, 2), (i, 3), (i + 1, 0), (i + 1, 1)] if busy else [(i, 3), (i + 1, 0), (i + 1, 1)]
+            if i + 1 >= LAST - 2:
+                made.append((i + 1, 2))
+            if i + 1 < LAST:
+                multiply_h(i, 0)
+            product_t3(*made.pop(0))
             multiply_h(i, 1)
-            product_t3(i + 1, 0)
+            product_t3(*made.pop(0))
             if i > 0:
                 product_out(i - 1, 0)
-            widen(b + 1, *pieces.pop(0), nc.scalar.copy)
-            if i > 0 and busy:
+            widen_piece()
+            if i == 0:
+                widen_piece()
+                widen_piece()
+            if busy:
                 scale_late(b, pair, 2)
             steps = turns_t2(i + 4)
-            if second and busy:
+            if i == 0:
+                steps = turns_plain(1, 4, 2) + steps
+            if single:
                 steps = steps[:2] + turns_late(b, 7, 1) + steps[2:]
             product_t1([t1_slots.pop(0) for n in range(1 if i in SKIPS else 3 if i in EXTRA else 2)], steps)
             multiply_h(i, 2)
+            product_t3(*made.pop(0))
             multiply_h(i, 3)
+            for block in made:
+                product_t3(*block)
+            if i > 0:
+                product_out(i - 1, 1)
+            widen_piece()
             if i + KEPT <= LAST:
                 load_t2(i + KEPT)
                 load_x1(i + KEPT)
-            if second and busy:
+            if single:
                 scale_late(b, 7, 1)
+            w_last = single or i + 2 == LAST
 
-        product_t3(LAST, 1)
-        product_t3(LAST, 2)
-        product_t3(LAST, 3, late_bank)
-        product_out(LAST - 2, 1)
+        product_t3(LAST, 3, ring_bank)
         multiply_h(LAST, 0)
         quantise_h(LAST - 1)
         for m in range(2):

from contextlib import ExitStack

import concourse.mybir as mybir
from concourse.masks import make_identity

NB, D, CO, CV, R = 8, 256, 1024, 512, 512
FLOPS = 2 * NB * (R * D * CO + R * CV * CO + D * R * CO)

F32 = mybir.dt.float32
BF16 = mybir.dt.bfloat16
I32 = mybir.dt.int32
U32 = mybir.dt.uint32
U8 = mybir.dt.uint8
FP8 = mybir.dt.float8_e4m3fn
FP8X4 = mybir.dt.float8_e4m3fn_x4
FP4X4 = mybir.dt.float4_e2m1fn_x4
MULT = mybir.AluOpType.mult

P = 128
PACK = 4
UNIT = 512
BLOCKS = UNIT // P
UNITS = NB * CO // UNIT
LAST = UNITS - 1
ROWS2 = 2 * CV
WORDS = CV // 2
SAMPLE_COLS = 2 * BLOCKS * CV
SHARED_FIRST, SHARED_COUNT = 2, 3

GPSIMD_WIDENS = 2560
SHORT_WIDENS = 1536
PIECE = 512
AFTER_PRODUCT = 256
FOUR_SHARED = (4, 6)
T1_LEAD = 3
SKIPS = (8, 13)
EXTRA = (12,)
GAPS = 3
HANDED_ON = 3
T3_BANKS = 3
RING = 5
RESULTS = 10
KEPT = 12


def tile_cptensorproduct_pa_t_w4_kernel(tc, x1, A, t2, w_bytes, w_scale, C_words, C_scales, out):
    nc = tc.nc
    with ExitStack() as ctx:
        const = ctx.enter_context(tc.tile_pool(name="const", bufs=1))
        loads = ctx.enter_context(tc.tile_pool(name="loads", bufs=UNITS))
        work = ctx.enter_context(tc.tile_pool(name="work", bufs=3))
        psum = ctx.enter_context(tc.psum_pool(name="psum", bufs=1))
        ctx.enter_context(tc.manual_schedule())

        x1_raw, t2_raw, w_raw = {}, {}, {}
        w_wide, w_shared, w_plain, late_banks, w_sorted, w_front = {}, {}, {}, {}, {}, {}
        w_grouped, w_codes, w_scales = {}, {}, {}
        t2_grouped, t2_codes, t2_scales = {}, {}, {}
        t1_sb, t3_banks = {}, {}
        h_grouped, h_codes, h_scales = {}, {}, {}
        ring_taken = []

        def ring_bank(shape):
            ring_taken.append(shape)
            return psum.tile(shape, F32, name="ring%d" % (len(ring_taken) % RING))

        def t3_bank(shape):
            return psum.tile(shape, F32, name="t3_bank", bufs=T3_BANKS)

        def handed_on(n, columns):
            return work.tile([P, columns], BF16, name="handed_on%d" % (n % (2 * HANDED_ON)), bufs=1, align_bytes=64)

        def load_w(i, first=0, last=BLOCKS):
            b, half = divmod(i, 2)
            if b not in w_raw:
                w_raw[b] = loads.tile([P, SAMPLE_COLS], U8, name="w_raw_bytes", bufs=NB)
            j0, j1 = BLOCKS * half + first, BLOCKS * half + last
            rows = w_bytes[b, j0 * P : j1 * P, :].rearrange("(j p) c -> p j c", p=P)
            nc.sync.dma_start(out=w_raw[b][:, j0 * CV : j1 * CV].rearrange("p (j c) -> p j c", c=CV), in_=rows)

        def load_t2(n):
            b, half = divmod(n, 2)
            t2_raw[n] = loads.tile([P, ROWS2], BF16, name="t2_rows", bufs=KEPT)
            rows = t2[b].rearrange("(m t) c -> m (t c)", t=PACK)
            nc.sync.dma_start(out=t2_raw[n][:], in_=rows[:, half * ROWS2 : (half + 1) * ROWS2])

        def load_x1(i):
            b, half = divmod(i, 2)
            x1_raw[i] = loads.tile([P, 2, UNIT], BF16, name="x1_rows", bufs=KEPT)
            rows = x1[b].rearrange("(p k) o -> p k o", k=2)
            nc.sync.dma_start(out=x1_raw[i][:], in_=rows[:, :, half * UNIT : (half + 1) * UNIT])

        def scale_plain(b, j, count):
            w_plain[b, j] = work.tile([P, count * CV], BF16, name="w_plain", bufs=4, align_bytes=64)
            for n in range(count):
                values = w_raw[b][:, (j + n) * CV : (j + n + 1) * CV].bitcast(FP8)
                nc.vector.tensor_tensor(out=w_plain[b, j][:, n * CV : (n + 1) * CV], in0=values, in1=scale_rows[:], op=MULT)

        def widen_sorted(b, j):
            w_sorted[b, j] = work.tile([P, ROWS2], BF16, name="w_sorted", align_bytes=64)
            target = w_sorted[b, j][:].rearrange("p (u q e) -> p q u e", u=2, e=2)
            values = w_raw[b][:, j * CV : (j + 2) * CV].bitcast(FP8).rearrange("p (q u e) -> p q u e", u=2, e=2)
            nc.vector.tensor_scalar(out=target, in0=values, scalar1=ones[:], scalar2=None, op0=MULT)

        def widen(b, first, last, copy):
            if b < NB:
                j = first // ROWS2 * 2
                if (j == 0 or b == 1) and (b, j) not in w_front:
                    w_front[b, j] = work.tile([P, ROWS2], BF16, name="w_front", align_bytes=64)
                tile, offset = (w_front[b, j], j * CV) if (b, j) in w_front else (w_wide[b], ROWS2)
                copy(out=tile[:, first - offset : last - offset], in_=w_raw[b][:, first:last].bitcast(FP8))

        def scale_late(b, j, count):
            values = late_banks[b, j][:].rearrange("p u r -> p (u r)").bitcast(BF16)
            values = values.rearrange("p (u r e) -> p r u e", u=2, e=2)
            factors = scale_cols[:].rearrange("p (u e) -> p u e", u=2).unsqueeze(1).to_broadcast([P, count * P, 2, 2])
            target = w_columns(b, j, count).rearrange("p (r u e) -> p r u e", u=2, e=2)
            nc.vector.tensor_tensor(out=target, in0=values, in1=factors, op=MULT)

        def scale_shared(b, first, count, tile, offset=0):
            columns = tile[:, offset : offset + count * CV]
            words = columns.bitcast(F32)
            for j in range(count):
                w_shared[b, first + j] = [words[:, (u * count + j) * P : (u * count + j + 1) * P] for u in range(2)]
            target = columns.rearrange("p (u j q e) -> p u j q e", u=2, j=count, e=2)
            values = w_wide[b][:, (first - 2) * CV : (first - 2 + count) * CV]
            values = values.rearrange("p (j q u e) -> p u j q e", j=count, u=2, e=2)
            factors = scale_sorted[:].rearrange("p (u q e) -> p u q e", u=2, e=2)
            factors = factors.unsqueeze(2).to_broadcast([P, 2, count, P, 2])
            nc.gpsimd.tensor_tensor(out=target, in0=values, in1=factors, op=MULT)

        def widen_piece():
            if waiting:
                b, first, last = waiting.pop(0)
                end = min(last, first + PIECE)
                widen(b, first, end, nc.scalar.copy)
                if end < last:
                    waiting.insert(0, (b, end, last))

        def w_columns(b, j, count):
            half, first = divmod(j, BLOCKS)
            i = 2 * b + half
            if i not in w_grouped:
                w_grouped[i] = work.tile([P, PACK * UNIT], BF16, name="w_by_column", align_bytes=64)
            return w_grouped[i][:, PACK * P * first : PACK * P * (first + count)]

        def turns(sources, take_bank, finish, early=False):
            blocks = len(sources[0])
            taken = [take_bank([P, 2, blocks * P])] if early else []

            def turn(u, j):
                if not taken:
                    taken.append(take_bank([P, 2, blocks * P]))
                nc.tensor.transpose(taken[0][:, u, j * P : (j + 1) * P], sources[u][j], ident[:])
                if (u, j) == (1, blocks - 1):
                    finish(taken[0])

            return [lambda u=u, j=j: turn(u, j) for u in range(2) for j in range(blocks)]

        def pairs_unsorted(tile, first, count):
            words = tile[:].bitcast(F32)
            return [[words[:, j * WORDS + u : (j + 1) * WORDS : 2] for j in range(first, first + count)] for u in range(2)]

        def pairs_sorted(tile, blocks, first, count):
            words = tile[:].bitcast(F32)
            return [[words[:, (u * blocks + j) * P : (u * blocks + j + 1) * P] for j in range(first, first + count)] for u in range(2)]

        def copy_turned(target, bank):
            words = target.bitcast(F32).rearrange("p (r u) -> p r u", u=2)
            nc.scalar.copy(out=words, in_=bank[:].rearrange("p u r -> p r u"))

        def turns_t2(n, take_bank=ring_bank):
            def finish(bank):
                t2_grouped[n] = handed_on(n, ROWS2)
                copy_turned(t2_grouped[n][:], bank)

            return turns(pairs_unsorted(t2_raw[n], 0, 2), take_bank, finish) if n <= LAST else []

        def turns_plain(b, j, count, take_bank=ring_bank):
            return turns(pairs_unsorted(w_plain[b, j], 0, count), take_bank, lambda bank: copy_turned(w_columns(b, j, count), bank))

        def turns_shared(b, j, count, take_bank=ring_bank):
            sources = [[w_shared[b, n][u] for n in range(j, j + count)] for u in range(2)]
            return turns(sources, take_bank, lambda bank: copy_turned(w_columns(b, j, count), bank))

        def turns_late(b, j, count, take_bank=t3_bank, at_once=False):
            def finish(bank):
                late_banks[b, j] = bank
                if at_once:
                    scale_late(b, j, count)

            sources = pairs_sorted(w_sorted[b, j], 2, 0, 2) if (b, j) in w_sorted else pairs_unsorted(w_front[b, j], 0, count) if (b, j) in w_front else pairs_unsorted(w_wide[b], j - 2, count)
            return turns(sources, take_bank, finish)

        def quantise_w(i):
            w_codes[i] = work.tile([P, UNIT], U32, name="w_code", bufs=3, align_bytes=64)
            w_scales[i] = work.tile([P, UNIT], U8, name="w_code_scale", bufs=3, align_bytes=64)
            nc.vector.quantize_mx(out=w_codes[i][:].bitcast(FP8X4), scales=w_scales[i][:], in_=w_grouped[i][:])

        def quantise_t2(n):
            if n <= LAST:
                b, half = divmod(n, 2)
                if half == 0:
                    t2_codes[b] = work.tile([P, R], U32, name="t2_code", bufs=2, align_bytes=64)
                    t2_scales[b] = work.tile([P, R], U8, name="t2_code_scale", bufs=2, align_bytes=64)
                m = slice(R // 2 * half, R // 2 * (half + 1))
                nc.vector.quantize_mx(out=t2_codes[b][:, m].bitcast(FP8X4), scales=t2_scales[b][:, m], in_=t2_grouped[n][:])

        def quantise_h(i, first=0, count=UNIT):
            if first == 0:
                h_codes[i] = work.tile([P, UNIT], U32, name="h_code", bufs=3, align_bytes=64)
                h_scales[i] = work.tile([P, UNIT], U8, name="h_code_scale", bufs=3, align_bytes=64)
            n = slice(first, first + count)
            columns = h_grouped[i][:, PACK * first : PACK * (first + count)]
            nc.vector.quantize_mx(out=h_codes[i][:, n].bitcast(FP8X4), scales=h_scales[i][:, n], in_=columns)

        def a_columns(n, k):
            t = n % PACK
            return a_raw[:, k, t:R:PACK] if n < 2 else a_perm[:, k, t, :]

        def product_t1(slots, steps):
            slots = [n for n in slots if n < PACK * UNITS]
            gaps = max(2 * len(slots) - 1, 1)
            done = 0
            for place, n in enumerate(slots):
                i, t = divmod(n, PACK)
                if t == 0:
                    t1_sb[i] = work.tile([P, PACK, UNIT], F32, name="t1_copy", bufs=4)
                bank = ring_bank([P, UNIT])
                for k in range(2):
                    nc.tensor.matmul(bank[:], lhsT=a_columns(n, k), rhs=x1_raw[i][:, k, :], start=(k == 0), stop=(k == 1))
                    if k == 1:
                        nc.scalar.copy(out=t1_sb[i][:, t, :], in_=bank[:])
                    until = min(len(steps), -(-len(steps) * (2 * place + k + 1) // gaps))
                    for step in steps[done:until]:
                        step()
                    done = until
            for step in steps[done:]:
                step()

        def product_t3(i, j, take_bank=t3_bank):
            b = i // 2
            t3_banks[i, j] = take_bank([P, PACK, P])
            n = slice(P * j, P * (j + 1))
            for t in range(PACK):
                m = slice(P * t, P * (t + 1))
                nc.tensor.matmul_mx(
                    out=t3_banks[i, j][:, t, :],
                    lhsT=t2_codes[b][:, m].bitcast(FP8X4),
                    lhsT_scale=t2_scales[b][:, m],
                    rhs=w_codes[i][:, n].bitcast(FP8X4),
                    rhs_scale=w_scales[i][:, n],
                    start=True,
                    stop=True,
                )

        def multiply_h(i, j):
            if j == 0:
                h_grouped[i] = work.tile([P, PACK * UNIT], BF16, name="h_by_column", bufs=2, align_bytes=64)
            h = h_grouped[i][:, PACK * P * j : PACK * P * (j + 1)].rearrange("p (c n t) -> p c t n", n=2, t=PACK)
            t1 = t1_sb[i][:, :, P * j : P * (j + 1)].rearrange("p t (c n) -> p c t n", n=2)
            t3 = t3_banks[i, j][:].rearrange("p t (c n) -> p c t n", n=2)
            nc.vector.tensor_tensor(out=h, in0=t3, in1=t1, op=MULT)

        def product_out(i, m, first=0, count=UNIT, take_bank=ring_bank, copy=nc.scalar.copy):
            b, half = divmod(i, 2)
            n = slice(first, first + count)
            bank = take_bank([P, UNIT])
            nc.tensor.matmul_mx(
                out=bank[:, :count],
                lhsT=c_words[:, 2 * P * m : 2 * P * (m + 1)].bitcast(FP4X4),
                lhsT_scale=c_scales[:, P * m : P * (m + 1)],
                rhs=h_codes[i][:, n].bitcast(FP8X4),
                rhs_scale=h_scales[i][:, n],
                start=True,
                stop=True,
            )
            result = work.tile([P, UNIT], F32, name="out_copy", bufs=RESULTS)
            copy(out=result[:, :count], in_=bank[:, :count])
            col = half * UNIT + first
            nc.sync.dma_start(out=out[b, P * m : P * (m + 1), col : col + count], in_=result[:, :count])

        scale_cols = const.tile([P, PACK], F32)
        nc.scalar.dma_start(out=scale_cols[:], in_=w_scale.rearrange("a b (p t) -> p (a b t)", t=PACK))
        ident = const.tile([P, P], F32)
        make_identity(nc, ident[:])
        c_scales = const.tile([P, D], U8, align_bytes=64)
        nc.vector.memset(c_scales[:].bitcast(I32), 0)
        ones = const.tile([P, 1], F32)
        nc.vector.memset(ones[:], 1.0)

        load_w(0)
        a_raw = const.tile([P, 2, R], BF16)
        nc.sync.dma_start(out=a_raw[:], in_=A.rearrange("(p k) r -> p k r", k=2))
        load_x1(0)
        load_w(1)
        load_t2(0)
        load_t2(1)
        load_x1(1)
        load_w(2)
        load_t2(2)
        load_w(3)
        load_w(4)
        load_w(5)
        load_t2(3)
        c_words = const.tile([P, 2 * D], U8, align_bytes=64)
        nc.sync.dma_start(out=c_words[:], in_=C_words[0])
        for q in range(4):
            rows = C_scales[0, 4 * q : 4 * q + 4, :].bitcast(I32)
            nc.sync.dma_start(out=c_scales[32 * q : 32 * q + 4, :].bitcast(I32), in_=rows)
        for i in range(2, UNITS):
            if i < KEPT:
                load_x1(i)
            if i + 4 <= LAST:
                load_w(i + 4)
            if i + 2 < KEPT:
                load_t2(i + 2)

        row_bank = ring_bank([P, PACK, P])
        for t in range(PACK):
            nc.tensor.transpose(row_bank[:, t, :], scale_cols[:, t : t + 1].to_broadcast([P, P]), ident[:])
        scale_rows = const.tile([P, CV], F32)
        nc.scalar.copy(out=scale_rows[:].rearrange("p (q t) -> p q t", t=PACK), in_=row_bank[:].rearrange("p t q -> p q t"))
        a_perm = const.tile([P, 2, PACK, P], BF16)
        nc.scalar.copy(out=a_perm[:], in_=a_raw[:].rearrange("p k (m t) -> p k t m", t=PACK))

        widen_sorted(0, 0)
        scale_sorted = const.tile([P, CV], F32)
        target = scale_sorted[:].rearrange("p (u q e) -> p u q e", u=2, e=2)
        nc.scalar.copy(out=target, in_=row_bank[:].rearrange("p (u e) q -> p u q e", u=2))
        scale_plain(0, 2, 2)
        product_t1([0], turns_late(0, 0, 2))
        scale_late(0, 0, 2)
        scale_plain(0, 4, 2)
        product_t1([1], turns_plain(0, 2, 2, t3_bank))
        scale_plain(0, 6, 2)
        product_t1([2, 3], turns_t2(0, t3_bank) + turns_t2(1) + turns_plain(0, 4, 2, t3_bank))
        scale_plain(1, 0, 2)
        quantise_t2(0)
        quantise_w(0)
        quantise_t2(1)
        product_t1([4, 5], turns_plain(0, 6, 2, t3_bank) + turns_t2(2))
        product_t1([6], turns_plain(1, 0, 2))
        widen_sorted(1, 2)
        scale_plain(1, 4, 2)
        product_t3(0, 0)
        product_t3(0, 1)

        t1_slots = list(range(7, PACK * (UNITS + 2)))
        waiting = [(1, 6 * CV, SAMPLE_COLS), (2, 0, ROWS2)]
        w_last = True
        for i in range(LAST):
            b, second = divmod(i + 2, 2)
            busy = i < LAST - 2
            four = b in FOUR_SHARED
            if i + 1 == LAST:
                multiply_h(i, 0)
            if w_last:
                if i > 0:
                    quantise_h(i - 1)
                quantise_t2(i + 2)
                quantise_w(i + 1)
            else:
                quantise_w(i + 1)
                quantise_t2(i + 2)
                quantise_h(i - 1)
            if second == 0 and b + 1 < NB:
                w_wide[b + 1] = handed_on(i + 2, 7 * CV)
                extra = 5 if four else None
                if extra:
                    scale_shared(b, extra, 1, w_wide[b + 1], 6 * CV)
                share = SHORT_WIDENS if extra else GPSIMD_WIDENS
                widen(b + 1, ROWS2, ROWS2 + share, nc.gpsimd.tensor_copy)
                after = 0 if i == 0 or four else AFTER_PRODUCT
                waiting.append((b + 1, ROWS2 + share + after, SAMPLE_COLS))
                if b + 2 < NB:
                    waiting.append((b + 2, 0, ROWS2))
            elif second == 1 and b + 1 < NB:
                count = 3
                scale_shared(b + 1, 2, count, handed_on(i + 2, 3 * CV))
                if after:
                    widen(b + 1, ROWS2 + share, ROWS2 + share + after, nc.gpsimd.tensor_copy)
            elif i + 3 == LAST:
                scale_shared(b, 5, 3, handed_on(i + 2, 3 * CV))

            pair = (6 if four or i == 1 else 5) if second else 2 if i == 0 else 0
            single = busy and second and pair == 5
            if i == 0:
                steps = turns_late(b, pair, 2) + turns_t2(3)
            elif i == 1:
                steps = turns_late(b, pair, 2)
            elif busy and second:
                steps = turns_shared(b, 4, 2 if four else 1) + turns_late(b, pair, 2)
            elif busy:
                steps = turns_late(b, pair, 2) + turns_shared(b, 2, 2)
            elif i + 2 == LAST:
                steps = turns_shared(b, 4, 2) + turns_shared(b, 6, 2)
            else:
                steps = []
            product_t1([t1_slots.pop(0) for n in range(2)], steps)
            made = [(i, 2), (i, 3), (i + 1, 0), (i + 1, 1)] if busy else [(i, 3), (i + 1, 0), (i + 1, 1)]
            if i + 1 >= LAST - 2:
                made.append((i + 1, 2))
            if i + 1 < LAST:
                multiply_h(i, 0)
            product_t3(*made.pop(0))
            multiply_h(i, 1)
            product_t3(*made.pop(0))
            if i > 0:
                product_out(i - 1, 0)
            widen_piece()
            if i == 0:
                widen_piece()
                widen_piece()
            if busy:
                scale_late(b, pair, 2)
            steps = turns_t2(i + 4)
            if i == 0:
                steps = turns_plain(1, 4, 2) + steps
            if single:
                steps = steps[:2] + turns_late(b, 7, 1) + steps[2:]
            product_t1([t1_slots.pop(0) for n in range(1 if i in SKIPS else 3 if i in EXTRA else 2)], steps)
            multiply_h(i, 2)
            product_t3(*made.pop(0))
            multiply_h(i, 3)
            for block in made:
                product_t3(*block)
            if i > 0:
                product_out(i - 1, 1)
            widen_piece()
            if i + KEPT <= LAST:
                load_t2(i + KEPT)
                load_x1(i + KEPT)
            if single:
                scale_late(b, 7, 1)
            w_last = single or i + 2 == LAST

        product_t3(LAST, 3, ring_bank)
        multiply_h(LAST, 0)
        quantise_h(LAST - 1)
        for m in range(2):
            product_out(LAST - 1, m)
        multiply_h(LAST, 1)
        multiply_h(LAST, 2)
        quantise_h(LAST, 0, 2 * P)
        for m in range(2):
            product_out(LAST, m, 0, 2 * P)
        multiply_h(LAST, 3)
        for first in (2 * P, 3 * P):
            quantise_h(LAST, first, P)
        for first in (2 * P, 3 * P):
            product_out(LAST, 0, first, P)
            product_out(LAST, 1, first, P, t3_bank, nc.vector.tensor_copy)
